import numpy as np
import ml_dtypes


def mxq(x, axis, fmt="e4m3"):
    dtype, down = {"e4m3": (ml_dtypes.float8_e4m3fn, 7), "e5m2": (ml_dtypes.float8_e5m2, 14)}[fmt]
    v = np.moveaxis(np.asarray(x, np.float32).astype(ml_dtypes.bfloat16).astype(np.float64), axis, -1)
    blocks = v.reshape(v.shape[:-1] + (-1, 32))
    amax = np.abs(blocks).max(-1, keepdims=True)
    byte = np.maximum(np.where(amax > 0, np.frexp(amax)[1] - 1 + 127, 0) - down, 1)
    scale = np.exp2(byte - 127.0)
    codes = (blocks / scale).astype(np.float32).astype(dtype).astype(np.float64)
    return np.moveaxis((codes * scale).reshape(v.shape), -1, axis)


WIDE = False


def mx_kscale(k):
    if not WIDE:
        return np.ones(k)
    levels = np.array([10, -10, 5, -5, 0])
    a = np.random.permutation(np.resize(levels, k // 512 * 4)).reshape(k // 512, 4)
    idx = np.arange(k)
    return np.exp2(a[idx // 512, idx % 128 // 32])


BF16 = ml_dtypes.bfloat16


def bf(x):
    return np.asarray(x, np.float32).astype(BF16)


def f64(x):
    return np.asarray(x).astype(np.float64)


B, H0, W0, H1, W1, C = 2, 24, 32, 24, 32, 512
L, S = H0 * W0, H1 * W1
THR = 0.2
TEMPERATURE = 0.1
BORDER = 2
NM = min(L, S) // 2
ND = NM // 16
DUP = 0.92
RB = 0.5
ZT = 4.5
SD = ZT - np.sqrt(ZT**2 - 2.0 * np.log(min(L, S) * THR / (1.0 - THR)))
SIG = SD / np.sqrt(1.0 + RB**2 / 2.0)
G = np.sqrt(SIG * TEMPERATURE * np.sqrt(C / 2.0))
MATCH = np.log(max(L, S)) + SD**2 / 2.0 + 3.5
ALPHA = MATCH / (SIG * np.sqrt(C / 2.0))


def interior_mask(h, w, b):
    vh = (np.arange(h) >= b) & (np.arange(h) < h - b)
    vw = (np.arange(w) >= b) & (np.arange(w) < w - b)
    return (vh[:, None] & vw[None, :]).reshape(-1)


def softmax(v, axis):
    e = np.exp(v - v.max(axis=axis, keepdims=True))
    return e / e.sum(axis=axis, keepdims=True)


def pick(h, w):
    rep = np.random.permutation(np.flatnonzero(interior_mask(h, w, BORDER)))[:ND]
    rest = np.random.permutation(np.setdiff1d(np.arange(h * w), rep))[:NM]
    return rep, rest


def setup_inputs():
    s = mx_kscale(C)
    x0 = np.random.standard_normal((B, L, C))
    x1 = np.random.standard_normal((B, S, C))
    for n in range(B):
        r0, m0 = pick(H0, W0)
        r1, m1 = pick(H1, W1)
        x1[n, m1] = ALPHA * x0[n, m0] + np.sqrt(1.0 - ALPHA**2) * x1[n, m1]
        x0[n, r0] = DUP * x0[n, m0[:ND]]
        x1[n, r1] = DUP * x1[n, m1[:ND]]
    return {"feat_c0": bf(x0 * s),
            "feat_c1": bf(x1 * s),
            "W": bf(np.random.standard_normal((C, C)) * G / np.sqrt(C) / s[None, :]),
            "b": bf(np.random.standard_normal(C) * RB * G),
            "h0c": H0, "w0c": W0, "h1c": H1, "w1c": W1}


def reference(feat_c0, feat_c1, W, b, h0c, w0c, h1c, w1c):
    scale = feat_c0.shape[-1] ** 0.5
    wq = mxq(f64(W), 1, "e4m3")
    f0 = ((mxq(f64(feat_c0), 2, "e4m3") @ wq.T) + f64(b)) / scale
    f1 = ((mxq(f64(feat_c1), 2, "e4m3") @ wq.T) + f64(b)) / scale
    sim = (mxq(f0, 2, "e4m3") @ mxq(f1, 2, "e4m3").transpose(0, 2, 1)) / TEMPERATURE

    conf_0to1 = softmax(sim, 2)
    conf_1to0 = softmax(sim, 1)

    mask = (conf_0to1 > THR) & (conf_0to1 == conf_0to1.max(axis=2, keepdims=True))
    mask = mask | ((conf_1to0 > THR) & (conf_1to0 == conf_1to0.max(axis=1, keepdims=True)))

    mask = mask & interior_mask(h0c, w0c, BORDER)[None, :, None]
    mask = mask & interior_mask(h1c, w1c, BORDER)[None, None, :]

    mconf = np.where(mask, np.maximum(conf_0to1, conf_1to0), 0.0)
    return np.stack([conf_0to1, conf_1to0, mconf])

@@ -1,0 +1,285 @@
+from contextlib import ExitStack
+import math
+
+import concourse.mybir as mybir
+from concourse.masks import make_identity
+
+F32 = mybir.dt.float32
+BF16 = mybir.dt.bfloat16
+U32 = mybir.dt.uint32
+U8 = mybir.dt.uint8
+FP8X4 = mybir.dt.float8_e4m3fn_x4
+ALU = mybir.AluOpType
+ACT = mybir.ActivationFunctionType
+AXIS = mybir.AxisListType
+
+P = 128
+PACK = 4
+BANK = 512
+BATCH = 2
+CELLS = 768
+FEATURES = 512
+CELL_TILES = CELLS // P
+REST = CELLS - BANK
+TOKENS = 2 * BATCH * CELLS
+CHUNK = BANK
+CHUNK_TILES = CHUNK // P
+BORDER = 2
+THRESHOLD = 0.2
+INV_TEMPERATURE = 10.0
+INV_SQRT_FEATURES = 1.0 / math.sqrt(FEATURES)
+
+FLOPS = 2 * TOKENS * FEATURES * FEATURES + 2 * BATCH * CELLS * CELLS * FEATURES
+
+
+def tile_coarsematching_kernel(tc, feat_c0, feat_c1, W, b, h0c, w0c, h1c, w1c, out):
+    nc = tc.nc
+    assert h0c * w0c == CELLS and h1c * w1c == CELLS
+    assert P % w0c == 0 and BANK % w1c == 0
+    assert BORDER * w0c <= P // 2 and BORDER * w0c % 32 == 0
+
+    with ExitStack() as ctx:
+        keep = ctx.enter_context(tc.tile_pool(name="keep", bufs=1))
+        stage = ctx.enter_context(tc.tile_pool(name="stage", bufs=3))
+        columns = ctx.enter_context(tc.tile_pool(name="columns", bufs=2))
+        work = ctx.enter_context(tc.tile_pool(name="work", bufs=4))
+        small = ctx.enter_context(tc.tile_pool(name="small", bufs=6))
+        psum = ctx.enter_context(tc.psum_pool(name="psum", bufs=8))
+
+        w_raw = keep.tile([P, PACK * FEATURES], BF16)
+        nc.sync.dma_start(
+            out=w_raw[:].rearrange("p (t k) -> p t k", t=PACK),
+            in_=W.rearrange("(p t) k -> p t k", t=PACK),
+        )
+        b_raw = keep.tile([P, PACK], BF16)
+        nc.sync.dma_start(out=b_raw[:], in_=b.rearrange("(p t) -> p t", t=PACK))
+        x_raw = keep.tile([P, (TOKENS // P) * FEATURES], BF16)
+        x_raw_tiles = x_raw[:].rearrange("p (r k) -> p r k", k=FEATURES)
+        for n in range(BATCH):
+            for g, feat in enumerate((feat_c0, feat_c1)):
+                first = (2 * n + g) * CELL_TILES
+                nc.sync.dma_start(
+                    out=x_raw_tiles[:, first : first + CELL_TILES, :],
+                    in_=feat[n].rearrange("(j p) k -> p j k", p=P),
+                )
+
+        identity = keep.tile([P, P], F32)
+        make_identity(nc, identity[:])
+        identity_bf = keep.tile([P, P], BF16)
+        nc.vector.tensor_copy(out=identity_bf[:], in_=identity[:])
+
+        edge = keep.tile([P, P], F32)
+        nc.vector.memset(edge[:], 0.0)
+        edge_rows = edge[:].rearrange("p (r w) -> p r w", w=w0c)
+        nc.vector.memset(edge_rows[:, :, 0:BORDER], 1.0)
+        nc.vector.memset(edge_rows[:, :, w0c - BORDER : w0c], 1.0)
+        edge_t = psum.tile([P, BANK], F32, tag="bank")
+        nc.tensor.transpose(edge_t[:, 0:P], edge[:], identity[:])
+        row_gate = keep.tile([P, CELL_TILES], F32)
+        nc.vector.tensor_copy(out=row_gate[:], in_=edge_t[:, 0:CELL_TILES])
+        nc.vector.memset(row_gate[0 : BORDER * w0c, 0:1], 1.0)
+        nc.vector.memset(row_gate[P - BORDER * w0c : P, CELL_TILES - 1 : CELL_TILES], 1.0)
+
+        mconf_tiles = []
+        for slot in range(3):
+            mconf = keep.tile([P, CELLS], F32, name="mconf%d" % slot)
+            nc.vector.memset(mconf[:], 0.0)
+            mconf_tiles.append(mconf)
+
+        b_scaled = keep.tile([P, PACK], F32)
+        nc.vector.tensor_scalar_mul(out=b_scaled[:], in0=b_raw[:], scalar1=INV_SQRT_FEATURES)
+
+        def quantise_k_last(raw, first_tile, codes, scales):
+            words = raw.bitcast(F32).rearrange("p (r u q) -> p r u q", u=2, q=P)
+            grouped = stage.tile([P, CHUNK * PACK], BF16, tag="grouped", align_bytes=64)
+            grouped_words = grouped[:].bitcast(F32).rearrange("p (h r c u) -> p h r c u", h=2, r=2, u=2)
+            for h in range(2):
+                flipped = psum.tile([P, 2, 2, P], F32, tag="bank")
+                for r in range(2):
+                    for u in range(2):
+                        nc.tensor.transpose(
+                            flipped[:, r, u, :], words[:, first_tile + 2 * h + r, u, :], identity[:]
+                        )
+                copy_out = nc.vector.tensor_copy if h == 0 else nc.scalar.copy
+                copy_out(out=grouped_words[:, h], in_=flipped[:].rearrange("p r u c -> p r c u"))
+            nc.vector.quantize_mx(out=codes.bitcast(FP8X4), scales=scales, in_=grouped[:])
+
+        w_codes = keep.tile([P, FEATURES], U32, align_bytes=64)
+        w_scales = keep.tile([P, FEATURES], U8, align_bytes=64)
+        quantise_k_last(w_raw[:], 0, w_codes[:], w_scales[:])
+
+        x_codes = keep.tile([P, TOKENS], U32, align_bytes=64)
+        x_scales = keep.tile([P, TOKENS], U8, align_bytes=64)
+        f_codes = keep.tile([P, TOKENS], U32, align_bytes=64)
+        f_scales = keep.tile([P, TOKENS], U8, align_bytes=64)
+
+        def project_chunk(c):
+            cols = slice(c * CHUNK, (c + 1) * CHUNK)
+            quantise_k_last(x_raw[:], c * CHUNK_TILES, x_codes[:, cols], x_scales[:, cols])
+            f_rows = stage.tile([P, PACK, CHUNK], BF16)
+            for t in range(PACK):
+                acc = psum.tile([P, BANK], F32, tag="bank")
+                nc.tensor.matmul_mx(
+                    out=acc[:],
+                    lhsT=w_codes[:, t * P : (t + 1) * P].bitcast(FP8X4),
+                    lhsT_scale=w_scales[:, t * P : (t + 1) * P],
+                    rhs=x_codes[:, cols].bitcast(FP8X4),
+                    rhs_scale=x_scales[:, cols],
+                    start=True,
+                    stop=True,
+                )
+                nc.scalar.activation(
+                    out=f_rows[:, t, :],
+                    in_=acc[:],
+                    func=ACT.Identity,
+                    bias=b_scaled[:, t : t + 1],
+                    scale=INV_SQRT_FEATURES,
+                )
+            f_grouped = stage.tile([P, CHUNK, PACK], BF16, align_bytes=64)
+            nc.vector.tensor_copy(
+                out=f_grouped[:].rearrange("p (c i) t -> p c t i", i=4),
+                in_=f_rows[:].rearrange("p t (c i) -> p c t i", i=4),
+            )
+            nc.vector.quantize_mx(
+                out=f_codes[:, cols].bitcast(FP8X4),
+                scales=f_scales[:, cols],
+                in_=f_grouped[:].rearrange("p c t -> p (c t)"),
+            )
+
+        def softmax_parts(on_partitions, along_free):
+            wide = psum.tile([P, BANK], F32, tag="bank")
+            narrow = psum.tile([P, BANK], F32, tag="bank")
+            for acc, start, width in ((wide, along_free, BANK), (narrow, along_free + BANK, REST)):
+                nc.tensor.matmul_mx(
+                    out=acc[:, 0:width],
+                    lhsT=f_codes[:, on_partitions : on_partitions + P].bitcast(FP8X4),
+                    lhsT_scale=f_scales[:, on_partitions : on_partitions + P],
+                    rhs=f_codes[:, start : start + width].bitcast(FP8X4),
+                    rhs_scale=f_scales[:, start : start + width],
+                    start=True,
+                    stop=True,
+                )
+            tops = small.tile([P, 2], F32)
+            nc.vector.reduce_max(out=tops[:, 0:1], in_=wide[:], axis=AXIS.X)
+            nc.vector.reduce_max(out=tops[:, 1:2], in_=narrow[:, 0:REST], axis=AXIS.X)
+            top = small.tile([P, 1], F32)
+            nc.vector.tensor_tensor(out=top[:], in0=tops[:, 0:1], in1=tops[:, 1:2], op=ALU.max)
+            shift = small.tile([P, 1], F32)
+            nc.scalar.mul(out=shift[:], in_=top[:], mul=-INV_TEMPERATURE)
+            numer = work.tile([P, CELLS], F32)
+            sums = small.tile([P, 2], F32)
+            nc.scalar.activation(
+                out=numer[:, 0:BANK], in_=wide[:], func=ACT.Exp,
+                bias=shift[:], scale=INV_TEMPERATURE, accum_out=sums[:, 0:1],
+            )
+            nc.scalar.activation(
+                out=numer[:, BANK:CELLS], in_=narrow[:, 0:REST], func=ACT.Exp,
+                bias=shift[:], scale=INV_TEMPERATURE, accum_out=sums[:, 1:2],
+            )
+            peak = small.tile([P, 1], F32)
+            nc.scalar.activation(
+                out=peak[:], in_=top[:], func=ACT.Exp, bias=shift[:], scale=INV_TEMPERATURE
+            )
+            total = small.tile([P, 1], F32)
+            nc.vector.tensor_add(out=total[:], in0=sums[:, 0:1], in1=sums[:, 1:2])
+            recip = small.tile([P, 1], F32)
+            nc.vector.reciprocal(out=recip[:], in_=total[:])
+            key = small.tile([P, 1], F32)
+            nc.vector.tensor_scalar(
+                out=key[:], in0=recip[:], scalar1=THRESHOLD, scalar2=peak[:],
+                op0=ALU.is_le, op1=ALU.add,
+            )
+            return numer, recip, key
+
+
+        def grid(ap):
+            return ap.rearrange("p (r w) -> p r w", w=w1c)
+
+        rows_in = h1c - 2 * BORDER
+        cols_in = w1c - 2 * BORDER
+        inner_w = slice(BORDER, w1c - BORDER)
+
+        conf_t = {}
+        miss_t = {}
+
+        def column_tile(n, j):
+            if j == 0:
+                conf_t[n] = columns.tile([P, CELL_TILES, CELLS], F32, name="conf_t")
+                miss_t[n] = columns.tile([P, CELL_TILES, CELLS], BF16, name="miss_t")
+            f0_at = 2 * n * CELLS
+            numer, recip, key = softmax_parts(f0_at + CELLS + j * P, f0_at)
+            nc.gpsimd.tensor_scalar(
+                out=conf_t[n][:, j, :], in0=numer[:], scalar1=recip[:], scalar2=0.0,
+                op0=ALU.mult, op1=ALU.add,
+            )
+            nc.gpsimd.tensor_scalar(
+                out=miss_t[n][:, j, :], in0=numer[:], scalar1=-1.0, scalar2=key[:],
+                op0=ALU.mult, op1=ALU.add,
+            )
+
+        def row_tile(n, i):
+            rows = slice(i * P, (i + 1) * P)
+            f0_at = 2 * n * CELLS
+            numer, recip, key = softmax_parts(f0_at + i * P, f0_at + CELLS)
+            conf0 = work.tile([P, CELLS], F32)
+            nc.gpsimd.tensor_scalar(
+                out=conf0[:], in0=numer[:], scalar1=recip[:], scalar2=0.0,
+                op0=ALU.mult, op1=ALU.add,
+            )
+            nc.sync.dma_start(out=out[0, n, rows, :], in_=conf0[:])
+
+            conf1_wide = psum.tile([P, BANK], F32, tag="bank")
+            conf1_narrow = psum.tile([P, BANK], F32, tag="bank")
+            miss1 = psum.tile([P, CELLS], BF16, tag="bank")
+            for j in range(CELL_TILES):
+                target = conf1_wide if j < BANK // P else conf1_narrow
+                at = (j * P) % BANK
+                nc.tensor.transpose(target[:, at : at + P], conf_t[n][:, j, rows], identity[:])
+            for j in range(CELL_TILES):
+                nc.tensor.transpose(miss1[:, j * P : (j + 1) * P], miss_t[n][:, j, rows], identity_bf[:])
+            conf1 = work.tile([P, CELLS], F32)
+            nc.scalar.copy(out=conf1[:, 0:BANK], in_=conf1_wide[:])
+            nc.scalar.copy(out=conf1[:, BANK:CELLS], in_=conf1_narrow[:, 0:REST])
+            nc.sync.dma_start(out=out[1, n, rows, :], in_=conf1[:])
+
+            inner_h = slice(BORDER, h1c - BORDER)
+            both = work.tile([P, rows_in, cols_in], F32)
+            nc.vector.scalar_tensor_tensor(
+                out=both[:],
+                in0=grid(numer[:])[:, inner_h, inner_w],
+                scalar=key[:],
+                in1=grid(miss1[:])[:, inner_h, inner_w],
+                op0=ALU.subtract,
+                op1=ALU.mult,
+            )
+            best = work.tile([P, rows_in, cols_in], F32)
+            nc.vector.tensor_tensor(
+                out=best[:],
+                in0=grid(conf0[:])[:, inner_h, inner_w],
+                in1=grid(conf1[:])[:, inner_h, inner_w],
+                op=ALU.max,
+            )
+            mconf = mconf_tiles[i % len(mconf_tiles)]
+            nc.vector.scalar_tensor_tensor(
+                out=grid(mconf[:])[:, inner_h, inner_w],
+                in0=both[:],
+                scalar=row_gate[:, i : i + 1],
+                in1=best[:],
+                op0=ALU.is_ge,
+                op1=ALU.mult,
+            )
+            nc.sync.dma_start(out=out[2, n, rows, :], in_=mconf[:])
+
+        chunks_a_batch = 2 * CELLS // CHUNK
+        tiles_a_chunk = CELL_TILES // chunks_a_batch
+        for c in range(chunks_a_batch):
+            project_chunk(c)
+        for c in range(chunks_a_batch):
+            project_chunk(chunks_a_batch + c)
+            for j in range(c * tiles_a_chunk, (c + 1) * tiles_a_chunk):
+                column_tile(0, j)
+        for i in range(CELL_TILES):
+            row_tile(0, i)
+            column_tile(1, i)
+        for i in range(CELL_TILES):
+            row_tile(1, i)

@@ -11,7 +11,6 @@ U8 = mybir.dt.uint8
 FP8X4 = mybir.dt.float8_e4m3fn_x4
 ALU = mybir.AluOpType
 ACT = mybir.ActivationFunctionType
-AXIS = mybir.AxisListType
 
 P = 128
 PACK = 4
@@ -24,6 +23,9 @@ REST = CELLS - BANK
 TOKENS = 2 * BATCH * CELLS
 CHUNK = BANK
 CHUNK_TILES = CHUNK // P
+CHUNKS = TOKENS // CHUNK
+JOBS_A_BATCH = 2 * CELL_TILES
+JOBS = BATCH * JOBS_A_BATCH
 BORDER = 2
 THRESHOLD = 0.2
 INV_TEMPERATURE = 10.0
@@ -40,11 +42,11 @@ def tile_coarsematching_kernel(tc, feat_c0, feat_c1, W, b, h0c, w0c, h1c, w1c, o
 
     with ExitStack() as ctx:
         keep = ctx.enter_context(tc.tile_pool(name="keep", bufs=1))
-        stage = ctx.enter_context(tc.tile_pool(name="stage", bufs=3))
+        stage = ctx.enter_context(tc.tile_pool(name="stage", bufs=2))
         columns = ctx.enter_context(tc.tile_pool(name="columns", bufs=2))
-        work = ctx.enter_context(tc.tile_pool(name="work", bufs=4))
-        small = ctx.enter_context(tc.tile_pool(name="small", bufs=6))
-        psum = ctx.enter_context(tc.psum_pool(name="psum", bufs=8))
+        work = ctx.enter_context(tc.tile_pool(name="work", bufs=3))
+        small = ctx.enter_context(tc.tile_pool(name="small", bufs=4))
+        psum = ctx.enter_context(tc.psum_pool(name="psum", bufs=4))
 
         w_raw = keep.tile([P, PACK * FEATURES], BF16)
         nc.sync.dma_start(
@@ -73,7 +75,7 @@ def tile_coarsematching_kernel(tc, feat_c0, feat_c1, W, b, h0c, w0c, h1c, w1c, o
         edge_rows = edge[:].rearrange("p (r w) -> p r w", w=w0c)
         nc.vector.memset(edge_rows[:, :, 0:BORDER], 1.0)
         nc.vector.memset(edge_rows[:, :, w0c - BORDER : w0c], 1.0)
-        edge_t = psum.tile([P, BANK], F32, tag="bank")
+        edge_t = psum.tile([P, BANK], F32, tag="aux")
         nc.tensor.transpose(edge_t[:, 0:P], edge[:], identity[:])
         row_gate = keep.tile([P, CELL_TILES], F32)
         nc.vector.tensor_copy(out=row_gate[:], in_=edge_t[:, 0:CELL_TILES])
@@ -89,36 +91,51 @@ def tile_coarsematching_kernel(tc, feat_c0, feat_c1, W, b, h0c, w0c, h1c, w1c, o
         b_scaled = keep.tile([P, PACK], F32)
         nc.vector.tensor_scalar_mul(out=b_scaled[:], in0=b_raw[:], scalar1=INV_SQRT_FEATURES)
 
-        def quantise_k_last(raw, first_tile, codes, scales):
+        def flip(raw, first_tile):
             words = raw.bitcast(F32).rearrange("p (r u q) -> p r u q", u=2, q=P)
-            grouped = stage.tile([P, CHUNK * PACK], BF16, tag="grouped", align_bytes=64)
-            grouped_words = grouped[:].bitcast(F32).rearrange("p (h r c u) -> p h r c u", h=2, r=2, u=2)
+            banks = []
             for h in range(2):
-                flipped = psum.tile([P, 2, 2, P], F32, tag="bank")
+                flipped = psum.tile([P, 2, 2, P], F32, tag="aux")
                 for r in range(2):
                     for u in range(2):
                         nc.tensor.transpose(
                             flipped[:, r, u, :], words[:, first_tile + 2 * h + r, u, :], identity[:]
                         )
-                copy_out = nc.vector.tensor_copy if h == 0 else nc.scalar.copy
-                copy_out(out=grouped_words[:, h], in_=flipped[:].rearrange("p r u c -> p r c u"))
-            nc.vector.quantize_mx(out=codes.bitcast(FP8X4), scales=scales, in_=grouped[:])
+                banks.append(flipped)
+            return banks
+
+        def gather(banks):
+            grouped = stage.tile([P, CHUNK * PACK], BF16, bufs=3, align_bytes=64)
+            halves = grouped[:].bitcast(F32).rearrange("p (h r c u) -> p h r c u", h=2, r=2, u=2)
+            nc.vector.tensor_copy(out=halves[:, 0], in_=banks[0][:].rearrange("p r u c -> p r c u"))
+            nc.scalar.copy(out=halves[:, 1], in_=banks[1][:].rearrange("p r u c -> p r c u"))
+            return grouped
 
         w_codes = keep.tile([P, FEATURES], U32, align_bytes=64)
         w_scales = keep.tile([P, FEATURES], U8, align_bytes=64)
-        quantise_k_last(w_raw[:], 0, w_codes[:], w_scales[:])
-
         x_codes = keep.tile([P, TOKENS], U32, align_bytes=64)
         x_scales = keep.tile([P, TOKENS], U8, align_bytes=64)
         f_codes = keep.tile([P, TOKENS], U32, align_bytes=64)
         f_scales = keep.tile([P, TOKENS], U8, align_bytes=64)
+        x_banks = {}
+        x_grouped = {}
+        f_rows = {}
+        f_grouped = {}
 
-        def project_chunk(c):
-            cols = slice(c * CHUNK, (c + 1) * CHUNK)
-            quantise_k_last(x_raw[:], c * CHUNK_TILES, x_codes[:, cols], x_scales[:, cols])
-            f_rows = stage.tile([P, PACK, CHUNK], BF16)
+        def chunk_columns(c):
+            return slice(c * CHUNK, (c + 1) * CHUNK)
+
+        def quantise_tokens(c):
+            cols = chunk_columns(c)
+            nc.vector.quantize_mx(
+                out=x_codes[:, cols].bitcast(FP8X4), scales=x_scales[:, cols], in_=x_grouped[c][:]
+            )
+
+        def project(c):
+            cols = chunk_columns(c)
+            f_rows[c] = stage.tile([P, PACK, CHUNK], BF16, name="f_rows")
             for t in range(PACK):
-                acc = psum.tile([P, BANK], F32, tag="bank")
+                acc = psum.tile([P, BANK], F32, tag="aux")
                 nc.tensor.matmul_mx(
                     out=acc[:],
                     lhsT=w_codes[:, t * P : (t + 1) * P].bitcast(FP8X4),
@@ -129,157 +146,245 @@ def tile_coarsematching_kernel(tc, feat_c0, feat_c1, W, b, h0c, w0c, h1c, w1c, o
                     stop=True,
                 )
                 nc.scalar.activation(
-                    out=f_rows[:, t, :],
+                    out=f_rows[c][:, t, :],
                     in_=acc[:],
                     func=ACT.Identity,
                     bias=b_scaled[:, t : t + 1],
                     scale=INV_SQRT_FEATURES,
                 )
-            f_grouped = stage.tile([P, CHUNK, PACK], BF16, align_bytes=64)
+
+        def regroup(c):
+            f_grouped[c] = stage.tile([P, CHUNK, PACK], BF16, name="f_grouped", align_bytes=64)
             nc.vector.tensor_copy(
-                out=f_grouped[:].rearrange("p (c i) t -> p c t i", i=4),
-                in_=f_rows[:].rearrange("p t (c i) -> p c t i", i=4),
+                out=f_grouped[c][:].rearrange("p (c i) t -> p c t i", i=4),
+                in_=f_rows[c][:].rearrange("p t (c i) -> p c t i", i=4),
             )
+
+        def quantise_features(c):
+            cols = chunk_columns(c)
             nc.vector.quantize_mx(
                 out=f_codes[:, cols].bitcast(FP8X4),
                 scales=f_scales[:, cols],
-                in_=f_grouped[:].rearrange("p c t -> p (c t)"),
+                in_=f_grouped[c][:].rearrange("p c t -> p (c t)"),
             )
 
-        def softmax_parts(on_partitions, along_free):
-            wide = psum.tile([P, BANK], F32, tag="bank")
-            narrow = psum.tile([P, BANK], F32, tag="bank")
-            for acc, start, width in ((wide, along_free, BANK), (narrow, along_free + BANK, REST)):
+        def front_round(k):
+            if 0 <= k < CHUNKS:
+                project(k)
+            if 0 <= k - 1 < CHUNKS:
+                regroup(k - 1)
+            if 0 <= k + 1 < CHUNKS:
+                quantise_tokens(k + 1)
+            if 0 <= k + 2 < CHUNKS:
+                x_banks[k + 2] = flip(x_raw[:], (k + 2) * CHUNK_TILES)
+            if 0 <= k - 1 < CHUNKS:
+                quantise_features(k - 1)
+            if 0 <= k + 2 < CHUNKS:
+                x_grouped[k + 2] = gather(x_banks[k + 2])
+
+        soft_t = {}
+        miss_t = {}
+        recip = {}
+        key = {}
+        numer = {}
+        sim_banks = {}
+        top = {}
+        total = {}
+        peak = {}
+
+        def job_parts(q):
+            n, job = divmod(q, JOBS_A_BATCH)
+            is_row, i = divmod(job, CELL_TILES)
+            return n, job, is_row, i
+
+        def job_values(q):
+            n, job, is_row, i = job_parts(q)
+            return numer[n, i][:] if is_row else soft_t[n][:, i, :]
+
+        def similarities(q):
+            n, job, is_row, i = job_parts(q)
+            f0_at = 2 * n * CELLS
+            f1_at = f0_at + CELLS
+            at = (f0_at if is_row else f1_at) + i * P
+            along = f1_at if is_row else f0_at
+            wide = psum.tile([P, BANK], F32, tag="sim")
+            narrow = psum.tile([P, BANK], F32, tag="sim")
+            for acc, first, width in ((wide, along, BANK), (narrow, along + BANK, REST)):
                 nc.tensor.matmul_mx(
                     out=acc[:, 0:width],
-                    lhsT=f_codes[:, on_partitions : on_partitions + P].bitcast(FP8X4),
-                    lhsT_scale=f_scales[:, on_partitions : on_partitions + P],
-                    rhs=f_codes[:, start : start + width].bitcast(FP8X4),
-                    rhs_scale=f_scales[:, start : start + width],
+                    lhsT=f_codes[:, at : at + P].bitcast(FP8X4),
+                    lhsT_scale=f_scales[:, at : at + P],
+                    rhs=f_codes[:, first : first + width].bitcast(FP8X4),
+                    rhs_scale=f_scales[:, first : first + width],
                     start=True,
                     stop=True,
                 )
-            tops = small.tile([P, 2], F32)
-            nc.vector.reduce_max(out=tops[:, 0:1], in_=wide[:], axis=AXIS.X)
-            nc.vector.reduce_max(out=tops[:, 1:2], in_=narrow[:, 0:REST], axis=AXIS.X)
-            top = small.tile([P, 1], F32)
-            nc.vector.tensor_tensor(out=top[:], in0=tops[:, 0:1], in1=tops[:, 1:2], op=ALU.max)
-            shift = small.tile([P, 1], F32)
-            nc.scalar.mul(out=shift[:], in_=top[:], mul=-INV_TEMPERATURE)
-            numer = work.tile([P, CELLS], F32)
-            sums = small.tile([P, 2], F32)
-            nc.scalar.activation(
-                out=numer[:, 0:BANK], in_=wide[:], func=ACT.Exp,
-                bias=shift[:], scale=INV_TEMPERATURE, accum_out=sums[:, 0:1],
-            )
-            nc.scalar.activation(
-                out=numer[:, BANK:CELLS], in_=narrow[:, 0:REST], func=ACT.Exp,
-                bias=shift[:], scale=INV_TEMPERATURE, accum_out=sums[:, 1:2],
-            )
-            peak = small.tile([P, 1], F32)
-            nc.scalar.activation(
-                out=peak[:], in_=top[:], func=ACT.Exp, bias=shift[:], scale=INV_TEMPERATURE
-            )
-            total = small.tile([P, 1], F32)
-            nc.vector.tensor_add(out=total[:], in0=sums[:, 0:1], in1=sums[:, 1:2])
-            recip = small.tile([P, 1], F32)
-            nc.vector.reciprocal(out=recip[:], in_=total[:])
-            key = small.tile([P, 1], F32)
+            sim_banks[q] = (wide, narrow)
+
+        def maxima(q):
+            n, job, is_row, i = job_parts(q)
+            if job == 0:
+                soft_t[n] = columns.tile([P, CELL_TILES, CELLS], F32, name="soft_t")
+                miss_t[n] = columns.tile([P, CELL_TILES, CELLS], BF16, name="miss_t")
+                recip[n] = columns.tile([P, JOBS_A_BATCH], F32, name="recip")
+                key[n] = columns.tile([P, JOBS_A_BATCH], F32, name="key")
+            if is_row:
+                numer[n, i] = work.tile([P, CELLS], F32, name="numer", bufs=7)
+            values = job_values(q)
+            wide, narrow = sim_banks[q]
+            top_wide = small.tile([P, 1], F32)
             nc.vector.tensor_scalar(
-                out=key[:], in0=recip[:], scalar1=THRESHOLD, scalar2=peak[:],
+                out=values[:, 0:BANK], in0=wide[:], scalar1=1.0, scalar2=None,
+                op0=ALU.mult, op1=ALU.max, accum_out=top_wide[:],
+            )
+            top[q] = small.tile([P, 1], F32, name="top")
+            nc.vector.tensor_scalar(
+                out=values[:, BANK:CELLS], in0=narrow[:, 0:REST], scalar1=1.0, scalar2=top_wide[:],
+                op0=ALU.mult, op1=ALU.max, accum_out=top[q][:],
+            )
+
+        def exponentials(q):
+            values = job_values(q)
+            shift = small.tile([P, 1], F32)
+            nc.scalar.mul(out=shift[:], in_=top[q][:], mul=-INV_TEMPERATURE)
+            total[q] = small.tile([P, 1], F32, name="total")
+            nc.scalar.activation(
+                out=values, in_=values, func=ACT.Exp,
+                bias=shift[:], scale=INV_TEMPERATURE, accum_out=total[q][:],
+            )
+            peak[q] = small.tile([P, 1], F32, name="peak")
+            nc.scalar.activation(
+                out=peak[q][:], in_=top[q][:], func=ACT.Exp, bias=shift[:], scale=INV_TEMPERATURE
+            )
+
+        def scalars(q):
+            n, job, is_row, i = job_parts(q)
+            one = slice(job, job + 1)
+            nc.vector.reciprocal(out=recip[n][:, one], in_=total[q][:])
+            nc.vector.tensor_scalar(
+                out=key[n][:, one], in0=recip[n][:, one], scalar1=THRESHOLD, scalar2=peak[q][:],
                 op0=ALU.is_le, op1=ALU.add,
             )
-            return numer, recip, key
 
+        def normalise(q):
+            n, job, is_row, i = job_parts(q)
+            one = slice(job, job + 1)
+            values = job_values(q)
+            if is_row:
+                conf0 = work.tile([P, CELLS], F32)
+                nc.gpsimd.tensor_scalar(
+                    out=conf0[:], in0=values, scalar1=recip[n][:, one], scalar2=0.0,
+                    op0=ALU.mult, op1=ALU.add,
+                )
+                nc.sync.dma_start(out=out[0, n, i * P : (i + 1) * P, :], in_=conf0[:])
+            else:
+                nc.gpsimd.tensor_scalar(
+                    out=miss_t[n][:, i, :], in0=values, scalar1=-1.0, scalar2=key[n][:, one],
+                    op0=ALU.mult, op1=ALU.add,
+                )
+                nc.gpsimd.tensor_scalar(
+                    out=values, in0=values, scalar1=recip[n][:, one], scalar2=0.0,
+                    op0=ALU.mult, op1=ALU.add,
+                )
 
-        def grid(ap):
-            return ap.rearrange("p (r w) -> p r w", w=w1c)
+        def numerator_round(q):
+            if 0 <= q + 2 < JOBS:
+                similarities(q + 2)
+            if 0 <= q + 1 < JOBS:
+                maxima(q + 1)
+            if 0 <= q < JOBS:
+                exponentials(q)
+            if 0 <= q - 1 < JOBS:
+                scalars(q - 1)
+                normalise(q - 1)
+
+        def interior(ap):
+            return ap.rearrange("p (r w) -> p r w", w=w1c)[
+                :, BORDER : h1c - BORDER, BORDER : w1c - BORDER
+            ]
 
         rows_in = h1c - 2 * BORDER
         cols_in = w1c - 2 * BORDER
-        inner_w = slice(BORDER, w1c - BORDER)
+        flipped_columns = {}
+        conf1 = {}
 
-        conf_t = {}
-        miss_t = {}
-
-        def column_tile(n, j):
-            if j == 0:
-                conf_t[n] = columns.tile([P, CELL_TILES, CELLS], F32, name="conf_t")
-                miss_t[n] = columns.tile([P, CELL_TILES, CELLS], BF16, name="miss_t")
-            f0_at = 2 * n * CELLS
-            numer, recip, key = softmax_parts(f0_at + CELLS + j * P, f0_at)
-            nc.gpsimd.tensor_scalar(
-                out=conf_t[n][:, j, :], in0=numer[:], scalar1=recip[:], scalar2=0.0,
-                op0=ALU.mult, op1=ALU.add,
-            )
-            nc.gpsimd.tensor_scalar(
-                out=miss_t[n][:, j, :], in0=numer[:], scalar1=-1.0, scalar2=key[:],
-                op0=ALU.mult, op1=ALU.add,
-            )
-
-        def row_tile(n, i):
+        def flip_columns(n, i):
             rows = slice(i * P, (i + 1) * P)
-            f0_at = 2 * n * CELLS
-            numer, recip, key = softmax_parts(f0_at + i * P, f0_at + CELLS)
-            conf0 = work.tile([P, CELLS], F32)
-            nc.gpsimd.tensor_scalar(
-                out=conf0[:], in0=numer[:], scalar1=recip[:], scalar2=0.0,
-                op0=ALU.mult, op1=ALU.add,
-            )
-            nc.sync.dma_start(out=out[0, n, rows, :], in_=conf0[:])
-
-            conf1_wide = psum.tile([P, BANK], F32, tag="bank")
-            conf1_narrow = psum.tile([P, BANK], F32, tag="bank")
-            miss1 = psum.tile([P, CELLS], BF16, tag="bank")
+            conf1_wide = psum.tile([P, BANK], F32, tag="aux")
+            conf1_narrow = psum.tile([P, BANK], F32, tag="aux")
+            miss1 = psum.tile([P, CELLS], BF16, tag="aux")
             for j in range(CELL_TILES):
                 target = conf1_wide if j < BANK // P else conf1_narrow
                 at = (j * P) % BANK
-                nc.tensor.transpose(target[:, at : at + P], conf_t[n][:, j, rows], identity[:])
+                nc.tensor.transpose(target[:, at : at + P], soft_t[n][:, j, rows], identity[:])
             for j in range(CELL_TILES):
                 nc.tensor.transpose(miss1[:, j * P : (j + 1) * P], miss_t[n][:, j, rows], identity_bf[:])
-            conf1 = work.tile([P, CELLS], F32)
-            nc.scalar.copy(out=conf1[:, 0:BANK], in_=conf1_wide[:])
-            nc.scalar.copy(out=conf1[:, BANK:CELLS], in_=conf1_narrow[:, 0:REST])
-            nc.sync.dma_start(out=out[1, n, rows, :], in_=conf1[:])
+            flipped_columns[n, i] = (conf1_wide, conf1_narrow, miss1)
 
-            inner_h = slice(BORDER, h1c - BORDER)
-            both = work.tile([P, rows_in, cols_in], F32)
+        def store_conf1(n, i):
+            conf1_wide, conf1_narrow, miss1 = flipped_columns[n, i]
+            conf1[n, i] = work.tile([P, CELLS], F32, name="conf1")
+            nc.scalar.copy(out=conf1[n, i][:, 0:BANK], in_=conf1_wide[:])
+            nc.scalar.copy(out=conf1[n, i][:, BANK:CELLS], in_=conf1_narrow[:, 0:REST])
+            nc.sync.dma_start(out=out[1, n, i * P : (i + 1) * P, :], in_=conf1[n, i][:])
+
+        def store_mconf(n, i):
+            miss1 = flipped_columns[n, i][2]
+            one = slice(CELL_TILES + i, CELL_TILES + i + 1)
+            both = work.tile([P, rows_in, cols_in], F32, bufs=2)
             nc.vector.scalar_tensor_tensor(
                 out=both[:],
-                in0=grid(numer[:])[:, inner_h, inner_w],
-                scalar=key[:],
-                in1=grid(miss1[:])[:, inner_h, inner_w],
+                in0=interior(numer[n, i][:]),
+                scalar=key[n][:, one],
+                in1=interior(miss1[:]),
                 op0=ALU.subtract,
                 op1=ALU.mult,
             )
-            best = work.tile([P, rows_in, cols_in], F32)
-            nc.vector.tensor_tensor(
+            best = work.tile([P, rows_in, cols_in], F32, bufs=2)
+            nc.vector.scalar_tensor_tensor(
                 out=best[:],
-                in0=grid(conf0[:])[:, inner_h, inner_w],
-                in1=grid(conf1[:])[:, inner_h, inner_w],
-                op=ALU.max,
+                in0=interior(numer[n, i][:]),
+                scalar=recip[n][:, one],
+                in1=interior(conf1[n, i][:]),
+                op0=ALU.mult,
+                op1=ALU.max,
             )
             mconf = mconf_tiles[i % len(mconf_tiles)]
             nc.vector.scalar_tensor_tensor(
-                out=grid(mconf[:])[:, inner_h, inner_w],
+                out=interior(mconf[:]),
                 in0=both[:],
                 scalar=row_gate[:, i : i + 1],
                 in1=best[:],
                 op0=ALU.is_ge,
                 op1=ALU.mult,
             )
-            nc.sync.dma_start(out=out[2, n, rows, :], in_=mconf[:])
+            nc.sync.dma_start(out=out[2, n, i * P : (i + 1) * P, :], in_=mconf[:])
 
-        chunks_a_batch = 2 * CELLS // CHUNK
-        tiles_a_chunk = CELL_TILES // chunks_a_batch
-        for c in range(chunks_a_batch):
-            project_chunk(c)
-        for c in range(chunks_a_batch):
-            project_chunk(chunks_a_batch + c)
-            for j in range(c * tiles_a_chunk, (c + 1) * tiles_a_chunk):
-                column_tile(0, j)
-        for i in range(CELL_TILES):
-            row_tile(0, i)
-            column_tile(1, i)
-        for i in range(CELL_TILES):
-            row_tile(1, i)
+        def output_round_flips(n, i):
+            if 0 <= i + 1 < CELL_TILES:
+                flip_columns(n, i + 1)
+
+        def output_round_rest(n, i):
+            if 0 <= i + 1 < CELL_TILES:
+                store_conf1(n, i + 1)
+            if 0 <= i < CELL_TILES:
+                store_mconf(n, i)
+
+        w_grouped = gather(flip(w_raw[:], 0))
+        front_round(-2)
+        nc.vector.quantize_mx(out=w_codes[:].bitcast(FP8X4), scales=w_scales[:], in_=w_grouped[:])
+        for k in range(-1, 4):
+            front_round(k)
+        first_output = JOBS_A_BATCH - 1
+        for q in range(-2, JOBS + 1):
+            with_output = q >= first_output and (q - first_output) % 2 == 0
+            if with_output:
+                output_round_flips(0, (q - first_output) // 2 - 1)
+            numerator_round(q)
+            if 0 <= q < 9 and q % 3 == 0:
+                front_round(4 + q // 3)
+            if with_output:
+                output_round_rest(0, (q - first_output) // 2 - 1)
+        for i in range(-1, CELL_TILES):
+            output_round_flips(1, i)
+            output_round_rest(1, i)

@@ -27,7 +27,7 @@ CHUNKS = TOKENS // CHUNK
 JOBS_A_BATCH = 2 * CELL_TILES
 JOBS = BATCH * JOBS_A_BATCH
 BORDER = 2
-THRESHOLD = 0.2
+INV_THRESHOLD = 5.0
 INV_TEMPERATURE = 10.0
 INV_SQRT_FEATURES = 1.0 / math.sqrt(FEATURES)
 
@@ -43,59 +43,80 @@ def tile_coarsematching_kernel(tc, feat_c0, feat_c1, W, b, h0c, w0c, h1c, w1c, o
     with ExitStack() as ctx:
         keep = ctx.enter_context(tc.tile_pool(name="keep", bufs=1))
         stage = ctx.enter_context(tc.tile_pool(name="stage", bufs=2))
-        columns = ctx.enter_context(tc.tile_pool(name="columns", bufs=2))
         work = ctx.enter_context(tc.tile_pool(name="work", bufs=3))
         small = ctx.enter_context(tc.tile_pool(name="small", bufs=4))
-        psum = ctx.enter_context(tc.psum_pool(name="psum", bufs=4))
+        psum = ctx.enter_context(tc.psum_pool(name="psum", bufs=1))
 
         w_raw = keep.tile([P, PACK * FEATURES], BF16)
-        nc.sync.dma_start(
-            out=w_raw[:].rearrange("p (t k) -> p t k", t=PACK),
-            in_=W.rearrange("(p t) k -> p t k", t=PACK),
-        )
+        w_raw_rows = w_raw[:].rearrange("p (t k) -> p t k", t=PACK)
+        W_rows = W.rearrange("(p t) k -> p t k", t=PACK)
+        for h in range(2):
+            nc.sync.dma_start(out=w_raw_rows[:, 2 * h : 2 * h + 2, :], in_=W_rows[:, 2 * h : 2 * h + 2, :])
         b_raw = keep.tile([P, PACK], BF16)
-        nc.sync.dma_start(out=b_raw[:], in_=b.rearrange("(p t) -> p t", t=PACK))
         x_raw = keep.tile([P, (TOKENS // P) * FEATURES], BF16)
         x_raw_tiles = x_raw[:].rearrange("p (r k) -> p r k", k=FEATURES)
-        for n in range(BATCH):
-            for g, feat in enumerate((feat_c0, feat_c1)):
-                first = (2 * n + g) * CELL_TILES
-                nc.sync.dma_start(
-                    out=x_raw_tiles[:, first : first + CELL_TILES, :],
-                    in_=feat[n].rearrange("(j p) k -> p j k", p=P),
-                )
+
+        def load_tokens(n, g, first, count):
+            feat = (feat_c0, feat_c1)[g]
+            at = (2 * n + g) * CELL_TILES + first
+            nc.sync.dma_start(
+                out=x_raw_tiles[:, at : at + count, :],
+                in_=feat[n].rearrange("(j p) k -> p j k", p=P)[:, first : first + count, :],
+            )
+
+        load_tokens(0, 0, 0, 4)
+        nc.sync.dma_start(out=b_raw[:], in_=b.rearrange("(p t) -> p t", t=PACK))
+        load_tokens(0, 0, 4, 2)
+        load_tokens(0, 1, 0, 2)
+        load_tokens(0, 1, 2, 4)
+        load_tokens(1, 0, 0, 6)
+        load_tokens(1, 1, 0, 6)
 
         identity = keep.tile([P, P], F32)
         make_identity(nc, identity[:])
         identity_bf = keep.tile([P, P], BF16)
-        nc.vector.tensor_copy(out=identity_bf[:], in_=identity[:])
+        warm = keep.tile([P, 1], F32)
+        nc.vector.memset(warm[:], 0.0)
+        nc.scalar.activation(out=warm[:], in_=warm[:], func=ACT.Exp)
 
         edge = keep.tile([P, P], F32)
-        nc.vector.memset(edge[:], 0.0)
+        nc.vector.memset(edge[:], INV_THRESHOLD)
         edge_rows = edge[:].rearrange("p (r w) -> p r w", w=w0c)
-        nc.vector.memset(edge_rows[:, :, 0:BORDER], 1.0)
-        nc.vector.memset(edge_rows[:, :, w0c - BORDER : w0c], 1.0)
-        edge_t = psum.tile([P, BANK], F32, tag="aux")
+        nc.vector.memset(edge_rows[:, :, 0:BORDER], 0.0)
+        nc.vector.memset(edge_rows[:, :, w0c - BORDER : w0c], 0.0)
+        nc.vector.tensor_copy(out=identity_bf[:], in_=identity[:])
+        edge_t = psum.tile([P, BANK], F32, tag="aux", bufs=5)
         nc.tensor.transpose(edge_t[:, 0:P], edge[:], identity[:])
-        row_gate = keep.tile([P, CELL_TILES], F32)
-        nc.vector.tensor_copy(out=row_gate[:], in_=edge_t[:, 0:CELL_TILES])
-        nc.vector.memset(row_gate[0 : BORDER * w0c, 0:1], 1.0)
-        nc.vector.memset(row_gate[P - BORDER * w0c : P, CELL_TILES - 1 : CELL_TILES], 1.0)
+        limit = keep.tile([P, CELL_TILES], F32)
+        nc.vector.tensor_copy(out=limit[:], in_=edge_t[:, 0:CELL_TILES])
+        nc.vector.memset(limit[0 : BORDER * w0c, 0:1], 0.0)
+        nc.vector.memset(limit[P - BORDER * w0c : P, CELL_TILES - 1 : CELL_TILES], 0.0)
 
         mconf_tiles = []
         for slot in range(3):
             mconf = keep.tile([P, CELLS], F32, name="mconf%d" % slot)
-            nc.vector.memset(mconf[:], 0.0)
+            nc.gpsimd.memset(mconf[:], 0.0)
             mconf_tiles.append(mconf)
+        miss_t = []
+        for n in range(BATCH):
+            miss = keep.tile([P, CELL_TILES, CELLS], BF16, name="miss_t%d" % n)
+            nc.gpsimd.memset(miss[:, :, 0 : BORDER * w0c], 1.0)
+            nc.gpsimd.memset(miss[:, :, CELLS - BORDER * w0c : CELLS], 1.0)
+            inner = miss[:].rearrange("p j (r w) -> p j r w", w=w0c)[:, :, BORDER : h0c - BORDER, :]
+            nc.gpsimd.memset(inner[:, :, :, 0:BORDER], 1.0)
+            nc.gpsimd.memset(inner[:, :, :, w0c - BORDER : w0c], 1.0)
+            miss_t.append(miss)
 
         b_scaled = keep.tile([P, PACK], F32)
-        nc.vector.tensor_scalar_mul(out=b_scaled[:], in0=b_raw[:], scalar1=INV_SQRT_FEATURES)
+
+        def aux_tile(shape, dtype, name):
+            return psum.tile(shape, dtype, tag="aux", bufs=5, name=name)
 
         def flip(raw, first_tile):
             words = raw.bitcast(F32).rearrange("p (r u q) -> p r u q", u=2, q=P)
             banks = []
             for h in range(2):
-                flipped = psum.tile([P, 2, 2, P], F32, tag="aux")
+                flipped = aux_tile([P, 2, 2, P], F32, "flipped")
                 for r in range(2):
                     for u in range(2):
                         nc.tensor.transpose(
@@ -104,10 +125,13 @@ def tile_coarsematching_kernel(tc, feat_c0, feat_c1, W, b, h0c, w0c, h1c, w1c, o
                 banks.append(flipped)
             return banks
 
-        def gather(banks):
-            grouped = stage.tile([P, CHUNK * PACK], BF16, bufs=3, align_bytes=64)
+        def gather(banks, vector_too):
+            grouped = stage.tile([P, CHUNK * PACK], BF16, name="grouped", bufs=3, align_bytes=64)
             halves = grouped[:].bitcast(F32).rearrange("p (h r c u) -> p h r c u", h=2, r=2, u=2)
-            nc.vector.tensor_copy(out=halves[:, 0], in_=banks[0][:].rearrange("p r u c -> p r c u"))
+            if vector_too:
+                nc.vector.tensor_copy(out=halves[:, 0], in_=banks[0][:].rearrange("p r u c -> p r c u"))
+            else:
+                nc.scalar.copy(out=halves[:, 0], in_=banks[0][:].rearrange("p r u c -> p r c u"))
             nc.scalar.copy(out=halves[:, 1], in_=banks[1][:].rearrange("p r u c -> p r c u"))
             return grouped
 
@@ -125,17 +149,24 @@ def tile_coarsematching_kernel(tc, feat_c0, feat_c1, W, b, h0c, w0c, h1c, w1c, o
         def chunk_columns(c):
             return slice(c * CHUNK, (c + 1) * CHUNK)
 
+        def flip_tokens(c):
+            x_banks[c] = flip(x_raw[:], c * CHUNK_TILES)
+
+        def gather_tokens(c, vector_too):
+            x_grouped[c] = gather(x_banks[c], vector_too)
+
         def quantise_tokens(c):
             cols = chunk_columns(c)
             nc.vector.quantize_mx(
                 out=x_codes[:, cols].bitcast(FP8X4), scales=x_scales[:, cols], in_=x_grouped[c][:]
             )
 
-        def project(c):
+        def project(c, first, last):
             cols = chunk_columns(c)
-            f_rows[c] = stage.tile([P, PACK, CHUNK], BF16, name="f_rows")
-            for t in range(PACK):
-                acc = psum.tile([P, BANK], F32, tag="aux")
+            if first == 0:
+                f_rows[c] = stage.tile([P, PACK, CHUNK], BF16, name="f_rows")
+            for t in range(first, last):
+                acc = aux_tile([P, BANK], F32, "acc")
                 nc.tensor.matmul_mx(
                     out=acc[:],
                     lhsT=w_codes[:, t * P : (t + 1) * P].bitcast(FP8X4),
@@ -168,29 +199,14 @@ def tile_coarsematching_kernel(tc, feat_c0, feat_c1, W, b, h0c, w0c, h1c, w1c, o
                 in_=f_grouped[c][:].rearrange("p c t -> p (c t)"),
             )
 
-        def front_round(k):
-            if 0 <= k < CHUNKS:
-                project(k)
-            if 0 <= k - 1 < CHUNKS:
-                regroup(k - 1)
-            if 0 <= k + 1 < CHUNKS:
-                quantise_tokens(k + 1)
-            if 0 <= k + 2 < CHUNKS:
-                x_banks[k + 2] = flip(x_raw[:], (k + 2) * CHUNK_TILES)
-            if 0 <= k - 1 < CHUNKS:
-                quantise_features(k - 1)
-            if 0 <= k + 2 < CHUNKS:
-                x_grouped[k + 2] = gather(x_banks[k + 2])
-
         soft_t = {}
-        miss_t = {}
+        total = {}
         recip = {}
         key = {}
         numer = {}
         sim_banks = {}
-        top = {}
-        total = {}
-        peak = {}
+        low_wide = {}
+        low = {}
 
         def job_parts(q):
             n, job = divmod(q, JOBS_A_BATCH)
@@ -207,8 +223,8 @@ def tile_coarsematching_kernel(tc, feat_c0, feat_c1, W, b, h0c, w0c, h1c, w1c, o
             f1_at = f0_at + CELLS
             at = (f0_at if is_row else f1_at) + i * P
             along = f1_at if is_row else f0_at
-            wide = psum.tile([P, BANK], F32, tag="sim")
-            narrow = psum.tile([P, BANK], F32, tag="sim")
+            wide = psum.tile([P, BANK], F32, name="wide", bufs=2)
+            narrow = psum.tile([P, BANK], F32, name="narrow", bufs=1)
             for acc, first, width in ((wide, along, BANK), (narrow, along + BANK, REST)):
                 nc.tensor.matmul_mx(
                     out=acc[:, 0:width],
@@ -221,57 +237,56 @@ def tile_coarsematching_kernel(tc, feat_c0, feat_c1, W, b, h0c, w0c, h1c, w1c, o
                 )
             sim_banks[q] = (wide, narrow)
 
-        def maxima(q):
+        def minimum_wide(q):
             n, job, is_row, i = job_parts(q)
             if job == 0:
-                soft_t[n] = columns.tile([P, CELL_TILES, CELLS], F32, name="soft_t")
-                miss_t[n] = columns.tile([P, CELL_TILES, CELLS], BF16, name="miss_t")
-                recip[n] = columns.tile([P, JOBS_A_BATCH], F32, name="recip")
-                key[n] = columns.tile([P, JOBS_A_BATCH], F32, name="key")
+                soft_t[n] = keep.tile([P, CELL_TILES, CELLS], F32, name="soft_t%d" % n)
+                total[n] = keep.tile([P, JOBS_A_BATCH], F32, name="total%d" % n)
+                recip[n] = keep.tile([P, JOBS_A_BATCH], F32, name="recip%d" % n)
+                key[n] = keep.tile([P, JOBS_A_BATCH], F32, name="key%d" % n)
             if is_row:
                 numer[n, i] = work.tile([P, CELLS], F32, name="numer", bufs=7)
-            values = job_values(q)
-            wide, narrow = sim_banks[q]
-            top_wide = small.tile([P, 1], F32)
+            low_wide[q] = small.tile([P, 1], F32, name="low_wide")
             nc.vector.tensor_scalar(
-                out=values[:, 0:BANK], in0=wide[:], scalar1=1.0, scalar2=None,
-                op0=ALU.mult, op1=ALU.max, accum_out=top_wide[:],
+                out=job_values(q)[:, 0:BANK], in0=sim_banks[q][0][:], scalar1=-INV_TEMPERATURE,
+                scalar2=None, op0=ALU.mult, op1=ALU.min, accum_out=low_wide[q][:],
             )
-            top[q] = small.tile([P, 1], F32, name="top")
+
+        def minimum_narrow(q):
+            low[q] = small.tile([P, 1], F32, name="low")
             nc.vector.tensor_scalar(
-                out=values[:, BANK:CELLS], in0=narrow[:, 0:REST], scalar1=1.0, scalar2=top_wide[:],
-                op0=ALU.mult, op1=ALU.max, accum_out=top[q][:],
+                out=job_values(q)[:, BANK:CELLS], in0=sim_banks[q][1][:, 0:REST], scalar1=-INV_TEMPERATURE,
+                scalar2=low_wide[q][:], op0=ALU.mult, op1=ALU.min, accum_out=low[q][:],
             )
 
         def exponentials(q):
-            values = job_values(q)
-            shift = small.tile([P, 1], F32)
-            nc.scalar.mul(out=shift[:], in_=top[q][:], mul=-INV_TEMPERATURE)
-            total[q] = small.tile([P, 1], F32, name="total")
+            n, job, is_row, i = job_parts(q)
             nc.scalar.activation(
-                out=values, in_=values, func=ACT.Exp,
-                bias=shift[:], scale=INV_TEMPERATURE, accum_out=total[q][:],
-            )
-            peak[q] = small.tile([P, 1], F32, name="peak")
-            nc.scalar.activation(
-                out=peak[q][:], in_=top[q][:], func=ACT.Exp, bias=shift[:], scale=INV_TEMPERATURE
+                out=job_values(q), in_=job_values(q), func=ACT.Exp,
+                bias=low[q][:], scale=-1.0, accum_out=total[n][:, job : job + 1],
             )
 
         def scalars(q):
             n, job, is_row, i = job_parts(q)
             one = slice(job, job + 1)
-            nc.vector.reciprocal(out=recip[n][:, one], in_=total[q][:])
-            nc.vector.tensor_scalar(
-                out=key[n][:, one], in0=recip[n][:, one], scalar1=THRESHOLD, scalar2=peak[q][:],
-                op0=ALU.is_le, op1=ALU.add,
-            )
+            nc.vector.reciprocal(out=recip[n][:, one], in_=total[n][:, one])
+            if is_row:
+                nc.vector.tensor_scalar(
+                    out=key[n][:, one], in0=total[n][:, one], scalar1=limit[:, i : i + 1], scalar2=1.0,
+                    op0=ALU.is_ge, op1=ALU.add,
+                )
+            else:
+                nc.vector.tensor_scalar(
+                    out=key[n][:, one], in0=total[n][:, one], scalar1=INV_THRESHOLD, scalar2=0.5,
+                    op0=ALU.is_ge, op1=ALU.max,
+                )
 
         def normalise(q):
             n, job, is_row, i = job_parts(q)
             one = slice(job, job + 1)
             values = job_values(q)
             if is_row:
-                conf0 = work.tile([P, CELLS], F32)
+                conf0 = work.tile([P, CELLS], F32, name="conf0")
                 nc.gpsimd.tensor_scalar(
                     out=conf0[:], in0=values, scalar1=recip[n][:, one], scalar2=0.0,
                     op0=ALU.mult, op1=ALU.add,
@@ -279,40 +294,32 @@ def tile_coarsematching_kernel(tc, feat_c0, feat_c1, W, b, h0c, w0c, h1c, w1c, o
                 nc.sync.dma_start(out=out[0, n, i * P : (i + 1) * P, :], in_=conf0[:])
             else:
                 nc.gpsimd.tensor_scalar(
-                    out=miss_t[n][:, i, :], in0=values, scalar1=-1.0, scalar2=key[n][:, one],
-                    op0=ALU.mult, op1=ALU.add,
+                    out=inner_rows(miss_t[n][:, i, :]), in0=inner_rows(values), scalar1=-0.5,
+                    scalar2=key[n][:, one], op0=ALU.mult, op1=ALU.add,
                 )
                 nc.gpsimd.tensor_scalar(
                     out=values, in0=values, scalar1=recip[n][:, one], scalar2=0.0,
                     op0=ALU.mult, op1=ALU.add,
                 )
 
-        def numerator_round(q):
-            if 0 <= q + 2 < JOBS:
-                similarities(q + 2)
-            if 0 <= q + 1 < JOBS:
-                maxima(q + 1)
-            if 0 <= q < JOBS:
-                exponentials(q)
-            if 0 <= q - 1 < JOBS:
-                scalars(q - 1)
-                normalise(q - 1)
+        def inner_rows(ap):
+            return ap.rearrange("p (r w) -> p r w", w=w0c)[:, BORDER : h0c - BORDER, BORDER : w0c - BORDER]
 
         def interior(ap):
-            return ap.rearrange("p (r w) -> p r w", w=w1c)[
-                :, BORDER : h1c - BORDER, BORDER : w1c - BORDER
-            ]
+            return ap.rearrange("p (r w) -> p r w", w=w1c)[:, BORDER : h1c - BORDER, BORDER : w1c - BORDER]
 
         rows_in = h1c - 2 * BORDER
         cols_in = w1c - 2 * BORDER
+        rows_wide = BANK // w1c - BORDER
         flipped_columns = {}
-        conf1 = {}
+        best = {}
+        mask = {}
 
         def flip_columns(n, i):
             rows = slice(i * P, (i + 1) * P)
-            conf1_wide = psum.tile([P, BANK], F32, tag="aux")
-            conf1_narrow = psum.tile([P, BANK], F32, tag="aux")
-            miss1 = psum.tile([P, CELLS], BF16, tag="aux")
+            conf1_wide = aux_tile([P, BANK], F32, "conf1_wide")
+            conf1_narrow = aux_tile([P, BANK], F32, "conf1_narrow")
+            miss1 = aux_tile([P, CELLS], BF16, "miss1")
             for j in range(CELL_TILES):
                 target = conf1_wide if j < BANK // P else conf1_narrow
                 at = (j * P) % BANK
@@ -323,68 +330,123 @@ def tile_coarsematching_kernel(tc, feat_c0, feat_c1, W, b, h0c, w0c, h1c, w1c, o
 
         def store_conf1(n, i):
             conf1_wide, conf1_narrow, miss1 = flipped_columns[n, i]
-            conf1[n, i] = work.tile([P, CELLS], F32, name="conf1")
-            nc.scalar.copy(out=conf1[n, i][:, 0:BANK], in_=conf1_wide[:])
-            nc.scalar.copy(out=conf1[n, i][:, BANK:CELLS], in_=conf1_narrow[:, 0:REST])
-            nc.sync.dma_start(out=out[1, n, i * P : (i + 1) * P, :], in_=conf1[n, i][:])
+            conf1 = work.tile([P, CELLS], F32, name="conf1")
+            nc.scalar.copy(out=conf1[:, 0:BANK], in_=conf1_wide[:])
+            nc.scalar.copy(out=conf1[:, BANK:CELLS], in_=conf1_narrow[:, 0:REST])
+            nc.sync.dma_start(out=out[1, n, i * P : (i + 1) * P, :], in_=conf1[:])
 
-        def store_mconf(n, i):
+        def keep_mask(n, i):
             miss1 = flipped_columns[n, i][2]
             one = slice(CELL_TILES + i, CELL_TILES + i + 1)
-            both = work.tile([P, rows_in, cols_in], F32, bufs=2)
+            mask[n, i] = work.tile([P, rows_in, cols_in], BF16, name="mask")
             nc.vector.scalar_tensor_tensor(
-                out=both[:],
-                in0=interior(numer[n, i][:]),
-                scalar=key[n][:, one],
-                in1=interior(miss1[:]),
-                op0=ALU.subtract,
-                op1=ALU.mult,
+                out=mask[n, i][:], in0=interior(numer[n, i][:]), scalar=key[n][:, one],
+                in1=interior(miss1[:]), op0=ALU.is_ge, op1=ALU.is_ge,
             )
-            best = work.tile([P, rows_in, cols_in], F32, bufs=2)
+
+        def best_of_two(n, i, second):
+            one = slice(CELL_TILES + i, CELL_TILES + i + 1)
+            if not second:
+                best[n, i] = work.tile([P, rows_in, cols_in], F32, name="best")
+            grid = flipped_columns[n, i][1 if second else 0][:].rearrange("p (r w) -> p r w", w=w1c)
+            rows = slice(rows_wide, rows_in) if second else slice(0, rows_wide)
+            first = 0 if second else BORDER
             nc.vector.scalar_tensor_tensor(
-                out=best[:],
-                in0=interior(numer[n, i][:]),
+                out=best[n, i][:, rows, :],
+                in0=interior(numer[n, i][:])[:, rows, :],
                 scalar=recip[n][:, one],
-                in1=interior(conf1[n, i][:]),
+                in1=grid[:, first : first + rows.stop - rows.start, BORDER : w1c - BORDER],
                 op0=ALU.mult,
                 op1=ALU.max,
             )
+
+        def store_mconf(n, i):
             mconf = mconf_tiles[i % len(mconf_tiles)]
-            nc.vector.scalar_tensor_tensor(
-                out=interior(mconf[:]),
-                in0=both[:],
-                scalar=row_gate[:, i : i + 1],
-                in1=best[:],
-                op0=ALU.is_ge,
-                op1=ALU.mult,
+            nc.gpsimd.tensor_tensor(
+                out=interior(mconf[:]), in0=mask[n, i][:], in1=best[n, i][:], op=ALU.mult
             )
             nc.sync.dma_start(out=out[2, n, i * P : (i + 1) * P, :], in_=mconf[:])
 
-        def output_round_flips(n, i):
-            if 0 <= i + 1 < CELL_TILES:
-                flip_columns(n, i + 1)
-
-        def output_round_rest(n, i):
-            if 0 <= i + 1 < CELL_TILES:
-                store_conf1(n, i + 1)
-            if 0 <= i < CELL_TILES:
-                store_mconf(n, i)
-
-        w_grouped = gather(flip(w_raw[:], 0))
-        front_round(-2)
+        w_banks = flip(w_raw[:], 0)
+        w_grouped = gather(w_banks, True)
+        flip_tokens(0)
         nc.vector.quantize_mx(out=w_codes[:].bitcast(FP8X4), scales=w_scales[:], in_=w_grouped[:])
-        for k in range(-1, 4):
-            front_round(k)
-        first_output = JOBS_A_BATCH - 1
-        for q in range(-2, JOBS + 1):
-            with_output = q >= first_output and (q - first_output) % 2 == 0
-            if with_output:
-                output_round_flips(0, (q - first_output) // 2 - 1)
-            numerator_round(q)
-            if 0 <= q < 9 and q % 3 == 0:
-                front_round(4 + q // 3)
-            if with_output:
-                output_round_rest(0, (q - first_output) // 2 - 1)
-        for i in range(-1, CELL_TILES):
-            output_round_flips(1, i)
-            output_round_rest(1, i)
+        gather_tokens(0, True)
+        nc.vector.tensor_scalar_mul(out=b_scaled[:], in0=b_raw[:], scalar1=INV_SQRT_FEATURES)
+        quantise_tokens(0)
+        flip_tokens(1)
+        gather_tokens(1, True)
+        project(0, 0, PACK)
+        quantise_tokens(1)
+        flip_tokens(2)
+        regroup(0)
+        gather_tokens(2, True)
+        project(1, 0, PACK)
+        quantise_features(0)
+        quantise_tokens(2)
+        regroup(1)
+        project(2, 0, PACK)
+        quantise_features(1)
+
+        front = {}
+        for c in range(3, CHUNKS):
+            at = 3 * (c - 3) - 1
+            front[at] = front.get(at, []) + [("flip", c)]
+            front[at + 1] = front.get(at + 1, []) + [("first half", c)]
+            front[at + 2] = front.get(at + 2, []) + [("second half", c)]
+            front[at + 3] = front.get(at + 3, []) + [("regroup", c)]
+            front[at + 4] = front.get(at + 4, []) + [("quantise", c)]
+
+        def front_step(step, c):
+            if step == "flip":
+                flip_tokens(c)
+                gather_tokens(c, False)
+            elif step == "first half":
+                quantise_tokens(c)
+                project(c, 0, 2)
+            elif step == "second half":
+                project(c, 2, PACK)
+            elif step == "regroup":
+                regroup(c)
+            else:
+                quantise_features(c)
+
+        def output_job(o):
+            return (o // CELL_TILES) * JOBS_A_BATCH + CELL_TILES + o % CELL_TILES
+
+        outputs = [divmod(o, CELL_TILES) for o in range(BATCH * CELL_TILES)]
+        out_at = {output_job(o): outputs[o] for o in range(len(outputs))}
+
+        for q in range(-2, JOBS + 4):
+            flips = out_at.get(q - 1)
+            shown = out_at.get(q - 2)
+            if 0 <= q + 2 < JOBS:
+                similarities(q + 2)
+            if flips:
+                flip_columns(*flips)
+            if q == -2:
+                regroup(2)
+            if q == -1:
+                quantise_features(2)
+            if 0 <= q + 1 < JOBS:
+                minimum_wide(q + 1)
+            if 0 <= q < JOBS:
+                exponentials(q)
+            if shown:
+                keep_mask(*shown)
+            for step, c in front.get(q, []):
+                front_step(step, c)
+            if 0 <= q + 1 < JOBS:
+                minimum_narrow(q + 1)
+            if shown:
+                best_of_two(*shown, False)
+            if 0 <= q - 1 < JOBS:
+                scalars(q - 1)
+            if shown:
+                best_of_two(*shown, True)
+            if flips:
+                store_conf1(*flips)
+            if 0 <= q - 1 < JOBS:
+                normalise(q - 1)
+            if shown:
+                store_mconf(*shown)

@@ -95,16 +95,16 @@ def tile_coarsematching_kernel(tc, feat_c0, feat_c1, W, b, h0c, w0c, h1c, w1c, o
         mconf_tiles = []
         for slot in range(3):
             mconf = keep.tile([P, CELLS], F32, name="mconf%d" % slot)
-            nc.gpsimd.memset(mconf[:], 0.0)
+            nc.vector.memset(mconf[:], 0.0)
             mconf_tiles.append(mconf)
         miss_t = []
         for n in range(BATCH):
             miss = keep.tile([P, CELL_TILES, CELLS], BF16, name="miss_t%d" % n)
-            nc.gpsimd.memset(miss[:, :, 0 : BORDER * w0c], 1.0)
-            nc.gpsimd.memset(miss[:, :, CELLS - BORDER * w0c : CELLS], 1.0)
+            nc.vector.memset(miss[:, :, 0 : BORDER * w0c], 1.0)
+            nc.vector.memset(miss[:, :, CELLS - BORDER * w0c : CELLS], 1.0)
             inner = miss[:].rearrange("p j (r w) -> p j r w", w=w0c)[:, :, BORDER : h0c - BORDER, :]
-            nc.gpsimd.memset(inner[:, :, :, 0:BORDER], 1.0)
-            nc.gpsimd.memset(inner[:, :, :, w0c - BORDER : w0c], 1.0)
+            nc.vector.memset(inner[:, :, :, 0:BORDER], 1.0)
+            nc.vector.memset(inner[:, :, :, w0c - BORDER : w0c], 1.0)
             miss_t.append(miss)
 
         b_scaled = keep.tile([P, PACK], F32)

@@ -27,6 +27,11 @@ CHUNKS = TOKENS // CHUNK
 JOBS_A_BATCH = 2 * CELL_TILES
 JOBS = BATCH * JOBS_A_BATCH
 BORDER = 2
+VECTOR_BIAS = ()
+SCALAR_CONF1 = (12, 14, 16)
+OUT_SLOT = (8, 9, 10, 11, 12, 13, 19, 20, 21, 22, 23, 24)
+REPEAT = (1, 1)
+GPSIMD_REGROUP = ()
 INV_THRESHOLD = 5.0
 INV_TEMPERATURE = 10.0
 INV_SQRT_FEATURES = 1.0 / math.sqrt(FEATURES)
@@ -37,8 +42,10 @@ FLOPS = 2 * TOKENS * FEATURES * FEATURES + 2 * BATCH * CELLS * CELLS * FEATURES
 def tile_coarsematching_kernel(tc, feat_c0, feat_c1, W, b, h0c, w0c, h1c, w1c, out):
     nc = tc.nc
     assert h0c * w0c == CELLS and h1c * w1c == CELLS
-    assert P % w0c == 0 and BANK % w1c == 0
+    assert h0c == h1c and w0c == w1c and P % w0c == 0
     assert BORDER * w0c <= P // 2 and BORDER * w0c % 32 == 0
+
+    FIRST, LAST = BORDER * w0c, CELLS - BORDER * w0c
 
     with ExitStack() as ctx:
         keep = ctx.enter_context(tc.tile_pool(name="keep", bufs=1))
@@ -100,11 +107,10 @@ def tile_coarsematching_kernel(tc, feat_c0, feat_c1, W, b, h0c, w0c, h1c, w1c, o
         miss_t = []
         for n in range(BATCH):
             miss = keep.tile([P, CELL_TILES, CELLS], BF16, name="miss_t%d" % n)
-            nc.vector.memset(miss[:, :, 0 : BORDER * w0c], 1.0)
-            nc.vector.memset(miss[:, :, CELLS - BORDER * w0c : CELLS], 1.0)
-            inner = miss[:].rearrange("p j (r w) -> p j r w", w=w0c)[:, :, BORDER : h0c - BORDER, :]
-            nc.vector.memset(inner[:, :, :, 0:BORDER], 1.0)
-            nc.vector.memset(inner[:, :, :, w0c - BORDER : w0c], 1.0)
+            nc.vector.memset(miss[:, :, 0:FIRST], 1.0)
+            nc.vector.memset(miss[:, :, LAST:CELLS], 1.0)
+            seams = miss[:, :, FIRST - BORDER : LAST - BORDER + w0c].rearrange("p j (r w) -> p j r w", w=w0c)
+            nc.vector.memset(seams[:, :, :, 0 : 2 * BORDER], 1.0)
             miss_t.append(miss)
 
         b_scaled = keep.tile([P, PACK], F32)
@@ -176,20 +182,30 @@ def tile_coarsematching_kernel(tc, feat_c0, feat_c1, W, b, h0c, w0c, h1c, w1c, o
                     start=True,
                     stop=True,
                 )
-                nc.scalar.activation(
-                    out=f_rows[c][:, t, :],
-                    in_=acc[:],
-                    func=ACT.Identity,
-                    bias=b_scaled[:, t : t + 1],
-                    scale=INV_SQRT_FEATURES,
-                )
+                if (c, t) in VECTOR_BIAS:
+                    nc.vector.tensor_scalar(
+                        out=f_rows[c][:, t, :], in0=acc[:], scalar1=INV_SQRT_FEATURES,
+                        scalar2=b_scaled[:, t : t + 1], op0=ALU.mult, op1=ALU.add,
+                    )
+                else:
+                    nc.scalar.activation(
+                        out=f_rows[c][:, t, :], in_=acc[:], func=ACT.Identity,
+                        bias=b_scaled[:, t : t + 1], scale=INV_SQRT_FEATURES,
+                    )
 
         def regroup(c):
             f_grouped[c] = stage.tile([P, CHUNK, PACK], BF16, name="f_grouped", align_bytes=64)
-            nc.vector.tensor_copy(
-                out=f_grouped[c][:].rearrange("p (c i) t -> p c t i", i=4),
-                in_=f_rows[c][:].rearrange("p t (c i) -> p c t i", i=4),
-            )
+            if c in GPSIMD_REGROUP:
+                nc.gpsimd.tensor_scalar(
+                    out=f_grouped[c][:].rearrange("p (c i) t -> p c t i", i=4),
+                    in0=f_rows[c][:].rearrange("p t (c i) -> p c t i", i=4),
+                    scalar1=1.0, scalar2=0.0, op0=ALU.mult, op1=ALU.add,
+                )
+            else:
+                nc.vector.tensor_copy(
+                    out=f_grouped[c][:].rearrange("p (c i) t -> p c t i", i=4),
+                    in_=f_rows[c][:].rearrange("p t (c i) -> p c t i", i=4),
+                )
 
         def quantise_features(c):
             cols = chunk_columns(c)
@@ -208,6 +224,16 @@ def tile_coarsematching_kernel(tc, feat_c0, feat_c1, W, b, h0c, w0c, h1c, w1c, o
         low_wide = {}
         low = {}
 
+        def inner_rows(ap):
+            return ap.rearrange("p (r w) -> p r w", w=w0c)[:, BORDER : h0c - BORDER, BORDER : w0c - BORDER]
+
+        def interior(ap):
+            return ap.rearrange("p (r w) -> p r w", w=w1c)[:, BORDER : h1c - BORDER, BORDER : w1c - BORDER]
+
+        rows_in = h1c - 2 * BORDER
+        cols_in = w1c - 2 * BORDER
+        rows_wide = BANK // w1c - BORDER
+
         def job_parts(q):
             n, job = divmod(q, JOBS_A_BATCH)
             is_row, i = divmod(job, CELL_TILES)
@@ -217,25 +243,28 @@ def tile_coarsematching_kernel(tc, feat_c0, feat_c1, W, b, h0c, w0c, h1c, w1c, o
             n, job, is_row, i = job_parts(q)
             return numer[n, i][:] if is_row else soft_t[n][:, i, :]
 
-        def similarities(q):
+        def similarities(q, rest):
             n, job, is_row, i = job_parts(q)
             f0_at = 2 * n * CELLS
             f1_at = f0_at + CELLS
             at = (f0_at if is_row else f1_at) + i * P
             along = f1_at if is_row else f0_at
-            wide = psum.tile([P, BANK], F32, name="wide", bufs=2)
-            narrow = psum.tile([P, BANK], F32, name="narrow", bufs=1)
-            for acc, first, width in ((wide, along, BANK), (narrow, along + BANK, REST)):
-                nc.tensor.matmul_mx(
-                    out=acc[:, 0:width],
-                    lhsT=f_codes[:, at : at + P].bitcast(FP8X4),
-                    lhsT_scale=f_scales[:, at : at + P],
-                    rhs=f_codes[:, first : first + width].bitcast(FP8X4),
-                    rhs_scale=f_scales[:, first : first + width],
-                    start=True,
-                    stop=True,
-                )
-            sim_banks[q] = (wide, narrow)
+            if rest:
+                acc = psum.tile([P, BANK], F32, name="narrow", bufs=1)
+            else:
+                acc = psum.tile([P, BANK], F32, name="wide", bufs=2)
+            first, width = (along + BANK, REST) if rest else (along, BANK)
+            for again in range(REPEAT[is_row] if not rest else 1):
+              nc.tensor.matmul_mx(
+                out=acc[:, 0:width],
+                lhsT=f_codes[:, at : at + P].bitcast(FP8X4),
+                lhsT_scale=f_scales[:, at : at + P],
+                rhs=f_codes[:, first : first + width].bitcast(FP8X4),
+                rhs_scale=f_scales[:, first : first + width],
+                start=True,
+                stop=True,
+              )
+            sim_banks[q, rest] = acc
 
         def minimum_wide(q):
             n, job, is_row, i = job_parts(q)
@@ -248,14 +277,14 @@ def tile_coarsematching_kernel(tc, feat_c0, feat_c1, W, b, h0c, w0c, h1c, w1c, o
                 numer[n, i] = work.tile([P, CELLS], F32, name="numer", bufs=7)
             low_wide[q] = small.tile([P, 1], F32, name="low_wide")
             nc.vector.tensor_scalar(
-                out=job_values(q)[:, 0:BANK], in0=sim_banks[q][0][:], scalar1=-INV_TEMPERATURE,
+                out=job_values(q)[:, 0:BANK], in0=sim_banks[q, False][:], scalar1=-INV_TEMPERATURE,
                 scalar2=None, op0=ALU.mult, op1=ALU.min, accum_out=low_wide[q][:],
             )
 
         def minimum_narrow(q):
             low[q] = small.tile([P, 1], F32, name="low")
             nc.vector.tensor_scalar(
-                out=job_values(q)[:, BANK:CELLS], in0=sim_banks[q][1][:, 0:REST], scalar1=-INV_TEMPERATURE,
+                out=job_values(q)[:, BANK:CELLS], in0=sim_banks[q, True][:, 0:REST], scalar1=-INV_TEMPERATURE,
                 scalar2=low_wide[q][:], op0=ALU.mult, op1=ALU.min, accum_out=low[q][:],
             )
 
@@ -277,8 +306,8 @@ def tile_coarsematching_kernel(tc, feat_c0, feat_c1, W, b, h0c, w0c, h1c, w1c, o
                 )
             else:
                 nc.vector.tensor_scalar(
-                    out=key[n][:, one], in0=total[n][:, one], scalar1=INV_THRESHOLD, scalar2=0.5,
-                    op0=ALU.is_ge, op1=ALU.max,
+                    out=key[n][:, one], in0=total[n][:, one], scalar1=INV_THRESHOLD,
+                    scalar2=0.5, op0=ALU.is_ge, op1=ALU.max,
                 )
 
         def normalise(q):
@@ -297,46 +326,43 @@ def tile_coarsematching_kernel(tc, feat_c0, feat_c1, W, b, h0c, w0c, h1c, w1c, o
                     out=inner_rows(miss_t[n][:, i, :]), in0=inner_rows(values), scalar1=-0.5,
                     scalar2=key[n][:, one], op0=ALU.mult, op1=ALU.add,
                 )
-                nc.gpsimd.tensor_scalar(
-                    out=values, in0=values, scalar1=recip[n][:, one], scalar2=0.0,
-                    op0=ALU.mult, op1=ALU.add,
-                )
+                if q in SCALAR_CONF1:
+                    nc.scalar.activation(out=values, in_=values, func=ACT.Copy, scale=recip[n][:, one])
+                else:
+                    nc.gpsimd.tensor_scalar(
+                        out=values, in0=values, scalar1=recip[n][:, one], scalar2=0.0,
+                        op0=ALU.mult, op1=ALU.add,
+                    )
 
-        def inner_rows(ap):
-            return ap.rearrange("p (r w) -> p r w", w=w0c)[:, BORDER : h0c - BORDER, BORDER : w0c - BORDER]
-
-        def interior(ap):
-            return ap.rearrange("p (r w) -> p r w", w=w1c)[:, BORDER : h1c - BORDER, BORDER : w1c - BORDER]
-
-        rows_in = h1c - 2 * BORDER
-        cols_in = w1c - 2 * BORDER
-        rows_wide = BANK // w1c - BORDER
         flipped_columns = {}
+        flipped_miss = {}
         best = {}
         mask = {}
 
-        def flip_columns(n, i):
+        def flip_conf1(n, i):
             rows = slice(i * P, (i + 1) * P)
-            conf1_wide = aux_tile([P, BANK], F32, "conf1_wide")
-            conf1_narrow = aux_tile([P, BANK], F32, "conf1_narrow")
+            banks = (aux_tile([P, BANK], F32, "conf1_wide"), aux_tile([P, BANK], F32, "conf1_narrow"))
+            for j in range(CELL_TILES):
+                at = (j * P) % BANK
+                nc.tensor.transpose(banks[j * P // BANK][:, at : at + P], soft_t[n][:, j, rows], identity[:])
+            flipped_columns[n, i] = banks
+
+        def flip_miss(n, i):
+            rows = slice(i * P, (i + 1) * P)
             miss1 = aux_tile([P, CELLS], BF16, "miss1")
             for j in range(CELL_TILES):
-                target = conf1_wide if j < BANK // P else conf1_narrow
-                at = (j * P) % BANK
-                nc.tensor.transpose(target[:, at : at + P], soft_t[n][:, j, rows], identity[:])
-            for j in range(CELL_TILES):
                 nc.tensor.transpose(miss1[:, j * P : (j + 1) * P], miss_t[n][:, j, rows], identity_bf[:])
-            flipped_columns[n, i] = (conf1_wide, conf1_narrow, miss1)
+            flipped_miss[n, i] = miss1
 
         def store_conf1(n, i):
-            conf1_wide, conf1_narrow, miss1 = flipped_columns[n, i]
+            conf1_wide, conf1_narrow = flipped_columns[n, i]
             conf1 = work.tile([P, CELLS], F32, name="conf1")
             nc.scalar.copy(out=conf1[:, 0:BANK], in_=conf1_wide[:])
             nc.scalar.copy(out=conf1[:, BANK:CELLS], in_=conf1_narrow[:, 0:REST])
             nc.sync.dma_start(out=out[1, n, i * P : (i + 1) * P, :], in_=conf1[:])
 
         def keep_mask(n, i):
-            miss1 = flipped_columns[n, i][2]
+            miss1 = flipped_miss[n, i]
             one = slice(CELL_TILES + i, CELL_TILES + i + 1)
             mask[n, i] = work.tile([P, rows_in, cols_in], BF16, name="mask")
             nc.vector.scalar_tensor_tensor(
@@ -360,11 +386,10 @@ def tile_coarsematching_kernel(tc, feat_c0, feat_c1, W, b, h0c, w0c, h1c, w1c, o
                 op1=ALU.max,
             )
 
-        def store_mconf(n, i):
+        def store_mconf(n, i, on_vector):
             mconf = mconf_tiles[i % len(mconf_tiles)]
-            nc.gpsimd.tensor_tensor(
-                out=interior(mconf[:]), in0=mask[n, i][:], in1=best[n, i][:], op=ALU.mult
-            )
+            engine = nc.vector if on_vector else nc.gpsimd
+            engine.tensor_tensor(out=interior(mconf[:]), in0=mask[n, i][:], in1=best[n, i][:], op=ALU.mult)
             nc.sync.dma_start(out=out[2, n, i * P : (i + 1) * P, :], in_=mconf[:])
 
         w_banks = flip(w_raw[:], 0)
@@ -391,18 +416,16 @@ def tile_coarsematching_kernel(tc, feat_c0, feat_c1, W, b, h0c, w0c, h1c, w1c, o
         front = {}
         for c in range(3, CHUNKS):
             at = 3 * (c - 3) - 1
-            front[at] = front.get(at, []) + [("flip", c)]
-            front[at + 1] = front.get(at + 1, []) + [("first half", c)]
-            front[at + 2] = front.get(at + 2, []) + [("second half", c)]
-            front[at + 3] = front.get(at + 3, []) + [("regroup", c)]
-            front[at + 4] = front.get(at + 4, []) + [("quantise", c)]
+            for k, step in enumerate(("flip", "quantise x", "first half", "second half", "regroup", "quantise f")):
+                front[at + k] = front.get(at + k, []) + [(step, c)]
 
         def front_step(step, c):
             if step == "flip":
                 flip_tokens(c)
                 gather_tokens(c, False)
-            elif step == "first half":
+            elif step == "quantise x":
                 quantise_tokens(c)
+            elif step == "first half":
                 project(c, 0, 2)
             elif step == "second half":
                 project(c, 2, PACK)
@@ -411,42 +434,39 @@ def tile_coarsematching_kernel(tc, feat_c0, feat_c1, W, b, h0c, w0c, h1c, w1c, o
             else:
                 quantise_features(c)
 
-        def output_job(o):
-            return (o // CELL_TILES) * JOBS_A_BATCH + CELL_TILES + o % CELL_TILES
+        flips_at = dict((OUT_SLOT[o], divmod(o, CELL_TILES)) for o in range(BATCH * CELL_TILES))
 
-        outputs = [divmod(o, CELL_TILES) for o in range(BATCH * CELL_TILES)]
-        out_at = {output_job(o): outputs[o] for o in range(len(outputs))}
-
-        for q in range(-2, JOBS + 4):
-            flips = out_at.get(q - 1)
-            shown = out_at.get(q - 2)
-            if 0 <= q + 2 < JOBS:
-                similarities(q + 2)
-            if flips:
-                flip_columns(*flips)
+        for q in range(-2, JOBS + 5):
+            s0, s1, s2 = flips_at.get(q), flips_at.get(q - 1), flips_at.get(q - 2)
             if q == -2:
                 regroup(2)
             if q == -1:
                 quantise_features(2)
-            if 0 <= q + 1 < JOBS:
-                minimum_wide(q + 1)
+            if 0 <= q + 2 < JOBS:
+                similarities(q + 2, False)
+            if s1:
+                store_conf1(*s1)
             if 0 <= q < JOBS:
                 exponentials(q)
-            if shown:
-                keep_mask(*shown)
-            for step, c in front.get(q, []):
-                front_step(step, c)
-            if 0 <= q + 1 < JOBS:
-                minimum_narrow(q + 1)
-            if shown:
-                best_of_two(*shown, False)
             if 0 <= q - 1 < JOBS:
                 scalars(q - 1)
-            if shown:
-                best_of_two(*shown, True)
-            if flips:
-                store_conf1(*flips)
+            if 0 <= q + 1 < JOBS:
+                minimum_wide(q + 1)
+            if s1:
+                best_of_two(*s1, False)
+                best_of_two(*s1, True)
+            if 0 <= q + 1 < JOBS:
+                minimum_narrow(q + 1)
+            if s1:
+                keep_mask(*s1)
             if 0 <= q - 1 < JOBS:
                 normalise(q - 1)
-            if shown:
-                store_mconf(*shown)
+            if s2:
+                store_mconf(*s2, s2[0] == 1 and s2[1] >= 4)
+            for step, c in front.get(q, []):
+                front_step(step, c)
+            if 0 <= q + 2 < JOBS:
+                similarities(q + 2, True)
+            if s0:
+                flip_conf1(*s0)
+                flip_miss(*s0)

@@ -27,11 +27,13 @@ CHUNKS = TOKENS // CHUNK
 JOBS_A_BATCH = 2 * CELL_TILES
 JOBS = BATCH * JOBS_A_BATCH
 BORDER = 2
+SCALAR_REGROUP = (5,)
 VECTOR_BIAS = ()
-SCALAR_CONF1 = (12, 14, 16)
-OUT_SLOT = (8, 9, 10, 11, 12, 13, 19, 20, 21, 22, 23, 24)
-REPEAT = (1, 1)
-GPSIMD_REGROUP = ()
+SCALAR_CONF1 = (0,1,2,3,4,5,12,13,14,15,16,17)
+OUT_SLOT = (8,9,11,13,15,17,19,20,21,22,23,24)
+REPEAT = (1,2)
+DIRECT = (3,4)
+COLUMN_LAG = 1
 INV_THRESHOLD = 5.0
 INV_TEMPERATURE = 10.0
 INV_SQRT_FEATURES = 1.0 / math.sqrt(FEATURES)
@@ -53,6 +55,7 @@ def tile_coarsematching_kernel(tc, feat_c0, feat_c1, W, b, h0c, w0c, h1c, w1c, o
         work = ctx.enter_context(tc.tile_pool(name="work", bufs=3))
         small = ctx.enter_context(tc.tile_pool(name="small", bufs=4))
         psum = ctx.enter_context(tc.psum_pool(name="psum", bufs=1))
+        ctx.enter_context(tc.manual_schedule())
 
         w_raw = keep.tile([P, PACK * FEATURES], BF16)
         w_raw_rows = w_raw[:].rearrange("p (t k) -> p t k", t=PACK)
@@ -82,9 +85,10 @@ def tile_coarsematching_kernel(tc, feat_c0, feat_c1, W, b, h0c, w0c, h1c, w1c, o
         identity = keep.tile([P, P], F32)
         make_identity(nc, identity[:])
         identity_bf = keep.tile([P, P], BF16)
+        zero = keep.tile([P, 1], F32)
+        nc.vector.memset(zero[:], 0.0)
         warm = keep.tile([P, 1], F32)
-        nc.vector.memset(warm[:], 0.0)
-        nc.scalar.activation(out=warm[:], in_=warm[:], func=ACT.Exp)
+        nc.scalar.activation(out=warm[:], in_=zero[:], func=ACT.Exp)
 
         edge = keep.tile([P, P], F32)
         nc.vector.memset(edge[:], INV_THRESHOLD)
@@ -92,7 +96,7 @@ def tile_coarsematching_kernel(tc, feat_c0, feat_c1, W, b, h0c, w0c, h1c, w1c, o
         nc.vector.memset(edge_rows[:, :, 0:BORDER], 0.0)
         nc.vector.memset(edge_rows[:, :, w0c - BORDER : w0c], 0.0)
         nc.vector.tensor_copy(out=identity_bf[:], in_=identity[:])
-        edge_t = psum.tile([P, BANK], F32, tag="aux", bufs=5)
+        edge_t = psum.tile([P, BANK], F32, tag="aux", bufs=4)
         nc.tensor.transpose(edge_t[:, 0:P], edge[:], identity[:])
         limit = keep.tile([P, CELL_TILES], F32)
         nc.vector.tensor_copy(out=limit[:], in_=edge_t[:, 0:CELL_TILES])
@@ -100,29 +104,33 @@ def tile_coarsematching_kernel(tc, feat_c0, feat_c1, W, b, h0c, w0c, h1c, w1c, o
         nc.vector.memset(limit[P - BORDER * w0c : P, CELL_TILES - 1 : CELL_TILES], 0.0)
 
         mconf_tiles = []
-        for slot in range(3):
+        for slot in range(4):
             mconf = keep.tile([P, CELLS], F32, name="mconf%d" % slot)
-            nc.vector.memset(mconf[:], 0.0)
+            nc.scalar.activation(out=mconf[:], in_=zero[:].to_broadcast([P, CELLS]), func=ACT.Copy)
             mconf_tiles.append(mconf)
-        miss_t = []
-        for n in range(BATCH):
-            miss = keep.tile([P, CELL_TILES, CELLS], BF16, name="miss_t%d" % n)
-            nc.vector.memset(miss[:, :, 0:FIRST], 1.0)
-            nc.vector.memset(miss[:, :, LAST:CELLS], 1.0)
-            seams = miss[:, :, FIRST - BORDER : LAST - BORDER + w0c].rearrange("p j (r w) -> p j r w", w=w0c)
-            nc.vector.memset(seams[:, :, :, 0 : 2 * BORDER], 1.0)
-            miss_t.append(miss)
+        miss_t = [keep.tile([P, CELL_TILES, CELLS], BF16, name="miss_t%d" % n) for n in range(BATCH)]
+
+        def clear_miss(n, fill):
+            fill(miss_t[n][:, :, 0:FIRST])
+            fill(miss_t[n][:, :, LAST:CELLS])
+            seams = miss_t[n][:, :, FIRST - BORDER : LAST - BORDER + w0c].rearrange("p j (r w) -> p j r w", w=w0c)
+            fill(seams[:, :, :, 0 : 2 * BORDER])
+
+        clear_miss(0, lambda cells: nc.vector.memset(cells, 1.0))
 
         b_scaled = keep.tile([P, PACK], F32)
 
         def aux_tile(shape, dtype, name):
-            return psum.tile(shape, dtype, tag="aux", bufs=5, name=name)
+            return psum.tile(shape, dtype, tag="aux", bufs=4, name=name)
 
-        def flip(raw, first_tile):
+        def flip(raw, first_tile, early):
             words = raw.bitcast(F32).rearrange("p (r u q) -> p r u q", u=2, q=P)
             banks = []
             for h in range(2):
-                flipped = aux_tile([P, 2, 2, P], F32, "flipped")
+                if early:
+                    flipped = psum.tile([P, 2, 2, P], F32, tag="wide", bufs=2, name="flipped")
+                else:
+                    flipped = aux_tile([P, 2, 2, P], F32, "flipped")
                 for r in range(2):
                     for u in range(2):
                         nc.tensor.transpose(
@@ -131,14 +139,14 @@ def tile_coarsematching_kernel(tc, feat_c0, feat_c1, W, b, h0c, w0c, h1c, w1c, o
                 banks.append(flipped)
             return banks
 
-        def gather(banks, vector_too):
+        def gather(banks, vector_banks):
             grouped = stage.tile([P, CHUNK * PACK], BF16, name="grouped", bufs=3, align_bytes=64)
             halves = grouped[:].bitcast(F32).rearrange("p (h r c u) -> p h r c u", h=2, r=2, u=2)
-            if vector_too:
-                nc.vector.tensor_copy(out=halves[:, 0], in_=banks[0][:].rearrange("p r u c -> p r c u"))
-            else:
-                nc.scalar.copy(out=halves[:, 0], in_=banks[0][:].rearrange("p r u c -> p r c u"))
-            nc.scalar.copy(out=halves[:, 1], in_=banks[1][:].rearrange("p r u c -> p r c u"))
+            for h in range(2):
+                if h < vector_banks:
+                    nc.vector.tensor_copy(out=halves[:, h], in_=banks[h][:].rearrange("p r u c -> p r c u"))
+                else:
+                    nc.scalar.copy(out=halves[:, h], in_=banks[h][:].rearrange("p r u c -> p r c u"))
             return grouped
 
         w_codes = keep.tile([P, FEATURES], U32, align_bytes=64)
@@ -155,11 +163,11 @@ def tile_coarsematching_kernel(tc, feat_c0, feat_c1, W, b, h0c, w0c, h1c, w1c, o
         def chunk_columns(c):
             return slice(c * CHUNK, (c + 1) * CHUNK)
 
-        def flip_tokens(c):
-            x_banks[c] = flip(x_raw[:], c * CHUNK_TILES)
+        def flip_tokens(c, early):
+            x_banks[c] = flip(x_raw[:], c * CHUNK_TILES, early)
 
-        def gather_tokens(c, vector_too):
-            x_grouped[c] = gather(x_banks[c], vector_too)
+        def gather_tokens(c, vector_banks):
+            x_grouped[c] = gather(x_banks[c], vector_banks)
 
         def quantise_tokens(c):
             cols = chunk_columns(c)
@@ -195,17 +203,11 @@ def tile_coarsematching_kernel(tc, feat_c0, feat_c1, W, b, h0c, w0c, h1c, w1c, o
 
         def regroup(c):
             f_grouped[c] = stage.tile([P, CHUNK, PACK], BF16, name="f_grouped", align_bytes=64)
-            if c in GPSIMD_REGROUP:
-                nc.gpsimd.tensor_scalar(
-                    out=f_grouped[c][:].rearrange("p (c i) t -> p c t i", i=4),
-                    in0=f_rows[c][:].rearrange("p t (c i) -> p c t i", i=4),
-                    scalar1=1.0, scalar2=0.0, op0=ALU.mult, op1=ALU.add,
-                )
-            else:
-                nc.vector.tensor_copy(
-                    out=f_grouped[c][:].rearrange("p (c i) t -> p c t i", i=4),
-                    in_=f_rows[c][:].rearrange("p t (c i) -> p c t i", i=4),
-                )
+            copy = nc.scalar.copy if c in SCALAR_REGROUP else nc.vector.tensor_copy
+            copy(
+                out=f_grouped[c][:].rearrange("p (c i) t -> p c t i", i=4),
+                in_=f_rows[c][:].rearrange("p t (c i) -> p c t i", i=4),
+            )
 
         def quantise_features(c):
             cols = chunk_columns(c)
@@ -214,6 +216,31 @@ def tile_coarsematching_kernel(tc, feat_c0, feat_c1, W, b, h0c, w0c, h1c, w1c, o
                 scales=f_scales[:, cols],
                 in_=f_grouped[c][:].rearrange("p c t -> p (c t)"),
             )
+
+        def project_direct(c, first, last):
+            if first == 0:
+                f_grouped[c] = stage.tile([P, CHUNK, PACK], BF16, name="f_grouped", align_bytes=64)
+            for r in range(first, last):
+                cols = slice(c * CHUNK + r * P, c * CHUNK + (r + 1) * P)
+                acc = aux_tile([P, PACK, P], F32, "acc")
+                for t in range(PACK):
+                    nc.tensor.matmul_mx(
+                        out=acc[:, t, :],
+                        lhsT=w_codes[:, t * P : (t + 1) * P].bitcast(FP8X4),
+                        lhsT_scale=w_scales[:, t * P : (t + 1) * P],
+                        rhs=x_codes[:, cols].bitcast(FP8X4),
+                        rhs_scale=x_scales[:, cols],
+                        start=True,
+                        stop=True,
+                    )
+                nc.vector.scalar_tensor_tensor(
+                    out=f_grouped[c][:, r * P : (r + 1) * P, :],
+                    in0=acc[:].rearrange("p t n -> p n t"),
+                    scalar=INV_SQRT_FEATURES,
+                    in1=b_scaled[:].unsqueeze(1).to_broadcast([P, P, PACK]),
+                    op0=ALU.mult,
+                    op1=ALU.add,
+                )
 
         soft_t = {}
         total = {}
@@ -250,9 +277,9 @@ def tile_coarsematching_kernel(tc, feat_c0, feat_c1, W, b, h0c, w0c, h1c, w1c, o
             at = (f0_at if is_row else f1_at) + i * P
             along = f1_at if is_row else f0_at
             if rest:
-                acc = psum.tile([P, BANK], F32, name="narrow", bufs=1)
+                acc = psum.tile([P, BANK], F32, name="narrow", tag="narrow", bufs=2)
             else:
-                acc = psum.tile([P, BANK], F32, name="wide", bufs=2)
+                acc = psum.tile([P, BANK], F32, name="wide", tag="wide", bufs=2)
             first, width = (along + BANK, REST) if rest else (along, BANK)
             for again in range(REPEAT[is_row] if not rest else 1):
               nc.tensor.matmul_mx(
@@ -295,10 +322,9 @@ def tile_coarsematching_kernel(tc, feat_c0, feat_c1, W, b, h0c, w0c, h1c, w1c, o
                 bias=low[q][:], scale=-1.0, accum_out=total[n][:, job : job + 1],
             )
 
-        def scalars(q):
+        def keys(q):
             n, job, is_row, i = job_parts(q)
             one = slice(job, job + 1)
-            nc.vector.reciprocal(out=recip[n][:, one], in_=total[n][:, one])
             if is_row:
                 nc.vector.tensor_scalar(
                     out=key[n][:, one], in0=total[n][:, one], scalar1=limit[:, i : i + 1], scalar2=1.0,
@@ -307,25 +333,29 @@ def tile_coarsematching_kernel(tc, feat_c0, feat_c1, W, b, h0c, w0c, h1c, w1c, o
             else:
                 nc.vector.tensor_scalar(
                     out=key[n][:, one], in0=total[n][:, one], scalar1=INV_THRESHOLD,
-                    scalar2=0.5, op0=ALU.is_ge, op1=ALU.max,
+                    scalar2=recip[n][:, one], op0=ALU.is_ge, op1=ALU.max,
                 )
+
+        def reciprocals(q):
+            n, job, is_row, i = job_parts(q)
+            one = slice(job, job + 1)
+            nc.vector.reciprocal(out=recip[n][:, one], in_=total[n][:, one])
 
         def normalise(q):
             n, job, is_row, i = job_parts(q)
             one = slice(job, job + 1)
             values = job_values(q)
             if is_row:
-                conf0 = work.tile([P, CELLS], F32, name="conf0")
-                nc.gpsimd.tensor_scalar(
-                    out=conf0[:], in0=values, scalar1=recip[n][:, one], scalar2=0.0,
-                    op0=ALU.mult, op1=ALU.add,
-                )
+                conf0 = work.tile([P, CELLS], F32, name="conf0", bufs=6)
+                if q in SCALAR_CONF1:
+                    nc.scalar.activation(out=conf0[:], in_=values, func=ACT.Copy, scale=recip[n][:, one])
+                else:
+                    nc.gpsimd.tensor_scalar(
+                        out=conf0[:], in0=values, scalar1=recip[n][:, one], scalar2=0.0,
+                        op0=ALU.mult, op1=ALU.add,
+                    )
                 nc.sync.dma_start(out=out[0, n, i * P : (i + 1) * P, :], in_=conf0[:])
             else:
-                nc.gpsimd.tensor_scalar(
-                    out=inner_rows(miss_t[n][:, i, :]), in0=inner_rows(values), scalar1=-0.5,
-                    scalar2=key[n][:, one], op0=ALU.mult, op1=ALU.add,
-                )
                 if q in SCALAR_CONF1:
                     nc.scalar.activation(out=values, in_=values, func=ACT.Copy, scale=recip[n][:, one])
                 else:
@@ -333,6 +363,10 @@ def tile_coarsematching_kernel(tc, feat_c0, feat_c1, W, b, h0c, w0c, h1c, w1c, o
                         out=values, in0=values, scalar1=recip[n][:, one], scalar2=0.0,
                         op0=ALU.mult, op1=ALU.add,
                     )
+                nc.gpsimd.tensor_scalar(
+                    out=inner_rows(miss_t[n][:, i, :]), in0=inner_rows(values), scalar1=-1.0,
+                    scalar2=key[n][:, one], op0=ALU.mult, op1=ALU.add,
+                )
 
         flipped_columns = {}
         flipped_miss = {}
@@ -356,7 +390,7 @@ def tile_coarsematching_kernel(tc, feat_c0, feat_c1, W, b, h0c, w0c, h1c, w1c, o
 
         def store_conf1(n, i):
             conf1_wide, conf1_narrow = flipped_columns[n, i]
-            conf1 = work.tile([P, CELLS], F32, name="conf1")
+            conf1 = work.tile([P, CELLS], F32, name="conf1", bufs=6)
             nc.scalar.copy(out=conf1[:, 0:BANK], in_=conf1_wide[:])
             nc.scalar.copy(out=conf1[:, BANK:CELLS], in_=conf1_narrow[:, 0:REST])
             nc.sync.dma_start(out=out[1, n, i * P : (i + 1) * P, :], in_=conf1[:])
@@ -392,25 +426,31 @@ def tile_coarsematching_kernel(tc, feat_c0, feat_c1, W, b, h0c, w0c, h1c, w1c, o
             engine.tensor_tensor(out=interior(mconf[:]), in0=mask[n, i][:], in1=best[n, i][:], op=ALU.mult)
             nc.sync.dma_start(out=out[2, n, i * P : (i + 1) * P, :], in_=mconf[:])
 
-        w_banks = flip(w_raw[:], 0)
-        w_grouped = gather(w_banks, True)
-        flip_tokens(0)
+        def projected(c, first, last):
+            (project_direct if c in DIRECT else project)(c, first, last)
+
+        w_banks = flip(w_raw[:], 0, True)
+        w_grouped = gather(w_banks, 1)
+        flip_tokens(0, False)
         nc.vector.quantize_mx(out=w_codes[:].bitcast(FP8X4), scales=w_scales[:], in_=w_grouped[:])
-        gather_tokens(0, True)
+        gather_tokens(0, 1)
         nc.vector.tensor_scalar_mul(out=b_scaled[:], in0=b_raw[:], scalar1=INV_SQRT_FEATURES)
+        flip_tokens(1, True)
         quantise_tokens(0)
-        flip_tokens(1)
-        gather_tokens(1, True)
-        project(0, 0, PACK)
+        gather_tokens(1, 0)
+        projected(0, 0, PACK)
         quantise_tokens(1)
-        flip_tokens(2)
-        regroup(0)
-        gather_tokens(2, True)
-        project(1, 0, PACK)
-        quantise_features(0)
+        clear_miss(1, lambda cells: nc.vector.memset(cells, 1.0))
+        flip_tokens(2, True)
+        gather_tokens(2, 2)
+        projected(1, 0, PACK)
         quantise_tokens(2)
-        regroup(1)
-        project(2, 0, PACK)
+        if 0 not in DIRECT:
+            regroup(0)
+        projected(2, 0, PACK)
+        quantise_features(0)
+        if 1 not in DIRECT:
+            regroup(1)
         quantise_features(1)
 
         front = {}
@@ -421,52 +461,56 @@ def tile_coarsematching_kernel(tc, feat_c0, feat_c1, W, b, h0c, w0c, h1c, w1c, o
 
         def front_step(step, c):
             if step == "flip":
-                flip_tokens(c)
-                gather_tokens(c, False)
+                flip_tokens(c, False)
+                gather_tokens(c, 0)
             elif step == "quantise x":
                 quantise_tokens(c)
             elif step == "first half":
-                project(c, 0, 2)
+                (project_direct if c in DIRECT else project)(c, 0, 2)
             elif step == "second half":
-                project(c, 2, PACK)
+                (project_direct if c in DIRECT else project)(c, 2, PACK)
             elif step == "regroup":
-                regroup(c)
+                if c not in DIRECT:
+                    regroup(c)
             else:
                 quantise_features(c)
 
         flips_at = dict((OUT_SLOT[o], divmod(o, CELL_TILES)) for o in range(BATCH * CELL_TILES))
 
         for q in range(-2, JOBS + 5):
-            s0, s1, s2 = flips_at.get(q), flips_at.get(q - 1), flips_at.get(q - 2)
+            s0, s1 = flips_at.get(q), flips_at.get(q - 1)
+            ready = [j for j in (q - 2, q - 1) if 0 <= j < JOBS and q - j == (1 if job_parts(j)[2] else COLUMN_LAG)]
             if q == -2:
-                regroup(2)
+                if 2 not in DIRECT:
+                    regroup(2)
             if q == -1:
                 quantise_features(2)
             if 0 <= q + 2 < JOBS:
                 similarities(q + 2, False)
+                similarities(q + 2, True)
+            for j in ready:
+                reciprocals(j)
+            if 0 <= q + 1 < JOBS:
+                minimum_wide(q + 1)
+            for j in ready:
+                keys(j)
+            if 0 <= q + 1 < JOBS:
+                minimum_narrow(q + 1)
             if s1:
                 store_conf1(*s1)
             if 0 <= q < JOBS:
                 exponentials(q)
-            if 0 <= q - 1 < JOBS:
-                scalars(q - 1)
-            if 0 <= q + 1 < JOBS:
-                minimum_wide(q + 1)
+            for step, c in front.get(q, []):
+                front_step(step, c)
+            if s0:
+                flip_conf1(*s0)
             if s1:
                 best_of_two(*s1, False)
                 best_of_two(*s1, True)
-            if 0 <= q + 1 < JOBS:
-                minimum_narrow(q + 1)
-            if s1:
                 keep_mask(*s1)
-            if 0 <= q - 1 < JOBS:
-                normalise(q - 1)
-            if s2:
-                store_mconf(*s2, s2[0] == 1 and s2[1] >= 4)
-            for step, c in front.get(q, []):
-                front_step(step, c)
-            if 0 <= q + 2 < JOBS:
-                similarities(q + 2, True)
             if s0:
-                flip_conf1(*s0)
                 flip_miss(*s0)
+            for j in ready:
+                normalise(j)
+            if s1:
+                store_mconf(*s1, s1 == (1, 5))

@@ -29,7 +29,7 @@ JOBS = BATCH * JOBS_A_BATCH
 BORDER = 2
 SCALAR_REGROUP = (5,)
 VECTOR_BIAS = ()
-SCALAR_CONF1 = (0,1,2,3,4,5,12,13,14,15,16,17)
+SCALAR_CONF1 = (0,1,2,3,4,5,12,13,14,15,16,17,19,21,23)
 OUT_SLOT = (8,9,11,13,15,17,19,20,21,22,23,24)
 REPEAT = (1,2)
 DIRECT = (3,4)
@@ -96,8 +96,17 @@ def tile_coarsematching_kernel(tc, feat_c0, feat_c1, W, b, h0c, w0c, h1c, w1c, o
         nc.vector.memset(edge_rows[:, :, 0:BORDER], 0.0)
         nc.vector.memset(edge_rows[:, :, w0c - BORDER : w0c], 0.0)
         nc.vector.tensor_copy(out=identity_bf[:], in_=identity[:])
+        calm = keep.tile([P, BANK], BF16)
+        nc.vector.memset(calm[:], 0.0)
+
+        def busy(count):
+            for k in range(count):
+                spare = psum.tile([P, BANK], F32, name="spare", tag="narrow", bufs=2)
+                nc.tensor.matmul(out=spare[:], lhsT=calm[:, 0:P], rhs=calm[:], start=True, stop=True)
+
         edge_t = psum.tile([P, BANK], F32, tag="aux", bufs=4)
         nc.tensor.transpose(edge_t[:, 0:P], edge[:], identity[:])
+        busy(4)
         limit = keep.tile([P, CELL_TILES], F32)
         nc.vector.tensor_copy(out=limit[:], in_=edge_t[:, 0:CELL_TILES])
         nc.vector.memset(limit[0 : BORDER * w0c, 0:1], 0.0)
@@ -373,9 +382,15 @@ def tile_coarsematching_kernel(tc, feat_c0, feat_c1, W, b, h0c, w0c, h1c, w1c, o
         best = {}
         mask = {}
 
-        def flip_conf1(n, i):
+        def flip_conf1(n, i, late):
             rows = slice(i * P, (i + 1) * P)
-            banks = (aux_tile([P, BANK], F32, "conf1_wide"), aux_tile([P, BANK], F32, "conf1_narrow"))
+            if late:
+                banks = (
+                    psum.tile([P, BANK], F32, name="conf1_wide", tag="wide", bufs=2),
+                    psum.tile([P, BANK], F32, name="conf1_narrow", tag="narrow", bufs=2),
+                )
+            else:
+                banks = (aux_tile([P, BANK], F32, "conf1_wide"), aux_tile([P, BANK], F32, "conf1_narrow"))
             for j in range(CELL_TILES):
                 at = (j * P) % BANK
                 nc.tensor.transpose(banks[j * P // BANK][:, at : at + P], soft_t[n][:, j, rows], identity[:])
@@ -391,8 +406,8 @@ def tile_coarsematching_kernel(tc, feat_c0, feat_c1, W, b, h0c, w0c, h1c, w1c, o
         def store_conf1(n, i):
             conf1_wide, conf1_narrow = flipped_columns[n, i]
             conf1 = work.tile([P, CELLS], F32, name="conf1", bufs=6)
-            nc.scalar.copy(out=conf1[:, 0:BANK], in_=conf1_wide[:])
             nc.scalar.copy(out=conf1[:, BANK:CELLS], in_=conf1_narrow[:, 0:REST])
+            nc.scalar.copy(out=conf1[:, 0:BANK], in_=conf1_wide[:])
             nc.sync.dma_start(out=out[1, n, i * P : (i + 1) * P, :], in_=conf1[:])
 
         def keep_mask(n, i):
@@ -406,7 +421,7 @@ def tile_coarsematching_kernel(tc, feat_c0, feat_c1, W, b, h0c, w0c, h1c, w1c, o
 
         def best_of_two(n, i, second):
             one = slice(CELL_TILES + i, CELL_TILES + i + 1)
-            if not second:
+            if (n, i) not in best:
                 best[n, i] = work.tile([P, rows_in, cols_in], F32, name="best")
             grid = flipped_columns[n, i][1 if second else 0][:].rearrange("p (r w) -> p r w", w=w1c)
             rows = slice(rows_wide, rows_in) if second else slice(0, rows_wide)
@@ -430,12 +445,15 @@ def tile_coarsematching_kernel(tc, feat_c0, feat_c1, W, b, h0c, w0c, h1c, w1c, o
             (project_direct if c in DIRECT else project)(c, first, last)
 
         w_banks = flip(w_raw[:], 0, True)
+        busy(1)
         w_grouped = gather(w_banks, 1)
         flip_tokens(0, False)
+        busy(1)
         nc.vector.quantize_mx(out=w_codes[:].bitcast(FP8X4), scales=w_scales[:], in_=w_grouped[:])
         gather_tokens(0, 1)
         nc.vector.tensor_scalar_mul(out=b_scaled[:], in0=b_raw[:], scalar1=INV_SQRT_FEATURES)
         flip_tokens(1, True)
+        busy(1)
         quantise_tokens(0)
         gather_tokens(1, 0)
         projected(0, 0, PACK)
@@ -503,7 +521,7 @@ def tile_coarsematching_kernel(tc, feat_c0, feat_c1, W, b, h0c, w0c, h1c, w1c, o
             for step, c in front.get(q, []):
                 front_step(step, c)
             if s0:
-                flip_conf1(*s0)
+                flip_conf1(*s0, q >= JOBS - 2)
             if s1:
                 best_of_two(*s1, False)
                 best_of_two(*s1, True)

@@ -31,7 +31,7 @@ SCALAR_REGROUP = (5,)
 VECTOR_BIAS = ()
 SCALAR_CONF1 = (0,1,2,3,4,5,12,13,14,15,16,17,19,21,23)
 OUT_SLOT = (8,9,11,13,15,17,19,20,21,22,23,24)
-REPEAT = (1,2)
+REPEAT = (1,1)
 DIRECT = (3,4)
 COLUMN_LAG = 1
 INV_THRESHOLD = 5.0
@@ -106,7 +106,6 @@ def tile_coarsematching_kernel(tc, feat_c0, feat_c1, W, b, h0c, w0c, h1c, w1c, o
 
         edge_t = psum.tile([P, BANK], F32, tag="aux", bufs=4)
         nc.tensor.transpose(edge_t[:, 0:P], edge[:], identity[:])
-        busy(4)
         limit = keep.tile([P, CELL_TILES], F32)
         nc.vector.tensor_copy(out=limit[:], in_=edge_t[:, 0:CELL_TILES])
         nc.vector.memset(limit[0 : BORDER * w0c, 0:1], 0.0)
@@ -445,15 +444,12 @@ def tile_coarsematching_kernel(tc, feat_c0, feat_c1, W, b, h0c, w0c, h1c, w1c, o
             (project_direct if c in DIRECT else project)(c, first, last)
 
         w_banks = flip(w_raw[:], 0, True)
-        busy(1)
         w_grouped = gather(w_banks, 1)
         flip_tokens(0, False)
-        busy(1)
         nc.vector.quantize_mx(out=w_codes[:].bitcast(FP8X4), scales=w_scales[:], in_=w_grouped[:])
         gather_tokens(0, 1)
         nc.vector.tensor_scalar_mul(out=b_scaled[:], in0=b_raw[:], scalar1=INV_SQRT_FEATURES)
         flip_tokens(1, True)
-        busy(1)
         quantise_tokens(0)
         gather_tokens(1, 0)
         projected(0, 0, PACK)

@@ -28,12 +28,9 @@ JOBS_A_BATCH = 2 * CELL_TILES
 JOBS = BATCH * JOBS_A_BATCH
 BORDER = 2
 SCALAR_REGROUP = (5,)
-VECTOR_BIAS = ()
 SCALAR_CONF1 = (0,1,2,3,4,5,12,13,14,15,16,17,19,21,23)
 OUT_SLOT = (8,9,11,13,15,17,19,20,21,22,23,24)
-REPEAT = (1,1)
 DIRECT = (3,4)
-COLUMN_LAG = 1
 INV_THRESHOLD = 5.0
 INV_TEMPERATURE = 10.0
 INV_SQRT_FEATURES = 1.0 / math.sqrt(FEATURES)
@@ -96,14 +93,6 @@ def tile_coarsematching_kernel(tc, feat_c0, feat_c1, W, b, h0c, w0c, h1c, w1c, o
         nc.vector.memset(edge_rows[:, :, 0:BORDER], 0.0)
         nc.vector.memset(edge_rows[:, :, w0c - BORDER : w0c], 0.0)
         nc.vector.tensor_copy(out=identity_bf[:], in_=identity[:])
-        calm = keep.tile([P, BANK], BF16)
-        nc.vector.memset(calm[:], 0.0)
-
-        def busy(count):
-            for k in range(count):
-                spare = psum.tile([P, BANK], F32, name="spare", tag="narrow", bufs=2)
-                nc.tensor.matmul(out=spare[:], lhsT=calm[:, 0:P], rhs=calm[:], start=True, stop=True)
-
         edge_t = psum.tile([P, BANK], F32, tag="aux", bufs=4)
         nc.tensor.transpose(edge_t[:, 0:P], edge[:], identity[:])
         limit = keep.tile([P, CELL_TILES], F32)
@@ -124,7 +113,8 @@ def tile_coarsematching_kernel(tc, feat_c0, feat_c1, W, b, h0c, w0c, h1c, w1c, o
             seams = miss_t[n][:, :, FIRST - BORDER : LAST - BORDER + w0c].rearrange("p j (r w) -> p j r w", w=w0c)
             fill(seams[:, :, :, 0 : 2 * BORDER])
 
-        clear_miss(0, lambda cells: nc.vector.memset(cells, 1.0))
+        for n in range(BATCH):
+            clear_miss(n, lambda cells: nc.vector.memset(cells, 1.0))
 
         b_scaled = keep.tile([P, PACK], F32)
 
@@ -198,16 +188,10 @@ def tile_coarsematching_kernel(tc, feat_c0, feat_c1, W, b, h0c, w0c, h1c, w1c, o
                     start=True,
                     stop=True,
                 )
-                if (c, t) in VECTOR_BIAS:
-                    nc.vector.tensor_scalar(
-                        out=f_rows[c][:, t, :], in0=acc[:], scalar1=INV_SQRT_FEATURES,
-                        scalar2=b_scaled[:, t : t + 1], op0=ALU.mult, op1=ALU.add,
-                    )
-                else:
-                    nc.scalar.activation(
-                        out=f_rows[c][:, t, :], in_=acc[:], func=ACT.Identity,
-                        bias=b_scaled[:, t : t + 1], scale=INV_SQRT_FEATURES,
-                    )
+                nc.scalar.activation(
+                    out=f_rows[c][:, t, :], in_=acc[:], func=ACT.Identity,
+                    bias=b_scaled[:, t : t + 1], scale=INV_SQRT_FEATURES,
+                )
 
         def regroup(c):
             f_grouped[c] = stage.tile([P, CHUNK, PACK], BF16, name="f_grouped", align_bytes=64)
@@ -289,8 +273,7 @@ def tile_coarsematching_kernel(tc, feat_c0, feat_c1, W, b, h0c, w0c, h1c, w1c, o
             else:
                 acc = psum.tile([P, BANK], F32, name="wide", tag="wide", bufs=2)
             first, width = (along + BANK, REST) if rest else (along, BANK)
-            for again in range(REPEAT[is_row] if not rest else 1):
-              nc.tensor.matmul_mx(
+            nc.tensor.matmul_mx(
                 out=acc[:, 0:width],
                 lhsT=f_codes[:, at : at + P].bitcast(FP8X4),
                 lhsT_scale=f_scales[:, at : at + P],
@@ -298,7 +281,7 @@ def tile_coarsematching_kernel(tc, feat_c0, feat_c1, W, b, h0c, w0c, h1c, w1c, o
                 rhs_scale=f_scales[:, first : first + width],
                 start=True,
                 stop=True,
-              )
+            )
             sim_banks[q, rest] = acc
 
         def minimum_wide(q):
@@ -434,11 +417,13 @@ def tile_coarsematching_kernel(tc, feat_c0, feat_c1, W, b, h0c, w0c, h1c, w1c, o
                 op1=ALU.max,
             )
 
-        def store_mconf(n, i, on_vector):
+        def product(n, i, on_vector):
             mconf = mconf_tiles[i % len(mconf_tiles)]
             engine = nc.vector if on_vector else nc.gpsimd
             engine.tensor_tensor(out=interior(mconf[:]), in0=mask[n, i][:], in1=best[n, i][:], op=ALU.mult)
-            nc.sync.dma_start(out=out[2, n, i * P : (i + 1) * P, :], in_=mconf[:])
+
+        def send_mconf(n, i):
+            nc.sync.dma_start(out=out[2, n, i * P : (i + 1) * P, :], in_=mconf_tiles[i % len(mconf_tiles)][:])
 
         def projected(c, first, last):
             (project_direct if c in DIRECT else project)(c, first, last)
@@ -454,7 +439,6 @@ def tile_coarsematching_kernel(tc, feat_c0, feat_c1, W, b, h0c, w0c, h1c, w1c, o
         gather_tokens(1, 0)
         projected(0, 0, PACK)
         quantise_tokens(1)
-        clear_miss(1, lambda cells: nc.vector.memset(cells, 1.0))
         flip_tokens(2, True)
         gather_tokens(2, 2)
         projected(1, 0, PACK)
@@ -492,28 +476,29 @@ def tile_coarsematching_kernel(tc, feat_c0, feat_c1, W, b, h0c, w0c, h1c, w1c, o
         flips_at = dict((OUT_SLOT[o], divmod(o, CELL_TILES)) for o in range(BATCH * CELL_TILES))
 
         for q in range(-2, JOBS + 5):
-            s0, s1 = flips_at.get(q), flips_at.get(q - 1)
-            ready = [j for j in (q - 2, q - 1) if 0 <= j < JOBS and q - j == (1 if job_parts(j)[2] else COLUMN_LAG)]
-            if q == -2:
-                if 2 not in DIRECT:
-                    regroup(2)
-            if q == -1:
-                quantise_features(2)
+            s0, s1, s2 = flips_at.get(q), flips_at.get(q - 1), flips_at.get(q - 2)
+            done = q - 1 if 0 <= q - 1 < JOBS else None
             if 0 <= q + 2 < JOBS:
                 similarities(q + 2, False)
                 similarities(q + 2, True)
-            for j in ready:
-                reciprocals(j)
+            if done is not None:
+                reciprocals(done)
             if 0 <= q + 1 < JOBS:
                 minimum_wide(q + 1)
-            for j in ready:
-                keys(j)
+            if done is not None:
+                keys(done)
+            if s1 and s1[0] == 0:
+                keep_mask(*s1)
             if 0 <= q + 1 < JOBS:
                 minimum_narrow(q + 1)
             if s1:
                 store_conf1(*s1)
+            if s2:
+                send_mconf(*s2)
             if 0 <= q < JOBS:
                 exponentials(q)
+            if done is not None:
+                normalise(done)
             for step, c in front.get(q, []):
                 front_step(step, c)
             if s0:
@@ -521,10 +506,13 @@ def tile_coarsematching_kernel(tc, feat_c0, feat_c1, W, b, h0c, w0c, h1c, w1c, o
             if s1:
                 best_of_two(*s1, False)
                 best_of_two(*s1, True)
-                keep_mask(*s1)
+                if s1[0] == 1:
+                    keep_mask(*s1)
             if s0:
                 flip_miss(*s0)
-            for j in ready:
-                normalise(j)
             if s1:
-                store_mconf(*s1, s1 == (1, 5))
+                product(*s1, s1 == (1, 5))
+            if q == -2 and 2 not in DIRECT:
+                regroup(2)
+            if q == -1:
+                quantise_features(2)

@@ -27,10 +27,7 @@ CHUNKS = TOKENS // CHUNK
 JOBS_A_BATCH = 2 * CELL_TILES
 JOBS = BATCH * JOBS_A_BATCH
 BORDER = 2
-SCALAR_REGROUP = (5,)
-SCALAR_CONF1 = (0,1,2,3,4,5,12,13,14,15,16,17,19,21,23)
-OUT_SLOT = (8,9,11,13,15,17,19,20,21,22,23,24)
-DIRECT = (3,4)
+EARLY_CHUNKS = CHUNKS // BATCH
 INV_THRESHOLD = 5.0
 INV_TEMPERATURE = 10.0
 INV_SQRT_FEATURES = 1.0 / math.sqrt(FEATURES)
@@ -42,9 +39,8 @@ def tile_coarsematching_kernel(tc, feat_c0, feat_c1, W, b, h0c, w0c, h1c, w1c, o
     nc = tc.nc
     assert h0c * w0c == CELLS and h1c * w1c == CELLS
     assert h0c == h1c and w0c == w1c and P % w0c == 0
-    assert BORDER * w0c <= P // 2 and BORDER * w0c % 32 == 0
-
     FIRST, LAST = BORDER * w0c, CELLS - BORDER * w0c
+    assert FIRST <= P // 2 and FIRST % 32 == 0
 
     with ExitStack() as ctx:
         keep = ctx.enter_context(tc.tile_pool(name="keep", bufs=1))
@@ -53,6 +49,15 @@ def tile_coarsematching_kernel(tc, feat_c0, feat_c1, W, b, h0c, w0c, h1c, w1c, o
         small = ctx.enter_context(tc.tile_pool(name="small", bufs=4))
         psum = ctx.enter_context(tc.psum_pool(name="psum", bufs=1))
         ctx.enter_context(tc.manual_schedule())
+
+        def wide_tile(shape, name):
+            return psum.tile(shape, F32, tag="wide", bufs=2, name=name)
+
+        def narrow_tile(name):
+            return psum.tile([P, BANK], F32, tag="narrow", bufs=2, name=name)
+
+        def aux_tile(shape, dtype, name):
+            return psum.tile(shape, dtype, tag="aux", bufs=4, name=name)
 
         w_raw = keep.tile([P, PACK * FEATURES], BF16)
         w_raw_rows = w_raw[:].rearrange("p (t k) -> p t k", t=PACK)
@@ -93,42 +98,46 @@ def tile_coarsematching_kernel(tc, feat_c0, feat_c1, W, b, h0c, w0c, h1c, w1c, o
         nc.vector.memset(edge_rows[:, :, 0:BORDER], 0.0)
         nc.vector.memset(edge_rows[:, :, w0c - BORDER : w0c], 0.0)
         nc.vector.tensor_copy(out=identity_bf[:], in_=identity[:])
-        edge_t = psum.tile([P, BANK], F32, tag="aux", bufs=4)
+
+        zero_columns = keep.tile([P, BANK], BF16)
+        nc.vector.memset(zero_columns[:], 0.0)
+
+        def hold_clock(count):
+            for k in range(count):
+                unused = narrow_tile("unused")
+                nc.tensor.matmul(
+                    out=unused[:], lhsT=zero_columns[:, 0:P], rhs=zero_columns[:], start=True, stop=True
+                )
+
+        edge_t = aux_tile([P, BANK], F32, "edge_t")
         nc.tensor.transpose(edge_t[:, 0:P], edge[:], identity[:])
+        hold_clock(3)
         limit = keep.tile([P, CELL_TILES], F32)
         nc.vector.tensor_copy(out=limit[:], in_=edge_t[:, 0:CELL_TILES])
-        nc.vector.memset(limit[0 : BORDER * w0c, 0:1], 0.0)
-        nc.vector.memset(limit[P - BORDER * w0c : P, CELL_TILES - 1 : CELL_TILES], 0.0)
+        nc.vector.memset(limit[0:FIRST, 0:1], 0.0)
+        nc.vector.memset(limit[P - FIRST : P, CELL_TILES - 1 : CELL_TILES], 0.0)
 
         mconf_tiles = []
         for slot in range(4):
             mconf = keep.tile([P, CELLS], F32, name="mconf%d" % slot)
             nc.scalar.activation(out=mconf[:], in_=zero[:].to_broadcast([P, CELLS]), func=ACT.Copy)
             mconf_tiles.append(mconf)
-        miss_t = [keep.tile([P, CELL_TILES, CELLS], BF16, name="miss_t%d" % n) for n in range(BATCH)]
-
-        def clear_miss(n, fill):
-            fill(miss_t[n][:, :, 0:FIRST])
-            fill(miss_t[n][:, :, LAST:CELLS])
-            seams = miss_t[n][:, :, FIRST - BORDER : LAST - BORDER + w0c].rearrange("p j (r w) -> p j r w", w=w0c)
-            fill(seams[:, :, :, 0 : 2 * BORDER])
-
+        miss_t = []
         for n in range(BATCH):
-            clear_miss(n, lambda cells: nc.vector.memset(cells, 1.0))
+            miss = keep.tile([P, CELL_TILES, CELLS], BF16, name="miss_t%d" % n)
+            nc.vector.memset(miss[:, :, 0:FIRST], 1.0)
+            nc.vector.memset(miss[:, :, LAST:CELLS], 1.0)
+            seams = miss[:, :, FIRST - BORDER : LAST - BORDER + w0c].rearrange("p j (r w) -> p j r w", w=w0c)
+            nc.vector.memset(seams[:, :, :, 0 : 2 * BORDER], 1.0)
+            miss_t.append(miss)
 
         b_scaled = keep.tile([P, PACK], F32)
-
-        def aux_tile(shape, dtype, name):
-            return psum.tile(shape, dtype, tag="aux", bufs=4, name=name)
 
         def flip(raw, first_tile, early):
             words = raw.bitcast(F32).rearrange("p (r u q) -> p r u q", u=2, q=P)
             banks = []
             for h in range(2):
-                if early:
-                    flipped = psum.tile([P, 2, 2, P], F32, tag="wide", bufs=2, name="flipped")
-                else:
-                    flipped = aux_tile([P, 2, 2, P], F32, "flipped")
+                flipped = wide_tile([P, 2, 2, P], "flipped") if early else aux_tile([P, 2, 2, P], F32, "flipped")
                 for r in range(2):
                     for u in range(2):
                         nc.tensor.transpose(
@@ -195,11 +204,12 @@ def tile_coarsematching_kernel(tc, feat_c0, feat_c1, W, b, h0c, w0c, h1c, w1c, o
 
         def regroup(c):
             f_grouped[c] = stage.tile([P, CHUNK, PACK], BF16, name="f_grouped", align_bytes=64)
-            copy = nc.scalar.copy if c in SCALAR_REGROUP else nc.vector.tensor_copy
-            copy(
-                out=f_grouped[c][:].rearrange("p (c i) t -> p c t i", i=4),
-                in_=f_rows[c][:].rearrange("p t (c i) -> p c t i", i=4),
-            )
+            grouped = f_grouped[c][:].rearrange("p (c i) t -> p c t i", i=4)
+            rows = f_rows[c][:].rearrange("p t (c i) -> p c t i", i=4)
+            if c == CHUNKS - 1:
+                nc.scalar.copy(out=grouped, in_=rows)
+            else:
+                nc.vector.tensor_copy(out=grouped, in_=rows)
 
         def quantise_features(c):
             cols = chunk_columns(c)
@@ -268,10 +278,7 @@ def tile_coarsematching_kernel(tc, feat_c0, feat_c1, W, b, h0c, w0c, h1c, w1c, o
             f1_at = f0_at + CELLS
             at = (f0_at if is_row else f1_at) + i * P
             along = f1_at if is_row else f0_at
-            if rest:
-                acc = psum.tile([P, BANK], F32, name="narrow", tag="narrow", bufs=2)
-            else:
-                acc = psum.tile([P, BANK], F32, name="wide", tag="wide", bufs=2)
+            acc = narrow_tile("narrow") if rest else wide_tile([P, BANK], "wide")
             first, width = (along + BANK, REST) if rest else (along, BANK)
             nc.tensor.matmul_mx(
                 out=acc[:, 0:width],
@@ -338,7 +345,7 @@ def tile_coarsematching_kernel(tc, feat_c0, feat_c1, W, b, h0c, w0c, h1c, w1c, o
             values = job_values(q)
             if is_row:
                 conf0 = work.tile([P, CELLS], F32, name="conf0", bufs=6)
-                if q in SCALAR_CONF1:
+                if n == BATCH - 1 and i % 2 == 0:
                     nc.scalar.activation(out=conf0[:], in_=values, func=ACT.Copy, scale=recip[n][:, one])
                 else:
                     nc.gpsimd.tensor_scalar(
@@ -347,13 +354,7 @@ def tile_coarsematching_kernel(tc, feat_c0, feat_c1, W, b, h0c, w0c, h1c, w1c, o
                     )
                 nc.sync.dma_start(out=out[0, n, i * P : (i + 1) * P, :], in_=conf0[:])
             else:
-                if q in SCALAR_CONF1:
-                    nc.scalar.activation(out=values, in_=values, func=ACT.Copy, scale=recip[n][:, one])
-                else:
-                    nc.gpsimd.tensor_scalar(
-                        out=values, in0=values, scalar1=recip[n][:, one], scalar2=0.0,
-                        op0=ALU.mult, op1=ALU.add,
-                    )
+                nc.scalar.activation(out=values, in_=values, func=ACT.Copy, scale=recip[n][:, one])
                 nc.gpsimd.tensor_scalar(
                     out=inner_rows(miss_t[n][:, i, :]), in0=inner_rows(values), scalar1=-1.0,
                     scalar2=key[n][:, one], op0=ALU.mult, op1=ALU.add,
@@ -367,10 +368,7 @@ def tile_coarsematching_kernel(tc, feat_c0, feat_c1, W, b, h0c, w0c, h1c, w1c, o
         def flip_conf1(n, i, late):
             rows = slice(i * P, (i + 1) * P)
             if late:
-                banks = (
-                    psum.tile([P, BANK], F32, name="conf1_wide", tag="wide", bufs=2),
-                    psum.tile([P, BANK], F32, name="conf1_narrow", tag="narrow", bufs=2),
-                )
+                banks = (wide_tile([P, BANK], "conf1_wide"), narrow_tile("conf1_narrow"))
             else:
                 banks = (aux_tile([P, BANK], F32, "conf1_wide"), aux_tile([P, BANK], F32, "conf1_narrow"))
             for j in range(CELL_TILES):
@@ -417,102 +415,112 @@ def tile_coarsematching_kernel(tc, feat_c0, feat_c1, W, b, h0c, w0c, h1c, w1c, o
                 op1=ALU.max,
             )
 
-        def product(n, i, on_vector):
+        def multiply_mconf(n, i):
+            on_vector = (n, i) == (BATCH - 1, CELL_TILES - 1)
             mconf = mconf_tiles[i % len(mconf_tiles)]
             engine = nc.vector if on_vector else nc.gpsimd
             engine.tensor_tensor(out=interior(mconf[:]), in0=mask[n, i][:], in1=best[n, i][:], op=ALU.mult)
 
-        def send_mconf(n, i):
+        def store_mconf(n, i):
             nc.sync.dma_start(out=out[2, n, i * P : (i + 1) * P, :], in_=mconf_tiles[i % len(mconf_tiles)][:])
 
-        def projected(c, first, last):
-            (project_direct if c in DIRECT else project)(c, first, last)
-
         w_banks = flip(w_raw[:], 0, True)
+        hold_clock(2)
         w_grouped = gather(w_banks, 1)
         flip_tokens(0, False)
+        hold_clock(2)
         nc.vector.quantize_mx(out=w_codes[:].bitcast(FP8X4), scales=w_scales[:], in_=w_grouped[:])
         gather_tokens(0, 1)
         nc.vector.tensor_scalar_mul(out=b_scaled[:], in0=b_raw[:], scalar1=INV_SQRT_FEATURES)
         flip_tokens(1, True)
+        hold_clock(2)
         quantise_tokens(0)
         gather_tokens(1, 0)
-        projected(0, 0, PACK)
+        project(0, 0, PACK)
         quantise_tokens(1)
         flip_tokens(2, True)
         gather_tokens(2, 2)
-        projected(1, 0, PACK)
+        project(1, 0, PACK)
         quantise_tokens(2)
-        if 0 not in DIRECT:
-            regroup(0)
-        projected(2, 0, PACK)
+        regroup(0)
+        project(2, 0, PACK)
         quantise_features(0)
-        if 1 not in DIRECT:
-            regroup(1)
+        regroup(1)
         quantise_features(1)
 
         front = {}
-        for c in range(3, CHUNKS):
-            at = 3 * (c - 3) - 1
+        for c in range(EARLY_CHUNKS, CHUNKS):
+            start = 3 * (c - EARLY_CHUNKS) - 1
             for k, step in enumerate(("flip", "quantise x", "first half", "second half", "regroup", "quantise f")):
-                front[at + k] = front.get(at + k, []) + [(step, c)]
+                front[start + k] = front.get(start + k, []) + [(step, c)]
 
         def front_step(step, c):
+            direct = c < CHUNKS - 1
             if step == "flip":
                 flip_tokens(c, False)
                 gather_tokens(c, 0)
             elif step == "quantise x":
                 quantise_tokens(c)
-            elif step == "first half":
-                (project_direct if c in DIRECT else project)(c, 0, 2)
-            elif step == "second half":
-                (project_direct if c in DIRECT else project)(c, 2, PACK)
+            elif step in ("first half", "second half"):
+                first = 0 if step == "first half" else 2
+                if direct:
+                    project_direct(c, first, first + 2)
+                else:
+                    project(c, first, first + 2)
             elif step == "regroup":
-                if c not in DIRECT:
+                if not direct:
                     regroup(c)
             else:
                 quantise_features(c)
 
-        flips_at = dict((OUT_SLOT[o], divmod(o, CELL_TILES)) for o in range(BATCH * CELL_TILES))
+        def flip_round(n, i):
+            complete = n * JOBS_A_BATCH + CELL_TILES + 1
+            return complete + max(1, 2 * i) if n == 0 else complete + i
 
-        for q in range(-2, JOBS + 5):
-            s0, s1, s2 = flips_at.get(q), flips_at.get(q - 1), flips_at.get(q - 2)
-            done = q - 1 if 0 <= q - 1 < JOBS else None
+        flips_at = {}
+        for n in range(BATCH):
+            for i in range(CELL_TILES):
+                flips_at[flip_round(n, i)] = (n, i)
+
+        for q in range(-2, JOBS + 3):
+            flips, shown, stored = flips_at.get(q), flips_at.get(q - 1), flips_at.get(q - 2)
             if 0 <= q + 2 < JOBS:
                 similarities(q + 2, False)
                 similarities(q + 2, True)
-            if done is not None:
-                reciprocals(done)
+            if 0 <= q - 1 < JOBS:
+                reciprocals(q - 1)
             if 0 <= q + 1 < JOBS:
                 minimum_wide(q + 1)
-            if done is not None:
-                keys(done)
-            if s1 and s1[0] == 0:
-                keep_mask(*s1)
+            if 0 <= q - 1 < JOBS:
+                keys(q - 1)
+            if shown and shown[0] == 0:
+                keep_mask(*shown)
             if 0 <= q + 1 < JOBS:
                 minimum_narrow(q + 1)
-            if s1:
-                store_conf1(*s1)
-            if s2:
-                send_mconf(*s2)
+            if shown:
+                store_conf1(*shown)
+                if stored:
+                    store_mconf(*stored)
             if 0 <= q < JOBS:
                 exponentials(q)
-            if done is not None:
-                normalise(done)
+            if 0 <= q - 1 < JOBS:
+                normalise(q - 1)
+            if stored and not shown:
+                store_mconf(*stored)
             for step, c in front.get(q, []):
                 front_step(step, c)
-            if s0:
-                flip_conf1(*s0, q >= JOBS - 2)
-            if s1:
-                best_of_two(*s1, False)
-                best_of_two(*s1, True)
-                if s1[0] == 1:
-                    keep_mask(*s1)
-            if s0:
-                flip_miss(*s0)
-            if s1:
-                product(*s1, s1 == (1, 5))
-            if q == -2 and 2 not in DIRECT:
-                regroup(2)
+            if flips:
+                flip_conf1(*flips, q >= JOBS - 2)
+            if shown:
+                best_of_two(*shown, False)
+                best_of_two(*shown, True)
+                if shown[0] == 1:
+                    keep_mask(*shown)
+            if flips:
+                flip_miss(*flips)
+            if shown:
+                multiply_mconf(*shown)
+            if q == -2:
+                regroup(EARLY_CHUNKS - 1)
             if q == -1:
-                quantise_features(2)
+                quantise_features(EARLY_CHUNKS - 1)

@@ -21,6 +21,10 @@ FEATURES = 512
 CELL_TILES = CELLS // P
 REST = CELLS - BANK
 TOKENS = 2 * BATCH * CELLS
+BORDER_CELLS = 64
+INNER = CELLS - 2 * BORDER_CELLS
+INNER_TILES = INNER // P
+SPAN = 2 * CELLS + BORDER_CELLS
 CHUNK = BANK
 CHUNK_TILES = CHUNK // P
 CHUNKS = TOKENS // CHUNK
@@ -39,8 +43,7 @@ def tile_coarsematching_kernel(tc, feat_c0, feat_c1, W, b, h0c, w0c, h1c, w1c, o
     nc = tc.nc
     assert h0c * w0c == CELLS and h1c * w1c == CELLS
     assert h0c == h1c and w0c == w1c and P % w0c == 0
-    FIRST, LAST = BORDER * w0c, CELLS - BORDER * w0c
-    assert FIRST <= P // 2 and FIRST % 32 == 0
+    assert BORDER_CELLS == BORDER * w0c and INNER % P == 0
 
     with ExitStack() as ctx:
         keep = ctx.enter_context(tc.tile_pool(name="keep", bufs=1))
@@ -71,10 +74,13 @@ def tile_coarsematching_kernel(tc, feat_c0, feat_c1, W, b, h0c, w0c, h1c, w1c, o
         def load_tokens(n, g, first, count):
             feat = (feat_c0, feat_c1)[g]
             at = (2 * n + g) * CELL_TILES + first
-            nc.sync.dma_start(
-                out=x_raw_tiles[:, at : at + count, :],
-                in_=feat[n].rearrange("(j p) k -> p j k", p=P)[:, first : first + count, :],
-            )
+            inner = min(count, INNER_TILES - first)
+            rows = feat[n, BORDER_CELLS + first * P : BORDER_CELLS + (first + inner) * P, :]
+            nc.sync.dma_start(out=x_raw_tiles[:, at : at + inner, :], in_=rows.rearrange("(j p) k -> p j k", p=P))
+            if inner < count:
+                half = P // 2
+                nc.sync.dma_start(out=x_raw_tiles[0:half, at + inner, :], in_=feat[n, CELLS - half : CELLS, :])
+                nc.sync.dma_start(out=x_raw_tiles[half:P, at + inner, :], in_=feat[n, 0:half, :])
 
         load_tokens(0, 0, 0, 4)
         nc.sync.dma_start(out=b_raw[:], in_=b.rearrange("(p t) -> p t", t=PACK))
@@ -112,23 +118,24 @@ def tile_coarsematching_kernel(tc, feat_c0, feat_c1, W, b, h0c, w0c, h1c, w1c, o
         edge_t = aux_tile([P, BANK], F32, "edge_t")
         nc.tensor.transpose(edge_t[:, 0:P], edge[:], identity[:])
         hold_clock(3)
-        limit = keep.tile([P, CELL_TILES], F32)
-        nc.vector.tensor_copy(out=limit[:], in_=edge_t[:, 0:CELL_TILES])
-        nc.vector.memset(limit[0:FIRST, 0:1], 0.0)
-        nc.vector.memset(limit[P - FIRST : P, CELL_TILES - 1 : CELL_TILES], 0.0)
+        limit = keep.tile([P, 1], F32)
+        nc.vector.tensor_copy(out=limit[:], in_=edge_t[:, 0:1])
 
         mconf_tiles = []
         for slot in range(4):
             mconf = keep.tile([P, CELLS], F32, name="mconf%d" % slot)
             nc.scalar.activation(out=mconf[:], in_=zero[:].to_broadcast([P, CELLS]), func=ACT.Copy)
             mconf_tiles.append(mconf)
+        for n in range(BATCH):
+            half = P // 2
+            for rows in (slice(0, half), slice(CELLS - half, CELLS)):
+                nc.sync.dma_start(out=out[2, n, rows, :], in_=mconf_tiles[n][0:half, :])
         miss_t = []
         for n in range(BATCH):
-            miss = keep.tile([P, CELL_TILES, CELLS], BF16, name="miss_t%d" % n)
-            nc.vector.memset(miss[:, :, 0:FIRST], 1.0)
-            nc.vector.memset(miss[:, :, LAST:CELLS], 1.0)
-            seams = miss[:, :, FIRST - BORDER : LAST - BORDER + w0c].rearrange("p j (r w) -> p j r w", w=w0c)
-            nc.vector.memset(seams[:, :, :, 0 : 2 * BORDER], 1.0)
+            miss = keep.tile([P, INNER_TILES, INNER], BF16, name="miss_t%d" % n)
+            grid_rows = miss[:].rearrange("p j (r w) -> p (j r) w", w=w0c)
+            nc.vector.memset(grid_rows[:, :, 0:BORDER], 1.0)
+            nc.vector.memset(grid_rows[:, :, w0c - BORDER : w0c], 1.0)
             miss_t.append(miss)
 
         b_scaled = keep.tile([P, PACK], F32)
@@ -160,8 +167,8 @@ def tile_coarsematching_kernel(tc, feat_c0, feat_c1, W, b, h0c, w0c, h1c, w1c, o
         w_scales = keep.tile([P, FEATURES], U8, align_bytes=64)
         x_codes = keep.tile([P, TOKENS], U32, align_bytes=64)
         x_scales = keep.tile([P, TOKENS], U8, align_bytes=64)
-        f_codes = keep.tile([P, TOKENS], U32, align_bytes=64)
-        f_scales = keep.tile([P, TOKENS], U8, align_bytes=64)
+        f_codes = keep.tile([P, BATCH * SPAN], U32, align_bytes=64)
+        f_scales = keep.tile([P, BATCH * SPAN], U8, align_bytes=64)
         x_banks = {}
         x_grouped = {}
         f_rows = {}
@@ -212,12 +219,23 @@ def tile_coarsematching_kernel(tc, feat_c0, feat_c1, W, b, h0c, w0c, h1c, w1c, o
                 nc.vector.tensor_copy(out=grouped, in_=rows)
 
         def quantise_features(c):
-            cols = chunk_columns(c)
-            nc.vector.quantize_mx(
-                out=f_codes[:, cols].bitcast(FP8X4),
-                scales=f_scales[:, cols],
-                in_=f_grouped[c][:].rearrange("p c t -> p (c t)"),
-            )
+            n, part = divmod(c, EARLY_CHUNKS)
+            first, end = part * CHUNK, (part + 1) * CHUNK
+            cuts = [first] + [CELLS] * (first < CELLS < end) + [end]
+            for lo, hi in zip(cuts[:-1], cuts[1:]):
+                at = n * SPAN + lo + (BORDER_CELLS if lo >= CELLS else 0)
+                cols = slice(at, at + hi - lo)
+                nc.vector.quantize_mx(
+                    out=f_codes[:, cols].bitcast(FP8X4),
+                    scales=f_scales[:, cols],
+                    in_=f_grouped[c][:, lo - first : hi - first, :].rearrange("p c t -> p (c t)"),
+                )
+
+        def repeat_border(n):
+            first = n * SPAN + CELLS
+            new, old = slice(first, first + BORDER_CELLS), slice(first + CELLS, first + CELLS + BORDER_CELLS)
+            nc.gpsimd.tensor_copy(out=f_codes[:, new], in_=f_codes[:, old])
+            nc.gpsimd.tensor_copy(out=f_scales[:, new], in_=f_scales[:, old])
 
         def project_direct(c, first, last):
             if first == 0:
@@ -253,15 +271,15 @@ def tile_coarsematching_kernel(tc, feat_c0, feat_c1, W, b, h0c, w0c, h1c, w1c, o
         low_wide = {}
         low = {}
 
-        def inner_rows(ap):
-            return ap.rearrange("p (r w) -> p r w", w=w0c)[:, BORDER : h0c - BORDER, BORDER : w0c - BORDER]
+        def inner_columns(ap):
+            return ap.rearrange("p (r w) -> p r w", w=w0c)[:, :, BORDER : w0c - BORDER]
 
         def interior(ap):
-            return ap.rearrange("p (r w) -> p r w", w=w1c)[:, BORDER : h1c - BORDER, BORDER : w1c - BORDER]
+            return inner_columns(ap[:, BORDER_CELLS : BORDER_CELLS + INNER])
 
         rows_in = h1c - 2 * BORDER
         cols_in = w1c - 2 * BORDER
-        rows_wide = BANK // w1c - BORDER
+        rows_wide = BANK // w1c
 
         def job_parts(q):
             n, job = divmod(q, JOBS_A_BATCH)
@@ -274,9 +292,9 @@ def tile_coarsematching_kernel(tc, feat_c0, feat_c1, W, b, h0c, w0c, h1c, w1c, o
 
         def similarities(q, rest):
             n, job, is_row, i = job_parts(q)
-            f0_at = 2 * n * CELLS
+            f0_at = n * SPAN
             f1_at = f0_at + CELLS
-            at = (f0_at if is_row else f1_at) + i * P
+            at = (f0_at if is_row else f1_at + BORDER_CELLS) + i * P
             along = f1_at if is_row else f0_at
             acc = narrow_tile("narrow") if rest else wide_tile([P, BANK], "wide")
             first, width = (along + BANK, REST) if rest else (along, BANK)
@@ -323,9 +341,11 @@ def tile_coarsematching_kernel(tc, feat_c0, feat_c1, W, b, h0c, w0c, h1c, w1c, o
         def keys(q):
             n, job, is_row, i = job_parts(q)
             one = slice(job, job + 1)
+            if i == INNER_TILES:
+                return
             if is_row:
                 nc.vector.tensor_scalar(
-                    out=key[n][:, one], in0=total[n][:, one], scalar1=limit[:, i : i + 1], scalar2=1.0,
+                    out=key[n][:, one], in0=total[n][:, one], scalar1=limit[:], scalar2=1.0,
                     op0=ALU.is_ge, op1=ALU.add,
                 )
             else:
@@ -338,6 +358,15 @@ def tile_coarsematching_kernel(tc, feat_c0, feat_c1, W, b, h0c, w0c, h1c, w1c, o
             n, job, is_row, i = job_parts(q)
             one = slice(job, job + 1)
             nc.vector.reciprocal(out=recip[n][:, one], in_=total[n][:, one])
+
+        def store_rows(which, n, i, tile):
+            if i < INNER_TILES:
+                first = BORDER_CELLS + i * P
+                nc.sync.dma_start(out=out[which, n, first : first + P, :], in_=tile[:])
+            else:
+                half = P // 2
+                nc.sync.dma_start(out=out[which, n, CELLS - half : CELLS, :], in_=tile[0:half, :])
+                nc.sync.dma_start(out=out[which, n, 0:half, :], in_=tile[half:P, :])
 
         def normalise(q):
             n, job, is_row, i = job_parts(q)
@@ -352,13 +381,14 @@ def tile_coarsematching_kernel(tc, feat_c0, feat_c1, W, b, h0c, w0c, h1c, w1c, o
                         out=conf0[:], in0=values, scalar1=recip[n][:, one], scalar2=0.0,
                         op0=ALU.mult, op1=ALU.add,
                     )
-                nc.sync.dma_start(out=out[0, n, i * P : (i + 1) * P, :], in_=conf0[:])
+                store_rows(0, n, i, conf0)
             else:
                 nc.scalar.activation(out=values, in_=values, func=ACT.Copy, scale=recip[n][:, one])
-                nc.gpsimd.tensor_scalar(
-                    out=inner_rows(miss_t[n][:, i, :]), in0=inner_rows(values), scalar1=-1.0,
-                    scalar2=key[n][:, one], op0=ALU.mult, op1=ALU.add,
-                )
+                if i < INNER_TILES:
+                    nc.gpsimd.tensor_scalar(
+                        out=inner_columns(miss_t[n][:, i, :]), in0=inner_columns(values[:, 0:INNER]), scalar1=-1.0,
+                        scalar2=key[n][:, one], op0=ALU.mult, op1=ALU.add,
+                    )
 
         flipped_columns = {}
         flipped_miss = {}
@@ -378,17 +408,19 @@ def tile_coarsematching_kernel(tc, feat_c0, feat_c1, W, b, h0c, w0c, h1c, w1c, o
 
         def flip_miss(n, i):
             rows = slice(i * P, (i + 1) * P)
-            miss1 = aux_tile([P, CELLS], BF16, "miss1")
-            for j in range(CELL_TILES):
+            miss1 = aux_tile([P, INNER], BF16, "miss1")
+            for j in range(INNER_TILES):
                 nc.tensor.transpose(miss1[:, j * P : (j + 1) * P], miss_t[n][:, j, rows], identity_bf[:])
             flipped_miss[n, i] = miss1
 
         def store_conf1(n, i):
             conf1_wide, conf1_narrow = flipped_columns[n, i]
             conf1 = work.tile([P, CELLS], F32, name="conf1", bufs=6)
-            nc.scalar.copy(out=conf1[:, BANK:CELLS], in_=conf1_narrow[:, 0:REST])
-            nc.scalar.copy(out=conf1[:, 0:BANK], in_=conf1_wide[:])
-            nc.sync.dma_start(out=out[1, n, i * P : (i + 1) * P, :], in_=conf1[:])
+            last = REST - BORDER_CELLS
+            nc.scalar.copy(out=conf1[:, CELLS - last : CELLS], in_=conf1_narrow[:, 0:last])
+            nc.scalar.copy(out=conf1[:, 0:BORDER_CELLS], in_=conf1_narrow[:, last:REST])
+            nc.scalar.copy(out=conf1[:, BORDER_CELLS : CELLS - last], in_=conf1_wide[:])
+            store_rows(1, n, i, conf1)
 
         def keep_mask(n, i):
             miss1 = flipped_miss[n, i]
@@ -396,7 +428,7 @@ def tile_coarsematching_kernel(tc, feat_c0, feat_c1, W, b, h0c, w0c, h1c, w1c, o
             mask[n, i] = work.tile([P, rows_in, cols_in], BF16, name="mask")
             nc.vector.scalar_tensor_tensor(
                 out=mask[n, i][:], in0=interior(numer[n, i][:]), scalar=key[n][:, one],
-                in1=interior(miss1[:]), op0=ALU.is_ge, op1=ALU.is_ge,
+                in1=inner_columns(miss1[:]), op0=ALU.is_ge, op1=ALU.is_ge,
             )
 
         def best_of_two(n, i, second):
@@ -405,24 +437,23 @@ def tile_coarsematching_kernel(tc, feat_c0, feat_c1, W, b, h0c, w0c, h1c, w1c, o
                 best[n, i] = work.tile([P, rows_in, cols_in], F32, name="best")
             grid = flipped_columns[n, i][1 if second else 0][:].rearrange("p (r w) -> p r w", w=w1c)
             rows = slice(rows_wide, rows_in) if second else slice(0, rows_wide)
-            first = 0 if second else BORDER
             nc.vector.scalar_tensor_tensor(
                 out=best[n, i][:, rows, :],
                 in0=interior(numer[n, i][:])[:, rows, :],
                 scalar=recip[n][:, one],
-                in1=grid[:, first : first + rows.stop - rows.start, BORDER : w1c - BORDER],
+                in1=grid[:, 0 : rows.stop - rows.start, BORDER : w1c - BORDER],
                 op0=ALU.mult,
                 op1=ALU.max,
             )
 
         def multiply_mconf(n, i):
-            on_vector = (n, i) == (BATCH - 1, CELL_TILES - 1)
+            on_vector = (n, i) == (BATCH - 1, INNER_TILES - 1)
             mconf = mconf_tiles[i % len(mconf_tiles)]
             engine = nc.vector if on_vector else nc.gpsimd
             engine.tensor_tensor(out=interior(mconf[:]), in0=mask[n, i][:], in1=best[n, i][:], op=ALU.mult)
 
         def store_mconf(n, i):
-            nc.sync.dma_start(out=out[2, n, i * P : (i + 1) * P, :], in_=mconf_tiles[i % len(mconf_tiles)][:])
+            store_rows(2, n, i, mconf_tiles[i % len(mconf_tiles)])
 
         w_banks = flip(w_raw[:], 0, True)
         hold_clock(2)
@@ -493,34 +524,39 @@ def tile_coarsematching_kernel(tc, feat_c0, feat_c1, W, b, h0c, w0c, h1c, w1c, o
                 minimum_wide(q + 1)
             if 0 <= q - 1 < JOBS:
                 keys(q - 1)
-            if shown and shown[0] == 0:
+            inner_stored = stored and stored[1] < INNER_TILES
+            inner_shown = shown and shown[1] < INNER_TILES
+            if inner_shown and shown[0] == 0:
                 keep_mask(*shown)
             if 0 <= q + 1 < JOBS:
                 minimum_narrow(q + 1)
             if shown:
                 store_conf1(*shown)
-                if stored:
+                if inner_stored:
                     store_mconf(*stored)
             if 0 <= q < JOBS:
                 exponentials(q)
             if 0 <= q - 1 < JOBS:
                 normalise(q - 1)
-            if stored and not shown:
+            if inner_stored and not shown:
                 store_mconf(*stored)
             for step, c in front.get(q, []):
                 front_step(step, c)
             if flips:
                 flip_conf1(*flips, q >= JOBS - 2)
-            if shown:
+            if inner_shown:
                 best_of_two(*shown, False)
                 best_of_two(*shown, True)
                 if shown[0] == 1:
                     keep_mask(*shown)
-            if flips:
+            if flips and flips[1] < INNER_TILES:
                 flip_miss(*flips)
-            if shown:
+            if inner_shown:
                 multiply_mconf(*shown)
             if q == -2:
                 regroup(EARLY_CHUNKS - 1)
             if q == -1:
                 quantise_features(EARLY_CHUNKS - 1)
+                repeat_border(0)
+            if q == 11:
+                repeat_border(1)

@@ -24,7 +24,6 @@ TOKENS = 2 * BATCH * CELLS
 BORDER_CELLS = 64
 INNER = CELLS - 2 * BORDER_CELLS
 INNER_TILES = INNER // P
-SPAN = 2 * CELLS + BORDER_CELLS
 CHUNK = BANK
 CHUNK_TILES = CHUNK // P
 CHUNKS = TOKENS // CHUNK
@@ -74,13 +73,18 @@ def tile_coarsematching_kernel(tc, feat_c0, feat_c1, W, b, h0c, w0c, h1c, w1c, o
         def load_tokens(n, g, first, count):
             feat = (feat_c0, feat_c1)[g]
             at = (2 * n + g) * CELL_TILES + first
+            if g == 1:
+                nc.sync.dma_start(
+                    out=x_raw_tiles[:, at : at + count, :],
+                    in_=feat[n].rearrange("(j p) k -> p j k", p=P)[:, first : first + count, :],
+                )
+                return
             inner = min(count, INNER_TILES - first)
             rows = feat[n, BORDER_CELLS + first * P : BORDER_CELLS + (first + inner) * P, :]
             nc.sync.dma_start(out=x_raw_tiles[:, at : at + inner, :], in_=rows.rearrange("(j p) k -> p j k", p=P))
             if inner < count:
-                half = P // 2
-                nc.sync.dma_start(out=x_raw_tiles[0:half, at + inner, :], in_=feat[n, CELLS - half : CELLS, :])
-                nc.sync.dma_start(out=x_raw_tiles[half:P, at + inner, :], in_=feat[n, 0:half, :])
+                nc.sync.dma_start(out=x_raw_tiles[0:P:2, at + inner, :], in_=feat[n, CELLS - BORDER_CELLS : CELLS, :])
+                nc.sync.dma_start(out=x_raw_tiles[1:P:2, at + inner, :], in_=feat[n, 0:BORDER_CELLS, :])
 
         load_tokens(0, 0, 0, 4)
         nc.sync.dma_start(out=b_raw[:], in_=b.rearrange("(p t) -> p t", t=PACK))
@@ -127,12 +131,11 @@ def tile_coarsematching_kernel(tc, feat_c0, feat_c1, W, b, h0c, w0c, h1c, w1c, o
             nc.scalar.activation(out=mconf[:], in_=zero[:].to_broadcast([P, CELLS]), func=ACT.Copy)
             mconf_tiles.append(mconf)
         for n in range(BATCH):
-            half = P // 2
-            for rows in (slice(0, half), slice(CELLS - half, CELLS)):
-                nc.sync.dma_start(out=out[2, n, rows, :], in_=mconf_tiles[n][0:half, :])
+            for rows in (slice(0, BORDER_CELLS), slice(CELLS - BORDER_CELLS, CELLS)):
+                nc.sync.dma_start(out=out[2, n, rows, :], in_=mconf_tiles[n][0:P:2, :])
         miss_t = []
         for n in range(BATCH):
-            miss = keep.tile([P, INNER_TILES, INNER], BF16, name="miss_t%d" % n)
+            miss = keep.tile([P, CELL_TILES, INNER], BF16, name="miss_t%d" % n)
             grid_rows = miss[:].rearrange("p j (r w) -> p (j r) w", w=w0c)
             nc.vector.memset(grid_rows[:, :, 0:BORDER], 1.0)
             nc.vector.memset(grid_rows[:, :, w0c - BORDER : w0c], 1.0)
@@ -167,8 +170,8 @@ def tile_coarsematching_kernel(tc, feat_c0, feat_c1, W, b, h0c, w0c, h1c, w1c, o
         w_scales = keep.tile([P, FEATURES], U8, align_bytes=64)
         x_codes = keep.tile([P, TOKENS], U32, align_bytes=64)
         x_scales = keep.tile([P, TOKENS], U8, align_bytes=64)
-        f_codes = keep.tile([P, BATCH * SPAN], U32, align_bytes=64)
-        f_scales = keep.tile([P, BATCH * SPAN], U8, align_bytes=64)
+        f_codes = keep.tile([P, TOKENS], U32, align_bytes=64)
+        f_scales = keep.tile([P, TOKENS], U8, align_bytes=64)
         x_banks = {}
         x_grouped = {}
         f_rows = {}
@@ -219,23 +222,12 @@ def tile_coarsematching_kernel(tc, feat_c0, feat_c1, W, b, h0c, w0c, h1c, w1c, o
                 nc.vector.tensor_copy(out=grouped, in_=rows)
 
         def quantise_features(c):
-            n, part = divmod(c, EARLY_CHUNKS)
-            first, end = part * CHUNK, (part + 1) * CHUNK
-            cuts = [first] + [CELLS] * (first < CELLS < end) + [end]
-            for lo, hi in zip(cuts[:-1], cuts[1:]):
-                at = n * SPAN + lo + (BORDER_CELLS if lo >= CELLS else 0)
-                cols = slice(at, at + hi - lo)
-                nc.vector.quantize_mx(
-                    out=f_codes[:, cols].bitcast(FP8X4),
-                    scales=f_scales[:, cols],
-                    in_=f_grouped[c][:, lo - first : hi - first, :].rearrange("p c t -> p (c t)"),
-                )
-
-        def repeat_border(n):
-            first = n * SPAN + CELLS
-            new, old = slice(first, first + BORDER_CELLS), slice(first + CELLS, first + CELLS + BORDER_CELLS)
-            nc.gpsimd.tensor_copy(out=f_codes[:, new], in_=f_codes[:, old])
-            nc.gpsimd.tensor_copy(out=f_scales[:, new], in_=f_scales[:, old])
+            cols = chunk_columns(c)
+            nc.vector.quantize_mx(
+                out=f_codes[:, cols].bitcast(FP8X4),
+                scales=f_scales[:, cols],
+                in_=f_grouped[c][:].rearrange("p c t -> p (c t)"),
+            )
 
         def project_direct(c, first, last):
             if first == 0:
@@ -279,7 +271,7 @@ def tile_coarsematching_kernel(tc, feat_c0, feat_c1, W, b, h0c, w0c, h1c, w1c, o
 
         rows_in = h1c - 2 * BORDER
         cols_in = w1c - 2 * BORDER
-        rows_wide = BANK // w1c
+        rows_wide = BANK // w1c - BORDER
 
         def job_parts(q):
             n, job = divmod(q, JOBS_A_BATCH)
@@ -292,9 +284,9 @@ def tile_coarsematching_kernel(tc, feat_c0, feat_c1, W, b, h0c, w0c, h1c, w1c, o
 
         def similarities(q, rest):
             n, job, is_row, i = job_parts(q)
-            f0_at = n * SPAN
+            f0_at = 2 * n * CELLS
             f1_at = f0_at + CELLS
-            at = (f0_at if is_row else f1_at + BORDER_CELLS) + i * P
+            at = (f0_at if is_row else f1_at) + i * P
             along = f1_at if is_row else f0_at
             acc = narrow_tile("narrow") if rest else wide_tile([P, BANK], "wide")
             first, width = (along + BANK, REST) if rest else (along, BANK)
@@ -341,7 +333,7 @@ def tile_coarsematching_kernel(tc, feat_c0, feat_c1, W, b, h0c, w0c, h1c, w1c, o
         def keys(q):
             n, job, is_row, i = job_parts(q)
             one = slice(job, job + 1)
-            if i == INNER_TILES:
+            if is_row and i == INNER_TILES:
                 return
             if is_row:
                 nc.vector.tensor_scalar(
@@ -364,9 +356,8 @@ def tile_coarsematching_kernel(tc, feat_c0, feat_c1, W, b, h0c, w0c, h1c, w1c, o
                 first = BORDER_CELLS + i * P
                 nc.sync.dma_start(out=out[which, n, first : first + P, :], in_=tile[:])
             else:
-                half = P // 2
-                nc.sync.dma_start(out=out[which, n, CELLS - half : CELLS, :], in_=tile[0:half, :])
-                nc.sync.dma_start(out=out[which, n, 0:half, :], in_=tile[half:P, :])
+                nc.sync.dma_start(out=out[which, n, CELLS - BORDER_CELLS : CELLS, :], in_=tile[0:P:2, :])
+                nc.sync.dma_start(out=out[which, n, 0:BORDER_CELLS, :], in_=tile[1:P:2, :])
 
         def normalise(q):
             n, job, is_row, i = job_parts(q)
@@ -384,11 +375,10 @@ def tile_coarsematching_kernel(tc, feat_c0, feat_c1, W, b, h0c, w0c, h1c, w1c, o
                 store_rows(0, n, i, conf0)
             else:
                 nc.scalar.activation(out=values, in_=values, func=ACT.Copy, scale=recip[n][:, one])
-                if i < INNER_TILES:
-                    nc.gpsimd.tensor_scalar(
-                        out=inner_columns(miss_t[n][:, i, :]), in0=inner_columns(values[:, 0:INNER]), scalar1=-1.0,
-                        scalar2=key[n][:, one], op0=ALU.mult, op1=ALU.add,
-                    )
+                nc.gpsimd.tensor_scalar(
+                    out=inner_columns(miss_t[n][:, i, :]), in0=inner_columns(values[:, 0:INNER]), scalar1=-1.0,
+                    scalar2=key[n][:, one], op0=ALU.mult, op1=ALU.add,
+                )
 
         flipped_columns = {}
         flipped_miss = {}
@@ -408,18 +398,16 @@ def tile_coarsematching_kernel(tc, feat_c0, feat_c1, W, b, h0c, w0c, h1c, w1c, o
 
         def flip_miss(n, i):
             rows = slice(i * P, (i + 1) * P)
-            miss1 = aux_tile([P, INNER], BF16, "miss1")
-            for j in range(INNER_TILES):
+            miss1 = aux_tile([P, CELLS], BF16, "miss1")
+            for j in range(CELL_TILES):
                 nc.tensor.transpose(miss1[:, j * P : (j + 1) * P], miss_t[n][:, j, rows], identity_bf[:])
             flipped_miss[n, i] = miss1
 
         def store_conf1(n, i):
             conf1_wide, conf1_narrow = flipped_columns[n, i]
             conf1 = work.tile([P, CELLS], F32, name="conf1", bufs=6)
-            last = REST - BORDER_CELLS
-            nc.scalar.copy(out=conf1[:, CELLS - last : CELLS], in_=conf1_narrow[:, 0:last])
-            nc.scalar.copy(out=conf1[:, 0:BORDER_CELLS], in_=conf1_narrow[:, last:REST])
-            nc.scalar.copy(out=conf1[:, BORDER_CELLS : CELLS - last], in_=conf1_wide[:])
+            nc.scalar.copy(out=conf1[:, BANK:CELLS], in_=conf1_narrow[:, 0:REST])
+            nc.scalar.copy(out=conf1[:, 0:BANK], in_=conf1_wide[:])
             store_rows(1, n, i, conf1)
 
         def keep_mask(n, i):
@@ -428,7 +416,7 @@ def tile_coarsematching_kernel(tc, feat_c0, feat_c1, W, b, h0c, w0c, h1c, w1c, o
             mask[n, i] = work.tile([P, rows_in, cols_in], BF16, name="mask")
             nc.vector.scalar_tensor_tensor(
                 out=mask[n, i][:], in0=interior(numer[n, i][:]), scalar=key[n][:, one],
-                in1=inner_columns(miss1[:]), op0=ALU.is_ge, op1=ALU.is_ge,
+                in1=interior(miss1[:]), op0=ALU.is_ge, op1=ALU.is_ge,
             )
 
         def best_of_two(n, i, second):
@@ -437,11 +425,12 @@ def tile_coarsematching_kernel(tc, feat_c0, feat_c1, W, b, h0c, w0c, h1c, w1c, o
                 best[n, i] = work.tile([P, rows_in, cols_in], F32, name="best")
             grid = flipped_columns[n, i][1 if second else 0][:].rearrange("p (r w) -> p r w", w=w1c)
             rows = slice(rows_wide, rows_in) if second else slice(0, rows_wide)
+            first = 0 if second else BORDER
             nc.vector.scalar_tensor_tensor(
                 out=best[n, i][:, rows, :],
                 in0=interior(numer[n, i][:])[:, rows, :],
                 scalar=recip[n][:, one],
-                in1=grid[:, 0 : rows.stop - rows.start, BORDER : w1c - BORDER],
+                in1=grid[:, first : first + rows.stop - rows.start, BORDER : w1c - BORDER],
                 op0=ALU.mult,
                 op1=ALU.max,
             )
@@ -557,6 +546,3 @@ def tile_coarsematching_kernel(tc, feat_c0, feat_c1, W, b, h0c, w0c, h1c, w1c, o
                 regroup(EARLY_CHUNKS - 1)
             if q == -1:
                 quantise_features(EARLY_CHUNKS - 1)
-                repeat_border(0)
-            if q == 11:
-                repeat_border(1)

@@ -83,8 +83,8 @@ def tile_coarsematching_kernel(tc, feat_c0, feat_c1, W, b, h0c, w0c, h1c, w1c, o
             rows = feat[n, BORDER_CELLS + first * P : BORDER_CELLS + (first + inner) * P, :]
             nc.sync.dma_start(out=x_raw_tiles[:, at : at + inner, :], in_=rows.rearrange("(j p) k -> p j k", p=P))
             if inner < count:
-                nc.sync.dma_start(out=x_raw_tiles[0:P:2, at + inner, :], in_=feat[n, CELLS - BORDER_CELLS : CELLS, :])
-                nc.sync.dma_start(out=x_raw_tiles[1:P:2, at + inner, :], in_=feat[n, 0:BORDER_CELLS, :])
+                nc.sync.dma_start(out=x_raw_tiles[0:BORDER_CELLS, at + inner, :], in_=feat[n, CELLS - BORDER_CELLS : CELLS, :])
+                nc.sync.dma_start(out=x_raw_tiles[BORDER_CELLS:P, at + inner, :], in_=feat[n, 0:BORDER_CELLS, :])
 
         load_tokens(0, 0, 0, 4)
         nc.sync.dma_start(out=b_raw[:], in_=b.rearrange("(p t) -> p t", t=PACK))
@@ -156,14 +156,19 @@ def tile_coarsematching_kernel(tc, feat_c0, feat_c1, W, b, h0c, w0c, h1c, w1c, o
                 banks.append(flipped)
             return banks
 
-        def gather(banks, vector_banks):
+        def gather(banks, vector_banks, border=False):
             grouped = stage.tile([P, CHUNK * PACK], BF16, name="grouped", bufs=3, align_bytes=64)
             halves = grouped[:].bitcast(F32).rearrange("p (h r c u) -> p h r c u", h=2, r=2, u=2)
             for h in range(2):
-                if h < vector_banks:
-                    nc.vector.tensor_copy(out=halves[:, h], in_=banks[h][:].rearrange("p r u c -> p r c u"))
+                copy = nc.vector.tensor_copy if h < vector_banks else nc.scalar.copy
+                if border and h == 0:
+                    copy(out=halves[:, h, 0], in_=banks[h][:, 0].rearrange("p u c -> p c u"))
+                    copy(
+                        out=halves[:, h, 1].rearrange("p (c e) u -> p c e u", e=2),
+                        in_=banks[h][:, 1].rearrange("p u (e c) -> p c e u", e=2),
+                    )
                 else:
-                    nc.scalar.copy(out=halves[:, h], in_=banks[h][:].rearrange("p r u c -> p r c u"))
+                    copy(out=halves[:, h], in_=banks[h][:].rearrange("p r u c -> p r c u"))
             return grouped
 
         w_codes = keep.tile([P, FEATURES], U32, align_bytes=64)
@@ -184,7 +189,7 @@ def tile_coarsematching_kernel(tc, feat_c0, feat_c1, W, b, h0c, w0c, h1c, w1c, o
             x_banks[c] = flip(x_raw[:], c * CHUNK_TILES, early)
 
         def gather_tokens(c, vector_banks):
-            x_grouped[c] = gather(x_banks[c], vector_banks)
+            x_grouped[c] = gather(x_banks[c], vector_banks, c % EARLY_CHUNKS == 1)
 
         def quantise_tokens(c):
             cols = chunk_columns(c)

@@ -31,6 +31,7 @@ JOBS_A_BATCH = 2 * CELL_TILES
 JOBS = BATCH * JOBS_A_BATCH
 BORDER = 2
 EARLY_CHUNKS = CHUNKS // BATCH
+FRONT_STEPS = (("flip", "gather", "quantise x"), ("first half",), (), ("second half",), ("regroup",), ("quantise f",))
 INV_THRESHOLD = 5.0
 INV_TEMPERATURE = 10.0
 INV_SQRT_FEATURES = 1.0 / math.sqrt(FEATURES)
@@ -48,7 +49,7 @@ def tile_coarsematching_kernel(tc, feat_c0, feat_c1, W, b, h0c, w0c, h1c, w1c, o
         keep = ctx.enter_context(tc.tile_pool(name="keep", bufs=1))
         stage = ctx.enter_context(tc.tile_pool(name="stage", bufs=2))
         work = ctx.enter_context(tc.tile_pool(name="work", bufs=3))
-        small = ctx.enter_context(tc.tile_pool(name="small", bufs=4))
+        small = ctx.enter_context(tc.tile_pool(name="small", bufs=6))
         psum = ctx.enter_context(tc.psum_pool(name="psum", bufs=1))
         ctx.enter_context(tc.manual_schedule())
 
@@ -86,7 +87,8 @@ def tile_coarsematching_kernel(tc, feat_c0, feat_c1, W, b, h0c, w0c, h1c, w1c, o
                 nc.sync.dma_start(out=x_raw_tiles[0:BORDER_CELLS, at + inner, :], in_=feat[n, CELLS - BORDER_CELLS : CELLS, :])
                 nc.sync.dma_start(out=x_raw_tiles[BORDER_CELLS:P, at + inner, :], in_=feat[n, 0:BORDER_CELLS, :])
 
-        load_tokens(0, 0, 0, 4)
+        load_tokens(0, 0, 0, 2)
+        load_tokens(0, 0, 2, 2)
         nc.sync.dma_start(out=b_raw[:], in_=b.rearrange("(p t) -> p t", t=PACK))
         load_tokens(0, 0, 4, 2)
         load_tokens(0, 1, 0, 2)
@@ -221,7 +223,7 @@ def tile_coarsematching_kernel(tc, feat_c0, feat_c1, W, b, h0c, w0c, h1c, w1c, o
             f_grouped[c] = stage.tile([P, CHUNK, PACK], BF16, name="f_grouped", align_bytes=64)
             grouped = f_grouped[c][:].rearrange("p (c i) t -> p c t i", i=4)
             rows = f_rows[c][:].rearrange("p t (c i) -> p c t i", i=4)
-            if c == CHUNKS - 1:
+            if c >= EARLY_CHUNKS - 1:
                 nc.scalar.copy(out=grouped, in_=rows)
             else:
                 nc.vector.tensor_copy(out=grouped, in_=rows)
@@ -314,7 +316,7 @@ def tile_coarsematching_kernel(tc, feat_c0, feat_c1, W, b, h0c, w0c, h1c, w1c, o
                 recip[n] = keep.tile([P, JOBS_A_BATCH], F32, name="recip%d" % n)
                 key[n] = keep.tile([P, JOBS_A_BATCH], F32, name="key%d" % n)
             if is_row:
-                numer[n, i] = work.tile([P, CELLS], F32, name="numer", bufs=7)
+                numer[n, i] = work.tile([P, CELLS], F32, name="numer", bufs=9)
             low_wide[q] = small.tile([P, 1], F32, name="low_wide")
             nc.vector.tensor_scalar(
                 out=job_values(q)[:, 0:BANK], in0=sim_banks[q, False][:], scalar1=-INV_TEMPERATURE,
@@ -341,12 +343,12 @@ def tile_coarsematching_kernel(tc, feat_c0, feat_c1, W, b, h0c, w0c, h1c, w1c, o
             if is_row and i == INNER_TILES:
                 return
             if is_row:
-                nc.vector.tensor_scalar(
+                nc.gpsimd.tensor_scalar(
                     out=key[n][:, one], in0=total[n][:, one], scalar1=limit[:], scalar2=1.0,
                     op0=ALU.is_ge, op1=ALU.add,
                 )
             else:
-                nc.vector.tensor_scalar(
+                nc.gpsimd.tensor_scalar(
                     out=key[n][:, one], in0=total[n][:, one], scalar1=INV_THRESHOLD,
                     scalar2=recip[n][:, one], op0=ALU.is_ge, op1=ALU.max,
                 )
@@ -370,7 +372,7 @@ def tile_coarsematching_kernel(tc, feat_c0, feat_c1, W, b, h0c, w0c, h1c, w1c, o
             values = job_values(q)
             if is_row:
                 conf0 = work.tile([P, CELLS], F32, name="conf0", bufs=6)
-                if n == BATCH - 1 and i % 2 == 0:
+                if (n, i) == (BATCH - 1, 0):
                     nc.scalar.activation(out=conf0[:], in_=values, func=ACT.Copy, scale=recip[n][:, one])
                 else:
                     nc.gpsimd.tensor_scalar(
@@ -379,7 +381,13 @@ def tile_coarsematching_kernel(tc, feat_c0, feat_c1, W, b, h0c, w0c, h1c, w1c, o
                     )
                 store_rows(0, n, i, conf0)
             else:
-                nc.scalar.activation(out=values, in_=values, func=ACT.Copy, scale=recip[n][:, one])
+                if n == 0 or i % 2 == 1:
+                    nc.gpsimd.tensor_scalar(
+                        out=values, in0=values, scalar1=recip[n][:, one], scalar2=0.0,
+                        op0=ALU.mult, op1=ALU.add,
+                    )
+                else:
+                    nc.scalar.activation(out=values, in_=values, func=ACT.Copy, scale=recip[n][:, one])
                 nc.gpsimd.tensor_scalar(
                     out=inner_columns(miss_t[n][:, i, :]), in0=inner_columns(values[:, 0:INNER]), scalar1=-1.0,
                     scalar2=key[n][:, one], op0=ALU.mult, op1=ALU.add,
@@ -455,7 +463,7 @@ def tile_coarsematching_kernel(tc, feat_c0, feat_c1, W, b, h0c, w0c, h1c, w1c, o
         flip_tokens(0, False)
         hold_clock(2)
         nc.vector.quantize_mx(out=w_codes[:].bitcast(FP8X4), scales=w_scales[:], in_=w_grouped[:])
-        gather_tokens(0, 1)
+        gather_tokens(0, 0)
         nc.vector.tensor_scalar_mul(out=b_scaled[:], in0=b_raw[:], scalar1=INV_SQRT_FEATURES)
         flip_tokens(1, True)
         hold_clock(2)
@@ -467,87 +475,101 @@ def tile_coarsematching_kernel(tc, feat_c0, feat_c1, W, b, h0c, w0c, h1c, w1c, o
         gather_tokens(2, 2)
         project(1, 0, PACK)
         quantise_tokens(2)
-        regroup(0)
         project(2, 0, PACK)
+        regroup(0)
         quantise_features(0)
         regroup(1)
         quantise_features(1)
+        regroup(2)
 
         front = {}
         for c in range(EARLY_CHUNKS, CHUNKS):
             start = 3 * (c - EARLY_CHUNKS) - 1
-            for k, step in enumerate(("flip", "quantise x", "first half", "second half", "regroup", "quantise f")):
-                front[start + k] = front.get(start + k, []) + [(step, c)]
+            for k, steps in enumerate(FRONT_STEPS):
+                for step in steps:
+                    front[start + k, step] = c
 
-        def front_step(step, c):
-            direct = c < CHUNKS - 1
+        def front_step(q, step):
+            c = front.get((q, step))
+            if c is None:
+                return
+            direct = c == EARLY_CHUNKS
             if step == "flip":
                 flip_tokens(c, False)
-                gather_tokens(c, 0)
+            elif step == "gather":
+                gather_tokens(c, 2 if c == CHUNKS - 1 else 0)
             elif step == "quantise x":
                 quantise_tokens(c)
             elif step in ("first half", "second half"):
                 first = 0 if step == "first half" else 2
-                if direct:
-                    project_direct(c, first, first + 2)
-                else:
-                    project(c, first, first + 2)
+                (project_direct if direct else project)(c, first, first + 2)
             elif step == "regroup":
                 if not direct:
                     regroup(c)
             else:
                 quantise_features(c)
 
-        def flip_round(n, i):
-            complete = n * JOBS_A_BATCH + CELL_TILES + 1
-            return complete + max(1, 2 * i) if n == 0 else complete + i
+        def tile_at(n, q):
+            i, rest = divmod(q - 8, 2) if n == 0 else (q - 20, 0)
+            return i if rest == 0 and 0 <= i < CELL_TILES else None
 
-        flips_at = {}
-        for n in range(BATCH):
-            for i in range(CELL_TILES):
-                flips_at[flip_round(n, i)] = (n, i)
+        def inner(i):
+            return i is not None and i < INNER_TILES
 
-        for q in range(-2, JOBS + 3):
-            flips, shown, stored = flips_at.get(q), flips_at.get(q - 1), flips_at.get(q - 2)
+        for q in range(-2, JOBS + 4):
+            flips, shown, stored = tile_at(0, q), tile_at(0, q - 1), tile_at(0, q - 2)
+            late, late_shown, late_stored = tile_at(1, q), tile_at(1, q - 1), tile_at(1, q - 2)
             if 0 <= q + 2 < JOBS:
                 similarities(q + 2, False)
                 similarities(q + 2, True)
-            if 0 <= q - 1 < JOBS:
-                reciprocals(q - 1)
-            if 0 <= q + 1 < JOBS:
-                minimum_wide(q + 1)
+            if inner(shown):
+                keep_mask(0, shown)
             if 0 <= q - 1 < JOBS:
                 keys(q - 1)
-            inner_stored = stored and stored[1] < INNER_TILES
-            inner_shown = shown and shown[1] < INNER_TILES
-            if inner_shown and shown[0] == 0:
-                keep_mask(*shown)
-            if 0 <= q + 1 < JOBS:
-                minimum_narrow(q + 1)
-            if shown:
-                store_conf1(*shown)
-                if inner_stored:
-                    store_mconf(*stored)
+            if shown is not None:
+                store_conf1(0, shown)
+            if late is not None:
+                flip_conf1(1, late, q >= JOBS - 2)
+            if inner(late_shown):
+                best_of_two(1, late_shown, False)
+                best_of_two(1, late_shown, True)
+            if inner(late_stored):
+                store_mconf(1, late_stored)
+            if inner(stored):
+                multiply_mconf(0, stored)
             if 0 <= q < JOBS:
                 exponentials(q)
+            if 0 <= q + 1 < JOBS:
+                minimum_narrow(q + 1)
+            front_step(q, "flip")
+            if inner(late):
+                flip_miss(1, late)
+            if 0 <= q + 2 < JOBS:
+                minimum_wide(q + 2)
+            if inner(late):
+                keep_mask(1, late)
+            front_step(q, "gather")
+            front_step(q, "second half")
+            front_step(q, "regroup")
             if 0 <= q - 1 < JOBS:
                 normalise(q - 1)
-            if inner_stored and not shown:
-                store_mconf(*stored)
-            for step, c in front.get(q, []):
-                front_step(step, c)
-            if flips:
-                flip_conf1(*flips, q >= JOBS - 2)
-            if inner_shown:
-                best_of_two(*shown, False)
-                best_of_two(*shown, True)
-                if shown[0] == 1:
-                    keep_mask(*shown)
-            if flips and flips[1] < INNER_TILES:
-                flip_miss(*flips)
-            if inner_shown:
-                multiply_mconf(*shown)
-            if q == -2:
-                regroup(EARLY_CHUNKS - 1)
+            if flips is not None:
+                flip_conf1(0, flips, False)
+            if inner(shown):
+                best_of_two(0, shown, False)
+                best_of_two(0, shown, True)
+            if late is not None:
+                store_conf1(1, late)
+            if inner(stored):
+                store_mconf(0, stored)
+            front_step(q, "quantise f")
             if q == -1:
                 quantise_features(EARLY_CHUNKS - 1)
+            if inner(late_shown):
+                multiply_mconf(1, late_shown)
+            front_step(q, "quantise x")
+            front_step(q, "first half")
+            if 0 <= q < JOBS:
+                reciprocals(q)
+            if inner(flips):
+                flip_miss(0, flips)

@@ -31,7 +31,7 @@ JOBS_A_BATCH = 2 * CELL_TILES
 JOBS = BATCH * JOBS_A_BATCH
 BORDER = 2
 EARLY_CHUNKS = CHUNKS // BATCH
-FRONT_STEPS = (("flip", "gather", "quantise x"), ("first half",), (), ("second half",), ("regroup",), ("quantise f",))
+FRONT_STEPS = (("flip", "gather"), ("quantise x",), ("first half",), ("second half",), ("regroup",), ("quantise f",))
 INV_THRESHOLD = 5.0
 INV_TEMPERATURE = 10.0
 INV_SQRT_FEATURES = 1.0 / math.sqrt(FEATURES)
@@ -343,12 +343,12 @@ def tile_coarsematching_kernel(tc, feat_c0, feat_c1, W, b, h0c, w0c, h1c, w1c, o
             if is_row and i == INNER_TILES:
                 return
             if is_row:
-                nc.gpsimd.tensor_scalar(
+                nc.vector.tensor_scalar(
                     out=key[n][:, one], in0=total[n][:, one], scalar1=limit[:], scalar2=1.0,
                     op0=ALU.is_ge, op1=ALU.add,
                 )
             else:
-                nc.gpsimd.tensor_scalar(
+                nc.vector.tensor_scalar(
                     out=key[n][:, one], in0=total[n][:, one], scalar1=INV_THRESHOLD,
                     scalar2=recip[n][:, one], op0=ALU.is_ge, op1=ALU.max,
                 )
@@ -372,7 +372,7 @@ def tile_coarsematching_kernel(tc, feat_c0, feat_c1, W, b, h0c, w0c, h1c, w1c, o
             values = job_values(q)
             if is_row:
                 conf0 = work.tile([P, CELLS], F32, name="conf0", bufs=6)
-                if (n, i) == (BATCH - 1, 0):
+                if n == BATCH - 1 and i % 2 == 0:
                     nc.scalar.activation(out=conf0[:], in_=values, func=ACT.Copy, scale=recip[n][:, one])
                 else:
                     nc.gpsimd.tensor_scalar(
@@ -381,14 +381,16 @@ def tile_coarsematching_kernel(tc, feat_c0, feat_c1, W, b, h0c, w0c, h1c, w1c, o
                     )
                 store_rows(0, n, i, conf0)
             else:
-                if n == 0 or i % 2 == 1:
+                second_half = n == 0 and i >= CELL_TILES // 2
+                if second_half or (n == 1 and i % 2 == 0):
                     nc.gpsimd.tensor_scalar(
                         out=values, in0=values, scalar1=recip[n][:, one], scalar2=0.0,
                         op0=ALU.mult, op1=ALU.add,
                     )
                 else:
                     nc.scalar.activation(out=values, in_=values, func=ACT.Copy, scale=recip[n][:, one])
-                nc.gpsimd.tensor_scalar(
+                engine = nc.vector if second_half else nc.gpsimd
+                engine.tensor_scalar(
                     out=inner_columns(miss_t[n][:, i, :]), in0=inner_columns(values[:, 0:INNER]), scalar1=-1.0,
                     scalar2=key[n][:, one], op0=ALU.mult, op1=ALU.add,
                 )
@@ -463,7 +465,7 @@ def tile_coarsematching_kernel(tc, feat_c0, feat_c1, W, b, h0c, w0c, h1c, w1c, o
         flip_tokens(0, False)
         hold_clock(2)
         nc.vector.quantize_mx(out=w_codes[:].bitcast(FP8X4), scales=w_scales[:], in_=w_grouped[:])
-        gather_tokens(0, 0)
+        gather_tokens(0, 1)
         nc.vector.tensor_scalar_mul(out=b_scaled[:], in0=b_raw[:], scalar1=INV_SQRT_FEATURES)
         flip_tokens(1, True)
         hold_clock(2)
@@ -484,7 +486,7 @@ def tile_coarsematching_kernel(tc, feat_c0, feat_c1, W, b, h0c, w0c, h1c, w1c, o
 
         front = {}
         for c in range(EARLY_CHUNKS, CHUNKS):
-            start = 3 * (c - EARLY_CHUNKS) - 1
+            start = 2 * (c - EARLY_CHUNKS)
             for k, steps in enumerate(FRONT_STEPS):
                 for step in steps:
                     front[start + k, step] = c
@@ -497,7 +499,7 @@ def tile_coarsematching_kernel(tc, feat_c0, feat_c1, W, b, h0c, w0c, h1c, w1c, o
             if step == "flip":
                 flip_tokens(c, False)
             elif step == "gather":
-                gather_tokens(c, 2 if c == CHUNKS - 1 else 0)
+                gather_tokens(c, 1 if c == CHUNKS - 1 else 0)
             elif step == "quantise x":
                 quantise_tokens(c)
             elif step in ("first half", "second half"):
@@ -509,67 +511,52 @@ def tile_coarsematching_kernel(tc, feat_c0, feat_c1, W, b, h0c, w0c, h1c, w1c, o
             else:
                 quantise_features(c)
 
-        def tile_at(n, q):
+        def tile_at(q):
+            n = 0 if q < 20 else 1
             i, rest = divmod(q - 8, 2) if n == 0 else (q - 20, 0)
-            return i if rest == 0 and 0 <= i < CELL_TILES else None
+            return (n, i) if rest == 0 and 0 <= i < CELL_TILES else None
 
-        def inner(i):
-            return i is not None and i < INNER_TILES
+        def inner(tile):
+            return tile is not None and tile[1] < INNER_TILES
 
         for q in range(-2, JOBS + 4):
-            flips, shown, stored = tile_at(0, q), tile_at(0, q - 1), tile_at(0, q - 2)
-            late, late_shown, late_stored = tile_at(1, q), tile_at(1, q - 1), tile_at(1, q - 2)
+            flips, shown, stored = tile_at(q), tile_at(q - 1), tile_at(q - 2)
+            front_step(q, "flip")
+            front_step(q, "quantise x")
+            front_step(q, "regroup")
+            front_step(q, "quantise f")
+            if inner(shown):
+                flip_miss(*shown)
+            if shown is not None:
+                store_conf1(*shown)
+            if flips is not None:
+                flip_conf1(*flips, q >= JOBS - 2)
+            if 0 <= q - 1 < JOBS:
+                reciprocals(q - 1)
+            if inner(shown):
+                keep_mask(*shown)
+            if inner(stored):
+                multiply_mconf(*stored)
+            if inner(flips):
+                best_of_two(*flips, False)
+                best_of_two(*flips, True)
+            if q == 0:
+                quantise_features(EARLY_CHUNKS - 1)
+            if inner(stored):
+                store_mconf(*stored)
+            front_step(q, "first half")
+            if 0 <= q < JOBS:
+                exponentials(q)
+            front_step(q, "second half")
             if 0 <= q + 2 < JOBS:
                 similarities(q + 2, False)
                 similarities(q + 2, True)
-            if inner(shown):
-                keep_mask(0, shown)
-            if 0 <= q - 1 < JOBS:
-                keys(q - 1)
-            if shown is not None:
-                store_conf1(0, shown)
-            if late is not None:
-                flip_conf1(1, late, q >= JOBS - 2)
-            if inner(late_shown):
-                best_of_two(1, late_shown, False)
-                best_of_two(1, late_shown, True)
-            if inner(late_stored):
-                store_mconf(1, late_stored)
-            if inner(stored):
-                multiply_mconf(0, stored)
-            if 0 <= q < JOBS:
-                exponentials(q)
+            front_step(q, "gather")
             if 0 <= q + 1 < JOBS:
                 minimum_narrow(q + 1)
-            front_step(q, "flip")
-            if inner(late):
-                flip_miss(1, late)
+            if 0 <= q - 1 < JOBS:
+                keys(q - 1)
             if 0 <= q + 2 < JOBS:
                 minimum_wide(q + 2)
-            if inner(late):
-                keep_mask(1, late)
-            front_step(q, "gather")
-            front_step(q, "second half")
-            front_step(q, "regroup")
             if 0 <= q - 1 < JOBS:
                 normalise(q - 1)
-            if flips is not None:
-                flip_conf1(0, flips, False)
-            if inner(shown):
-                best_of_two(0, shown, False)
-                best_of_two(0, shown, True)
-            if late is not None:
-                store_conf1(1, late)
-            if inner(stored):
-                store_mconf(0, stored)
-            front_step(q, "quantise f")
-            if q == -1:
-                quantise_features(EARLY_CHUNKS - 1)
-            if inner(late_shown):
-                multiply_mconf(1, late_shown)
-            front_step(q, "quantise x")
-            front_step(q, "first half")
-            if 0 <= q < JOBS:
-                reciprocals(q)
-            if inner(flips):
-                flip_miss(0, flips)

@@ -19,6 +19,7 @@ BATCH = 2
 CELLS = 768
 FEATURES = 512
 CELL_TILES = CELLS // P
+HALF = CELLS // 2
 REST = CELLS - BANK
 TOKENS = 2 * BATCH * CELLS
 BORDER_CELLS = 64
@@ -31,7 +32,7 @@ JOBS_A_BATCH = 2 * CELL_TILES
 JOBS = BATCH * JOBS_A_BATCH
 BORDER = 2
 EARLY_CHUNKS = CHUNKS // BATCH
-FRONT_STEPS = (("flip", "gather"), ("quantise x",), ("first half",), ("second half",), ("regroup",), ("quantise f",))
+FRONT_STEPS = (("flip", "gather"), ("quantise x",), (), ("first half",), ("second half",), ("regroup",), ("quantise f",))
 INV_THRESHOLD = 5.0
 INV_TEMPERATURE = 10.0
 INV_SQRT_FEATURES = 1.0 / math.sqrt(FEATURES)
@@ -87,8 +88,7 @@ def tile_coarsematching_kernel(tc, feat_c0, feat_c1, W, b, h0c, w0c, h1c, w1c, o
                 nc.sync.dma_start(out=x_raw_tiles[0:BORDER_CELLS, at + inner, :], in_=feat[n, CELLS - BORDER_CELLS : CELLS, :])
                 nc.sync.dma_start(out=x_raw_tiles[BORDER_CELLS:P, at + inner, :], in_=feat[n, 0:BORDER_CELLS, :])
 
-        load_tokens(0, 0, 0, 2)
-        load_tokens(0, 0, 2, 2)
+        load_tokens(0, 0, 0, 4)
         nc.sync.dma_start(out=b_raw[:], in_=b.rearrange("(p t) -> p t", t=PACK))
         load_tokens(0, 0, 4, 2)
         load_tokens(0, 1, 0, 2)
@@ -223,7 +223,7 @@ def tile_coarsematching_kernel(tc, feat_c0, feat_c1, W, b, h0c, w0c, h1c, w1c, o
             f_grouped[c] = stage.tile([P, CHUNK, PACK], BF16, name="f_grouped", align_bytes=64)
             grouped = f_grouped[c][:].rearrange("p (c i) t -> p c t i", i=4)
             rows = f_rows[c][:].rearrange("p t (c i) -> p c t i", i=4)
-            if c >= EARLY_CHUNKS - 1:
+            if c % EARLY_CHUNKS == EARLY_CHUNKS - 1:
                 nc.scalar.copy(out=grouped, in_=rows)
             else:
                 nc.vector.tensor_copy(out=grouped, in_=rows)
@@ -261,6 +261,11 @@ def tile_coarsematching_kernel(tc, feat_c0, feat_c1, W, b, h0c, w0c, h1c, w1c, o
                     op1=ALU.add,
                 )
 
+        half_pass = CELL_TILES // 2
+        job_list = [(0, is_row, i) for is_row in (False, True) for i in range(CELL_TILES)]
+        job_list += [(1, True, i) for i in range(half_pass)]
+        job_list += [(1, False, i) for i in range(CELL_TILES)]
+        job_list += [(1, True, i) for i in range(half_pass, CELL_TILES)]
         soft_t = {}
         total = {}
         recip = {}
@@ -278,12 +283,10 @@ def tile_coarsematching_kernel(tc, feat_c0, feat_c1, W, b, h0c, w0c, h1c, w1c, o
 
         rows_in = h1c - 2 * BORDER
         cols_in = w1c - 2 * BORDER
-        rows_wide = BANK // w1c - BORDER
 
         def job_parts(q):
-            n, job = divmod(q, JOBS_A_BATCH)
-            is_row, i = divmod(job, CELL_TILES)
-            return n, job, is_row, i
+            n, is_row, i = job_list[q]
+            return n, is_row * CELL_TILES + i, is_row, i
 
         def job_values(q):
             n, job, is_row, i = job_parts(q)
@@ -310,7 +313,7 @@ def tile_coarsematching_kernel(tc, feat_c0, feat_c1, W, b, h0c, w0c, h1c, w1c, o
 
         def minimum_wide(q):
             n, job, is_row, i = job_parts(q)
-            if job == 0:
+            if n not in soft_t:
                 soft_t[n] = keep.tile([P, CELL_TILES, CELLS], F32, name="soft_t%d" % n)
                 total[n] = keep.tile([P, JOBS_A_BATCH], F32, name="total%d" % n)
                 recip[n] = keep.tile([P, JOBS_A_BATCH], F32, name="recip%d" % n)
@@ -358,21 +361,23 @@ def tile_coarsematching_kernel(tc, feat_c0, feat_c1, W, b, h0c, w0c, h1c, w1c, o
             one = slice(job, job + 1)
             nc.vector.reciprocal(out=recip[n][:, one], in_=total[n][:, one])
 
-        def store_rows(which, n, i, tile):
+        def store_rows(which, n, i, tile, cols=slice(0, CELLS)):
             if i < INNER_TILES:
                 first = BORDER_CELLS + i * P
-                nc.sync.dma_start(out=out[which, n, first : first + P, :], in_=tile[:])
+                nc.sync.dma_start(out=out[which, n, first : first + P, cols], in_=tile[:, cols])
             else:
-                nc.sync.dma_start(out=out[which, n, CELLS - BORDER_CELLS : CELLS, :], in_=tile[0:P:2, :])
-                nc.sync.dma_start(out=out[which, n, 0:BORDER_CELLS, :], in_=tile[1:P:2, :])
+                nc.sync.dma_start(out=out[which, n, CELLS - BORDER_CELLS : CELLS, cols], in_=tile[0:P:2, cols])
+                nc.sync.dma_start(out=out[which, n, 0:BORDER_CELLS, cols], in_=tile[1:P:2, cols])
 
         def normalise(q):
             n, job, is_row, i = job_parts(q)
             one = slice(job, job + 1)
             values = job_values(q)
             if is_row:
-                conf0 = work.tile([P, CELLS], F32, name="conf0", bufs=6)
-                if n == BATCH - 1 and i % 2 == 0:
+                conf0 = work.tile([P, CELLS], F32, name="conf0", bufs=5)
+                if n == 1 and i % 2 == 0:
+                    nc.vector.tensor_scalar_mul(out=conf0[:], in0=values, scalar1=recip[n][:, one])
+                elif n == 1 or i == 0:
                     nc.scalar.activation(out=conf0[:], in_=values, func=ACT.Copy, scale=recip[n][:, one])
                 else:
                     nc.gpsimd.tensor_scalar(
@@ -381,31 +386,38 @@ def tile_coarsematching_kernel(tc, feat_c0, feat_c1, W, b, h0c, w0c, h1c, w1c, o
                     )
                 store_rows(0, n, i, conf0)
             else:
-                second_half = n == 0 and i >= CELL_TILES // 2
-                if second_half or (n == 1 and i % 2 == 0):
+                if i == CELL_TILES - 1:
+                    nc.vector.tensor_scalar_mul(out=values, in0=values, scalar1=recip[n][:, one])
+                elif i % 2 == 0:
                     nc.gpsimd.tensor_scalar(
                         out=values, in0=values, scalar1=recip[n][:, one], scalar2=0.0,
                         op0=ALU.mult, op1=ALU.add,
                     )
                 else:
                     nc.scalar.activation(out=values, in_=values, func=ACT.Copy, scale=recip[n][:, one])
-                engine = nc.vector if second_half else nc.gpsimd
+                engine = nc.vector if n == 0 and i >= half_pass else nc.gpsimd
                 engine.tensor_scalar(
                     out=inner_columns(miss_t[n][:, i, :]), in0=inner_columns(values[:, 0:INNER]), scalar1=-1.0,
                     scalar2=key[n][:, one], op0=ALU.mult, op1=ALU.add,
                 )
 
         flipped_columns = {}
+        conf1_tiles = {}
         flipped_miss = {}
         best = {}
         mask = {}
 
-        def flip_conf1(n, i, late):
+        def flip_half(n, i, right):
             rows = slice(i * P, (i + 1) * P)
-            if late:
-                banks = (wide_tile([P, BANK], "conf1_wide"), narrow_tile("conf1_narrow"))
-            else:
-                banks = (aux_tile([P, BANK], F32, "conf1_wide"), aux_tile([P, BANK], F32, "conf1_narrow"))
+            bank = aux_tile([P, BANK], F32, "conf1_half")
+            for j in range(half_pass):
+                tile = j + (half_pass if right else 0)
+                nc.tensor.transpose(bank[:, j * P : (j + 1) * P], soft_t[n][:, tile, rows], identity[:])
+            flipped_columns[n, i, right] = bank
+
+        def flip_whole(n, i):
+            rows = slice(i * P, (i + 1) * P)
+            banks = (aux_tile([P, BANK], F32, "conf1_wide"), aux_tile([P, BANK], F32, "conf1_narrow"))
             for j in range(CELL_TILES):
                 at = (j * P) % BANK
                 nc.tensor.transpose(banks[j * P // BANK][:, at : at + P], soft_t[n][:, j, rows], identity[:])
@@ -418,9 +430,16 @@ def tile_coarsematching_kernel(tc, feat_c0, feat_c1, W, b, h0c, w0c, h1c, w1c, o
                 nc.tensor.transpose(miss1[:, j * P : (j + 1) * P], miss_t[n][:, j, rows], identity_bf[:])
             flipped_miss[n, i] = miss1
 
-        def store_conf1(n, i):
+        def store_half(n, i, right):
+            if not right:
+                conf1_tiles[n, i] = work.tile([P, CELLS], F32, name="conf1_halves", bufs=6)
+            cols = slice(HALF, CELLS) if right else slice(0, HALF)
+            nc.scalar.copy(out=conf1_tiles[n, i][:, cols], in_=flipped_columns[n, i, right][:, 0:HALF])
+            store_rows(1, n, i, conf1_tiles[n, i], cols)
+
+        def store_whole(n, i):
             conf1_wide, conf1_narrow = flipped_columns[n, i]
-            conf1 = work.tile([P, CELLS], F32, name="conf1", bufs=6)
+            conf1 = work.tile([P, CELLS], F32, name="conf1", bufs=3)
             nc.scalar.copy(out=conf1[:, BANK:CELLS], in_=conf1_narrow[:, 0:REST])
             nc.scalar.copy(out=conf1[:, 0:BANK], in_=conf1_wide[:])
             store_rows(1, n, i, conf1)
@@ -438,8 +457,13 @@ def tile_coarsematching_kernel(tc, feat_c0, feat_c1, W, b, h0c, w0c, h1c, w1c, o
             one = slice(CELL_TILES + i, CELL_TILES + i + 1)
             if (n, i) not in best:
                 best[n, i] = work.tile([P, rows_in, cols_in], F32, name="best")
-            grid = flipped_columns[n, i][1 if second else 0][:].rearrange("p (r w) -> p r w", w=w1c)
-            rows = slice(rows_wide, rows_in) if second else slice(0, rows_wide)
+            if n == 0:
+                conf1, width = flipped_columns[n, i][1 if second else 0], BANK
+            else:
+                conf1, width = (flipped_columns[n, i, True] if second else conf1_tiles[n, i]), HALF
+            grid = conf1[:, 0:width].rearrange("p (r w) -> p r w", w=w1c)
+            cut = width // w1c - BORDER
+            rows = slice(cut, rows_in) if second else slice(0, cut)
             first = 0 if second else BORDER
             nc.vector.scalar_tensor_tensor(
                 out=best[n, i][:, rows, :],
@@ -451,10 +475,8 @@ def tile_coarsematching_kernel(tc, feat_c0, feat_c1, W, b, h0c, w0c, h1c, w1c, o
             )
 
         def multiply_mconf(n, i):
-            on_vector = (n, i) == (BATCH - 1, INNER_TILES - 1)
             mconf = mconf_tiles[i % len(mconf_tiles)]
-            engine = nc.vector if on_vector else nc.gpsimd
-            engine.tensor_tensor(out=interior(mconf[:]), in0=mask[n, i][:], in1=best[n, i][:], op=ALU.mult)
+            nc.gpsimd.tensor_tensor(out=interior(mconf[:]), in0=mask[n, i][:], in1=best[n, i][:], op=ALU.mult)
 
         def store_mconf(n, i):
             store_rows(2, n, i, mconf_tiles[i % len(mconf_tiles)])
@@ -470,7 +492,7 @@ def tile_coarsematching_kernel(tc, feat_c0, feat_c1, W, b, h0c, w0c, h1c, w1c, o
         flip_tokens(1, True)
         hold_clock(2)
         quantise_tokens(0)
-        gather_tokens(1, 0)
+        gather_tokens(1, 2)
         project(0, 0, PACK)
         quantise_tokens(1)
         flip_tokens(2, True)
@@ -486,7 +508,7 @@ def tile_coarsematching_kernel(tc, feat_c0, feat_c1, W, b, h0c, w0c, h1c, w1c, o
 
         front = {}
         for c in range(EARLY_CHUNKS, CHUNKS):
-            start = 2 * (c - EARLY_CHUNKS)
+            start = 2 * (c - EARLY_CHUNKS) - 1
             for k, steps in enumerate(FRONT_STEPS):
                 for step in steps:
                     front[start + k, step] = c
@@ -499,7 +521,7 @@ def tile_coarsematching_kernel(tc, feat_c0, feat_c1, W, b, h0c, w0c, h1c, w1c, o
             if step == "flip":
                 flip_tokens(c, False)
             elif step == "gather":
-                gather_tokens(c, 1 if c == CHUNKS - 1 else 0)
+                gather_tokens(c, 0)
             elif step == "quantise x":
                 quantise_tokens(c)
             elif step in ("first half", "second half"):
@@ -512,51 +534,62 @@ def tile_coarsematching_kernel(tc, feat_c0, feat_c1, W, b, h0c, w0c, h1c, w1c, o
                 quantise_features(c)
 
         def tile_at(q):
-            n = 0 if q < 20 else 1
-            i, rest = divmod(q - 8, 2) if n == 0 else (q - 20, 0)
+            n, i, rest = (0,) + divmod(q - 8, 2) if q < 20 else (1, q - 27, 0)
             return (n, i) if rest == 0 and 0 <= i < CELL_TILES else None
+
+        def left_at(q):
+            return q - 21 if 0 <= q - 21 < CELL_TILES else None
 
         def inner(tile):
             return tile is not None and tile[1] < INNER_TILES
 
-        for q in range(-2, JOBS + 4):
-            flips, shown, stored = tile_at(q), tile_at(q - 1), tile_at(q - 2)
-            front_step(q, "flip")
-            front_step(q, "quantise x")
-            front_step(q, "regroup")
-            front_step(q, "quantise f")
-            if inner(shown):
-                flip_miss(*shown)
-            if shown is not None:
-                store_conf1(*shown)
-            if flips is not None:
-                flip_conf1(*flips, q >= JOBS - 2)
-            if 0 <= q - 1 < JOBS:
-                reciprocals(q - 1)
-            if inner(shown):
-                keep_mask(*shown)
-            if inner(stored):
-                multiply_mconf(*stored)
-            if inner(flips):
-                best_of_two(*flips, False)
-                best_of_two(*flips, True)
+        for q in range(-2, 36):
+            ahead, now, last, before, first = (tile_at(q + k) for k in (1, 0, -1, -2, -3))
             if q == 0:
                 quantise_features(EARLY_CHUNKS - 1)
-            if inner(stored):
-                store_mconf(*stored)
+            left = left_at(q)
+            if left is not None:
+                flip_half(1, left, False)
+                store_half(1, left, False)
+            if inner(first):
+                store_mconf(*first)
+            front_step(q, "quantise f")
+            if 0 <= q - 1 < JOBS:
+                reciprocals(q - 1)
+            if inner(before):
+                multiply_mconf(*before)
             front_step(q, "first half")
-            if 0 <= q < JOBS:
-                exponentials(q)
             front_step(q, "second half")
+            front_step(q, "regroup")
+            if inner(last):
+                keep_mask(*last)
+            if inner(now):
+                best_of_two(*now, False)
+                best_of_two(*now, True)
+            if 0 <= q + 1 < JOBS:
+                minimum_narrow(q + 1)
             if 0 <= q + 2 < JOBS:
                 similarities(q + 2, False)
                 similarities(q + 2, True)
-            front_step(q, "gather")
-            if 0 <= q + 1 < JOBS:
-                minimum_narrow(q + 1)
+                minimum_wide(q + 2)
+            front_step(q, "flip")
             if 0 <= q - 1 < JOBS:
                 keys(q - 1)
-            if 0 <= q + 2 < JOBS:
-                minimum_wide(q + 2)
-            if 0 <= q - 1 < JOBS:
-                normalise(q - 1)
+            front_step(q, "quantise x")
+            if 0 <= q - 2 < JOBS:
+                normalise(q - 2)
+            if last is not None:
+                if last[0] == 0:
+                    store_whole(*last)
+                else:
+                    store_half(*last, True)
+            if inner(now):
+                flip_miss(*now)
+            if ahead is not None:
+                if ahead[0] == 0:
+                    flip_whole(*ahead)
+                else:
+                    flip_half(*ahead, True)
+            if 0 <= q < JOBS:
+                exponentials(q)
+            front_step(q, "gather")

from contextlib import ExitStack
import math

import concourse.mybir as mybir
from concourse.masks import make_identity

F32 = mybir.dt.float32
BF16 = mybir.dt.bfloat16
U32 = mybir.dt.uint32
U8 = mybir.dt.uint8
FP8X4 = mybir.dt.float8_e4m3fn_x4
ALU = mybir.AluOpType
ACT = mybir.ActivationFunctionType

P = 128
PACK = 4
BANK = 512
BATCH = 2
CELLS = 768
FEATURES = 512
CELL_TILES = CELLS // P
HALF = CELLS // 2
REST = CELLS - BANK
TOKENS = 2 * BATCH * CELLS
BORDER_CELLS = 64
INNER = CELLS - 2 * BORDER_CELLS
INNER_TILES = INNER // P
CHUNK = BANK
CHUNK_TILES = CHUNK // P
CHUNKS = TOKENS // CHUNK
JOBS_A_BATCH = 2 * CELL_TILES
JOBS = BATCH * JOBS_A_BATCH
BORDER = 2
EARLY_CHUNKS = CHUNKS // BATCH
FRONT_STEPS = (("flip", "gather"), ("quantise x",), (), ("first half",), ("second half",), ("regroup",), ("quantise f",))
INV_THRESHOLD = 5.0
INV_TEMPERATURE = 10.0
INV_SQRT_FEATURES = 1.0 / math.sqrt(FEATURES)

FLOPS = 2 * TOKENS * FEATURES * FEATURES + 2 * BATCH * CELLS * CELLS * FEATURES


def tile_coarsematching_kernel(tc, feat_c0, feat_c1, W, b, h0c, w0c, h1c, w1c, out):
    nc = tc.nc
    assert h0c * w0c == CELLS and h1c * w1c == CELLS
    assert h0c == h1c and w0c == w1c and P % w0c == 0
    assert BORDER_CELLS == BORDER * w0c and INNER % P == 0

    with ExitStack() as ctx:
        keep = ctx.enter_context(tc.tile_pool(name="keep", bufs=1))
        stage = ctx.enter_context(tc.tile_pool(name="stage", bufs=2))
        work = ctx.enter_context(tc.tile_pool(name="work", bufs=3))
        small = ctx.enter_context(tc.tile_pool(name="small", bufs=6))
        psum = ctx.enter_context(tc.psum_pool(name="psum", bufs=1))
        ctx.enter_context(tc.manual_schedule())

        def wide_tile(shape, name):
            return psum.tile(shape, F32, tag="wide", bufs=2, name=name)

        def narrow_tile(name):
            return psum.tile([P, BANK], F32, tag="narrow", bufs=2, name=name)

        def aux_tile(shape, dtype, name):
            return psum.tile(shape, dtype, tag="aux", bufs=4, name=name)

        w_raw = keep.tile([P, PACK * FEATURES], BF16)
        w_raw_rows = w_raw[:].rearrange("p (t k) -> p t k", t=PACK)
        W_rows = W.rearrange("(p t) k -> p t k", t=PACK)
        for h in range(2):
            nc.sync.dma_start(out=w_raw_rows[:, 2 * h : 2 * h + 2, :], in_=W_rows[:, 2 * h : 2 * h + 2, :])
        b_raw = keep.tile([P, PACK], BF16)
        x_raw = keep.tile([P, (TOKENS // P) * FEATURES], BF16)
        x_raw_tiles = x_raw[:].rearrange("p (r k) -> p r k", k=FEATURES)

        def load_tokens(n, g, first, count):
            feat = (feat_c0, feat_c1)[g]
            at = (2 * n + g) * CELL_TILES + first
            if g == 1:
                nc.sync.dma_start(
                    out=x_raw_tiles[:, at : at + count, :],
                    in_=feat[n].rearrange("(j p) k -> p j k", p=P)[:, first : first + count, :],
                )
                return
            inner = min(count, INNER_TILES - first)
            rows = feat[n, BORDER_CELLS + first * P : BORDER_CELLS + (first + inner) * P, :]
            nc.sync.dma_start(out=x_raw_tiles[:, at : at + inner, :], in_=rows.rearrange("(j p) k -> p j k", p=P))
            if inner < count:
                nc.sync.dma_start(out=x_raw_tiles[0:BORDER_CELLS, at + inner, :], in_=feat[n, CELLS - BORDER_CELLS : CELLS, :])
                nc.sync.dma_start(out=x_raw_tiles[BORDER_CELLS:P, at + inner, :], in_=feat[n, 0:BORDER_CELLS, :])

        load_tokens(0, 0, 0, 4)
        nc.sync.dma_start(out=b_raw[:], in_=b.rearrange("(p t) -> p t", t=PACK))
        load_tokens(0, 0, 4, 2)
        load_tokens(0, 1, 0, 2)
        load_tokens(0, 1, 2, 4)
        load_tokens(1, 0, 0, 6)
        load_tokens(1, 1, 0, 6)

        identity = keep.tile([P, P], F32)
        make_identity(nc, identity[:])
        identity_bf = keep.tile([P, P], BF16)
        zero = keep.tile([P, 1], F32)
        nc.vector.memset(zero[:], 0.0)
        warm = keep.tile([P, 1], F32)
        nc.scalar.activation(out=warm[:], in_=zero[:], func=ACT.Exp)

        edge = keep.tile([P, P], F32)
        nc.vector.memset(edge[:], INV_THRESHOLD)
        edge_rows = edge[:].rearrange("p (r w) -> p r w", w=w0c)
        nc.vector.memset(edge_rows[:, :, 0:BORDER], 0.0)
        nc.vector.memset(edge_rows[:, :, w0c - BORDER : w0c], 0.0)
        nc.vector.tensor_copy(out=identity_bf[:], in_=identity[:])

        zero_columns = keep.tile([P, BANK], BF16)
        nc.vector.memset(zero_columns[:], 0.0)

        def hold_clock(count):
            for k in range(count):
                unused = narrow_tile("unused")
                nc.tensor.matmul(
                    out=unused[:], lhsT=zero_columns[:, 0:P], rhs=zero_columns[:], start=True, stop=True
                )

        edge_t = aux_tile([P, BANK], F32, "edge_t")
        nc.tensor.transpose(edge_t[:, 0:P], edge[:], identity[:])
        hold_clock(3)
        limit = keep.tile([P, 1], F32)
        nc.vector.tensor_copy(out=limit[:], in_=edge_t[:, 0:1])

        mconf_tiles = []
        for slot in range(4):
            mconf = keep.tile([P, CELLS], F32, name="mconf%d" % slot)
            nc.scalar.activation(out=mconf[:], in_=zero[:].to_broadcast([P, CELLS]), func=ACT.Copy)
            mconf_tiles.append(mconf)
        for n in range(BATCH):
            for rows in (slice(0, BORDER_CELLS), slice(CELLS - BORDER_CELLS, CELLS)):
                nc.sync.dma_start(out=out[2, n, rows, :], in_=mconf_tiles[n][0:P:2, :])
        miss_t = []
        for n in range(BATCH):
            miss = keep.tile([P, CELL_TILES, INNER], BF16, name="miss_t%d" % n)
            grid_rows = miss[:].rearrange("p j (r w) -> p (j r) w", w=w0c)
            nc.vector.memset(grid_rows[:, :, 0:BORDER], 1.0)
            nc.vector.memset(grid_rows[:, :, w0c - BORDER : w0c], 1.0)
            miss_t.append(miss)

        b_scaled = keep.tile([P, PACK], F32)

        def flip(raw, first_tile, early):
            words = raw.bitcast(F32).rearrange("p (r u q) -> p r u q", u=2, q=P)
            banks = []
            for h in range(2):
                flipped = wide_tile([P, 2, 2, P], "flipped") if early else aux_tile([P, 2, 2, P], F32, "flipped")
                for r in range(2):
                    for u in range(2):
                        nc.tensor.transpose(
                            flipped[:, r, u, :], words[:, first_tile + 2 * h + r, u, :], identity[:]
                        )
                banks.append(flipped)
            return banks

        def gather(banks, vector_banks, border=False):
            grouped = stage.tile([P, CHUNK * PACK], BF16, name="grouped", bufs=3, align_bytes=64)
            halves = grouped[:].bitcast(F32).rearrange("p (h r c u) -> p h r c u", h=2, r=2, u=2)
            for h in range(2):
                copy = nc.vector.tensor_copy if h < vector_banks else nc.scalar.copy
                if border and h == 0:
                    copy(out=halves[:, h, 0], in_=banks[h][:, 0].rearrange("p u c -> p c u"))
                    copy(
                        out=halves[:, h, 1].rearrange("p (c e) u -> p c e u", e=2),
                        in_=banks[h][:, 1].rearrange("p u (e c) -> p c e u", e=2),
                    )
                else:
                    copy(out=halves[:, h], in_=banks[h][:].rearrange("p r u c -> p r c u"))
            return grouped

        w_codes = keep.tile([P, FEATURES], U32, align_bytes=64)
        w_scales = keep.tile([P, FEATURES], U8, align_bytes=64)
        x_codes = keep.tile([P, TOKENS], U32, align_bytes=64)
        x_scales = keep.tile([P, TOKENS], U8, align_bytes=64)
        f_codes = keep.tile([P, TOKENS], U32, align_bytes=64)
        f_scales = keep.tile([P, TOKENS], U8, align_bytes=64)
        x_banks = {}
        x_grouped = {}
        f_rows = {}
        f_grouped = {}

        def chunk_columns(c):
            return slice(c * CHUNK, (c + 1) * CHUNK)

        def flip_tokens(c, early):
            x_banks[c] = flip(x_raw[:], c * CHUNK_TILES, early)

        def gather_tokens(c, vector_banks):
            x_grouped[c] = gather(x_banks[c], vector_banks, c % EARLY_CHUNKS == 1)

        def quantise_tokens(c):
            cols = chunk_columns(c)
            nc.vector.quantize_mx(
                out=x_codes[:, cols].bitcast(FP8X4), scales=x_scales[:, cols], in_=x_grouped[c][:]
            )

        def project(c, first, last):
            cols = chunk_columns(c)
            if first == 0:
                f_rows[c] = stage.tile([P, PACK, CHUNK], BF16, name="f_rows")
            for t in range(first, last):
                acc = aux_tile([P, BANK], F32, "acc")
                nc.tensor.matmul_mx(
                    out=acc[:],
                    lhsT=w_codes[:, t * P : (t + 1) * P].bitcast(FP8X4),
                    lhsT_scale=w_scales[:, t * P : (t + 1) * P],
                    rhs=x_codes[:, cols].bitcast(FP8X4),
                    rhs_scale=x_scales[:, cols],
                    start=True,
                    stop=True,
                )
                nc.scalar.activation(
                    out=f_rows[c][:, t, :], in_=acc[:], func=ACT.Identity,
                    bias=b_scaled[:, t : t + 1], scale=INV_SQRT_FEATURES,
                )

        def regroup(c):
            f_grouped[c] = stage.tile([P, CHUNK, PACK], BF16, name="f_grouped", align_bytes=64)
            grouped = f_grouped[c][:].rearrange("p (c i) t -> p c t i", i=4)
            rows = f_rows[c][:].rearrange("p t (c i) -> p c t i", i=4)
            if c % EARLY_CHUNKS == EARLY_CHUNKS - 1:
                nc.scalar.copy(out=grouped, in_=rows)
            else:
                nc.vector.tensor_copy(out=grouped, in_=rows)

        def quantise_features(c):
            cols = chunk_columns(c)
            nc.vector.quantize_mx(
                out=f_codes[:, cols].bitcast(FP8X4),
                scales=f_scales[:, cols],
                in_=f_grouped[c][:].rearrange("p c t -> p (c t)"),
            )

        def project_direct(c, first, last):
            if first == 0:
                f_grouped[c] = stage.tile([P, CHUNK, PACK], BF16, name="f_grouped", align_bytes=64)
            for r in range(first, last):
                cols = slice(c * CHUNK + r * P, c * CHUNK + (r + 1) * P)
                acc = aux_tile([P, PACK, P], F32, "acc")
                for t in range(PACK):
                    nc.tensor.matmul_mx(
                        out=acc[:, t, :],
                        lhsT=w_codes[:, t * P : (t + 1) * P].bitcast(FP8X4),
                        lhsT_scale=w_scales[:, t * P : (t + 1) * P],
                        rhs=x_codes[:, cols].bitcast(FP8X4),
                        rhs_scale=x_scales[:, cols],
                        start=True,
                        stop=True,
                    )
                nc.vector.scalar_tensor_tensor(
                    out=f_grouped[c][:, r * P : (r + 1) * P, :],
                    in0=acc[:].rearrange("p t n -> p n t"),
                    scalar=INV_SQRT_FEATURES,
                    in1=b_scaled[:].unsqueeze(1).to_broadcast([P, P, PACK]),
                    op0=ALU.mult,
                    op1=ALU.add,
                )

        half_pass = CELL_TILES // 2
        job_list = [(0, is_row, i) for is_row in (False, True) for i in range(CELL_TILES)]
        job_list += [(1, True, i) for i in range(half_pass)]
        job_list += [(1, False, i) for i in range(CELL_TILES)]
        job_list += [(1, True, i) for i in range(half_pass, CELL_TILES)]
        soft_t = {}
        total = {}
        recip = {}
        key = {}
        numer = {}
        sim_banks = {}
        low_wide = {}
        low = {}

        def inner_columns(ap):
            return ap.rearrange("p (r w) -> p r w", w=w0c)[:, :, BORDER : w0c - BORDER]

        def interior(ap):
            return inner_columns(ap[:, BORDER_CELLS : BORDER_CELLS + INNER])

        rows_in = h1c - 2 * BORDER
        cols_in = w1c - 2 * BORDER

        def job_parts(q):
            n, is_row, i = job_list[q]
            return n, is_row * CELL_TILES + i, is_row, i

        def job_values(q):
            n, job, is_row, i = job_parts(q)
            return numer[n, i][:] if is_row else soft_t[n][:, i, :]

        def similarities(q, rest):
            n, job, is_row, i = job_parts(q)
            f0_at = 2 * n * CELLS
            f1_at = f0_at + CELLS
            at = (f0_at if is_row else f1_at) + i * P
            along = f1_at if is_row else f0_at
            acc = narrow_tile("narrow") if rest else wide_tile([P, BANK], "wide")
            first, width = (along + BANK, REST) if rest else (along, BANK)
            nc.tensor.matmul_mx(
                out=acc[:, 0:width],
                lhsT=f_codes[:, at : at + P].bitcast(FP8X4),
                lhsT_scale=f_scales[:, at : at + P],
                rhs=f_codes[:, first : first + width].bitcast(FP8X4),
                rhs_scale=f_scales[:, first : first + width],
                start=True,
                stop=True,
            )
            sim_banks[q, rest] = acc

        def minimum_wide(q):
            n, job, is_row, i = job_parts(q)
            if n not in soft_t:
                soft_t[n] = keep.tile([P, CELL_TILES, CELLS], F32, name="soft_t%d" % n)
                total[n] = keep.tile([P, JOBS_A_BATCH], F32, name="total%d" % n)
                recip[n] = keep.tile([P, JOBS_A_BATCH], F32, name="recip%d" % n)
                key[n] = keep.tile([P, JOBS_A_BATCH], F32, name="key%d" % n)
            if is_row:
                numer[n, i] = work.tile([P, CELLS], F32, name="numer", bufs=9)
            low_wide[q] = small.tile([P, 1], F32, name="low_wide")
            nc.vector.tensor_scalar(
                out=job_values(q)[:, 0:BANK], in0=sim_banks[q, False][:], scalar1=-INV_TEMPERATURE,
                scalar2=None, op0=ALU.mult, op1=ALU.min, accum_out=low_wide[q][:],
            )

        def minimum_narrow(q):
            low[q] = small.tile([P, 1], F32, name="low")
            nc.vector.tensor_scalar(
                out=job_values(q)[:, BANK:CELLS], in0=sim_banks[q, True][:, 0:REST], scalar1=-INV_TEMPERATURE,
                scalar2=low_wide[q][:], op0=ALU.mult, op1=ALU.min, accum_out=low[q][:],
            )

        def exponentials(q):
            n, job, is_row, i = job_parts(q)
            nc.scalar.activation(
                out=job_values(q), in_=job_values(q), func=ACT.Exp,
                bias=low[q][:], scale=-1.0, accum_out=total[n][:, job : job + 1],
            )

        def keys(q):
            n, job, is_row, i = job_parts(q)
            one = slice(job, job + 1)
            if is_row and i == INNER_TILES:
                return
            if is_row:
                nc.vector.tensor_scalar(
                    out=key[n][:, one], in0=total[n][:, one], scalar1=limit[:], scalar2=1.0,
                    op0=ALU.is_ge, op1=ALU.add,
                )
            else:
                nc.vector.tensor_scalar(
                    out=key[n][:, one], in0=total[n][:, one], scalar1=INV_THRESHOLD,
                    scalar2=recip[n][:, one], op0=ALU.is_ge, op1=ALU.max,
                )

        def reciprocals(q):
            n, job, is_row, i = job_parts(q)
            one = slice(job, job + 1)
            nc.vector.reciprocal(out=recip[n][:, one], in_=total[n][:, one])

        def store_rows(which, n, i, tile, cols=slice(0, CELLS)):
            if i < INNER_TILES:
                first = BORDER_CELLS + i * P
                nc.sync.dma_start(out=out[which, n, first : first + P, cols], in_=tile[:, cols])
            else:
                nc.sync.dma_start(out=out[which, n, CELLS - BORDER_CELLS : CELLS, cols], in_=tile[0:P:2, cols])
                nc.sync.dma_start(out=out[which, n, 0:BORDER_CELLS, cols], in_=tile[1:P:2, cols])

        def normalise(q):
            n, job, is_row, i = job_parts(q)
            one = slice(job, job + 1)
            values = job_values(q)
            if is_row:
                conf0 = work.tile([P, CELLS], F32, name="conf0", bufs=5)
                if n == 1 and i % 2 == 0:
                    nc.vector.tensor_scalar_mul(out=conf0[:], in0=values, scalar1=recip[n][:, one])
                elif n == 1 or i == 0:
                    nc.scalar.activation(out=conf0[:], in_=values, func=ACT.Copy, scale=recip[n][:, one])
                else:
                    nc.gpsimd.tensor_scalar(
                        out=conf0[:], in0=values, scalar1=recip[n][:, one], scalar2=0.0,
                        op0=ALU.mult, op1=ALU.add,
                    )
                store_rows(0, n, i, conf0)
            else:
                if i == CELL_TILES - 1:
                    nc.vector.tensor_scalar_mul(out=values, in0=values, scalar1=recip[n][:, one])
                elif i % 2 == 0:
                    nc.gpsimd.tensor_scalar(
                        out=values, in0=values, scalar1=recip[n][:, one], scalar2=0.0,
                        op0=ALU.mult, op1=ALU.add,
                    )
                else:
                    nc.scalar.activation(out=values, in_=values, func=ACT.Copy, scale=recip[n][:, one])
                engine = nc.vector if n == 0 and i >= half_pass else nc.gpsimd
                engine.tensor_scalar(
                    out=inner_columns(miss_t[n][:, i, :]), in0=inner_columns(values[:, 0:INNER]), scalar1=-1.0,
                    scalar2=key[n][:, one], op0=ALU.mult, op1=ALU.add,
                )

        flipped_columns = {}
        conf1_tiles = {}
        flipped_miss = {}
        best = {}
        mask = {}

        def flip_half(n, i, right):
            rows = slice(i * P, (i + 1) * P)
            bank = aux_tile([P, BANK], F32, "conf1_half")
            for j in range(half_pass):
                tile = j + (half_pass if right else 0)
                nc.tensor.transpose(bank[:, j * P : (j + 1) * P], soft_t[n][:, tile, rows], identity[:])
            flipped_columns[n, i, right] = bank

        def flip_whole(n, i):
            rows = slice(i * P, (i + 1) * P)
            banks = (aux_tile([P, BANK], F32, "conf1_wide"), aux_tile([P, BANK], F32, "conf1_narrow"))
            for j in range(CELL_TILES):
                at = (j * P) % BANK
                nc.tensor.transpose(banks[j * P // BANK][:, at : at + P], soft_t[n][:, j, rows], identity[:])
            flipped_columns[n, i] = banks

        def flip_miss(n, i):
            rows = slice(i * P, (i + 1) * P)
            miss1 = aux_tile([P, CELLS], BF16, "miss1")
            for j in range(CELL_TILES):
                nc.tensor.transpose(miss1[:, j * P : (j + 1) * P], miss_t[n][:, j, rows], identity_bf[:])
            flipped_miss[n, i] = miss1

        def store_half(n, i, right):
            if not right:
                conf1_tiles[n, i] = work.tile([P, CELLS], F32, name="conf1_halves", bufs=6)
            cols = slice(HALF, CELLS) if right else slice(0, HALF)
            nc.scalar.copy(out=conf1_tiles[n, i][:, cols], in_=flipped_columns[n, i, right][:, 0:HALF])
            store_rows(1, n, i, conf1_tiles[n, i], cols)

        def store_whole(n, i):
            conf1_wide, conf1_narrow = flipped_columns[n, i]
            conf1 = work.tile([P, CELLS], F32, name="conf1", bufs=3)
            nc.scalar.copy(out=conf1[:, BANK:CELLS], in_=conf1_narrow[:, 0:REST])
            nc.scalar.copy(out=conf1[:, 0:BANK], in_=conf1_wide[:])
            store_rows(1, n, i, conf1)

        def keep_mask(n, i):
            miss1 = flipped_miss[n, i]
            one = slice(CELL_TILES + i, CELL_TILES + i + 1)
            mask[n, i] = work.tile([P, rows_in, cols_in], BF16, name="mask")
            nc.vector.scalar_tensor_tensor(
                out=mask[n, i][:], in0=interior(numer[n, i][:]), scalar=key[n][:, one],
                in1=interior(miss1[:]), op0=ALU.is_ge, op1=ALU.is_ge,
            )

        def best_of_two(n, i, second):
            one = slice(CELL_TILES + i, CELL_TILES + i + 1)
            if (n, i) not in best:
                best[n, i] = work.tile([P, rows_in, cols_in], F32, name="best")
            if n == 0:
                conf1, width = flipped_columns[n, i][1 if second else 0], BANK
            else:
                conf1, width = (flipped_columns[n, i, True] if second else conf1_tiles[n, i]), HALF
            grid = conf1[:, 0:width].rearrange("p (r w) -> p r w", w=w1c)
            cut = width // w1c - BORDER
            rows = slice(cut, rows_in) if second else slice(0, cut)
            first = 0 if second else BORDER
            nc.vector.scalar_tensor_tensor(
                out=best[n, i][:, rows, :],
                in0=interior(numer[n, i][:])[:, rows, :],
                scalar=recip[n][:, one],
                in1=grid[:, first : first + rows.stop - rows.start, BORDER : w1c - BORDER],
                op0=ALU.mult,
                op1=ALU.max,
            )

        def multiply_mconf(n, i):
            mconf = mconf_tiles[i % len(mconf_tiles)]
            nc.gpsimd.tensor_tensor(out=interior(mconf[:]), in0=mask[n, i][:], in1=best[n, i][:], op=ALU.mult)

        def store_mconf(n, i):
            store_rows(2, n, i, mconf_tiles[i % len(mconf_tiles)])

        w_banks = flip(w_raw[:], 0, True)
        hold_clock(2)
        w_grouped = gather(w_banks, 1)
        flip_tokens(0, False)
        hold_clock(2)
        nc.vector.quantize_mx(out=w_codes[:].bitcast(FP8X4), scales=w_scales[:], in_=w_grouped[:])
        gather_tokens(0, 1)
        nc.vector.tensor_scalar_mul(out=b_scaled[:], in0=b_raw[:], scalar1=INV_SQRT_FEATURES)
        flip_tokens(1, True)
        hold_clock(2)
        quantise_tokens(0)
        gather_tokens(1, 2)
        project(0, 0, PACK)
        quantise_tokens(1)
        flip_tokens(2, True)
        gather_tokens(2, 2)
        project(1, 0, PACK)
        quantise_tokens(2)
        project(2, 0, PACK)
        regroup(0)
        quantise_features(0)
        regroup(1)
        quantise_features(1)
        regroup(2)

        front = {}
        for c in range(EARLY_CHUNKS, CHUNKS):
            start = 2 * (c - EARLY_CHUNKS) - 1
            for k, steps in enumerate(FRONT_STEPS):
                for step in steps:
                    front[start + k, step] = c

        def front_step(q, step):
            c = front.get((q, step))
            if c is None:
                return
            direct = c == EARLY_CHUNKS
            if step == "flip":
                flip_tokens(c, False)
            elif step == "gather":
                gather_tokens(c, 0)
            elif step == "quantise x":
                quantise_tokens(c)
            elif step in ("first half", "second half"):
                first = 0 if step == "first half" else 2
                (project_direct if direct else project)(c, first, first + 2)
            elif step == "regroup":
                if not direct:
                    regroup(c)
            else:
                quantise_features(c)

        def tile_at(q):
            n, i, rest = (0,) + divmod(q - 8, 2) if q < 20 else (1, q - 27, 0)
            return (n, i) if rest == 0 and 0 <= i < CELL_TILES else None

        def left_at(q):
            return q - 21 if 0 <= q - 21 < CELL_TILES else None

        def inner(tile):
            return tile is not None and tile[1] < INNER_TILES

        for q in range(-2, 36):
            ahead, now, last, before, first = (tile_at(q + k) for k in (1, 0, -1, -2, -3))
            if q == 0:
                quantise_features(EARLY_CHUNKS - 1)
            left = left_at(q)
            if left is not None:
                flip_half(1, left, False)
                store_half(1, left, False)
            if inner(first):
                store_mconf(*first)
            front_step(q, "quantise f")
            if 0 <= q - 1 < JOBS:
                reciprocals(q - 1)
            if inner(before):
                multiply_mconf(*before)
            front_step(q, "first half")
            front_step(q, "second half")
            front_step(q, "regroup")
            if inner(last):
                keep_mask(*last)
            if inner(now):
                best_of_two(*now, False)
                best_of_two(*now, True)
            if 0 <= q + 1 < JOBS:
                minimum_narrow(q + 1)
            if 0 <= q + 2 < JOBS:
                similarities(q + 2, False)
                similarities(q + 2, True)
                minimum_wide(q + 2)
            front_step(q, "flip")
            if 0 <= q - 1 < JOBS:
                keys(q - 1)
            front_step(q, "quantise x")
            if 0 <= q - 2 < JOBS:
                normalise(q - 2)
            if last is not None:
                if last[0] == 0:
                    store_whole(*last)
                else:
                    store_half(*last, True)
            if inner(now):
                flip_miss(*now)
            if ahead is not None:
                if ahead[0] == 0:
                    flip_whole(*ahead)
                else:
                    flip_half(*ahead, True)
            if 0 <= q < JOBS:
                exponentials(q)
            front_step(q, "gather")
